import numpy as np
import ml_dtypes


def mxq(x, axis, fmt="e4m3"):
    dtype, down = {"e4m3": (ml_dtypes.float8_e4m3fn, 7), "e5m2": (ml_dtypes.float8_e5m2, 14)}[fmt]
    v = np.moveaxis(np.asarray(x, np.float32).astype(ml_dtypes.bfloat16).astype(np.float64), axis, -1)
    blocks = v.reshape(v.shape[:-1] + (-1, 32))
    amax = np.abs(blocks).max(-1, keepdims=True)
    byte = np.maximum(np.where(amax > 0, np.frexp(amax)[1] - 1 + 127, 0) - down, 1)
    scale = np.exp2(byte - 127.0)
    codes = (blocks / scale).astype(np.float32).astype(dtype).astype(np.float64)
    return np.moveaxis((codes * scale).reshape(v.shape), -1, axis)


WIDE = False


def mx_kscale(k):
    if not WIDE:
        return np.ones(k)
    levels = np.array([10, -10, 5, -5, 0])
    a = np.random.permutation(np.resize(levels, k // 512 * 4)).reshape(k // 512, 4)
    idx = np.arange(k)
    return np.exp2(a[idx // 512, idx % 128 // 32])


BF16 = ml_dtypes.bfloat16


def bf(x):
    return np.asarray(x, np.float32).astype(BF16)


def f64(x):
    return np.asarray(x).astype(np.float64)


E2M1 = np.array([0.0, 0.5, 1.0, 1.5, 2.0, 3.0, 4.0, 6.0, -0.0, -0.5, -1.0, -1.5, -2.0, -3.0, -4.0, -6.0])


def pack_weight(w, fmt):
    k, n = w.shape
    w = f64(bf(w)).reshape(k // 32, 32, n)
    amax = np.abs(w).max(1)
    if fmt == "e4m3":
        byte = np.frexp(amax)[1] - 1 + 127 - 7
    else:
        mant, ex = np.frexp(amax / 6.0)
        byte = np.where(mant > 0.5, ex, ex - 1) + 127
    byte = np.clip(np.where(amax > 0, byte, 1), 1, 254)
    scaled = (w * np.exp2(127.0 - byte)[:, None, :]).reshape(k, n).astype(np.float32)
    by_word = np.ascontiguousarray(scaled.reshape(k // 512, 128, 4, n).transpose(0, 1, 3, 2))
    if fmt == "e4m3":
        words = by_word.astype(ml_dtypes.float8_e4m3fn).view(np.uint8)
    else:
        c = by_word.astype(ml_dtypes.float4_e2m1fn).view(np.uint8) & 0xF
        words = c[..., 0::2] | (c[..., 1::2] << 4)
    return np.ascontiguousarray(words), np.ascontiguousarray(byte.astype(np.uint8).reshape(k // 512, 16, n))


def unpack_weight(words, scales, fmt):
    g, p, n, _ = words.shape
    if fmt == "e4m3":
        vals = np.ascontiguousarray(words).view(ml_dtypes.float8_e4m3fn).astype(np.float64)
    else:
        nib = np.empty((g, p, n, 4), np.uint8)
        nib[..., 0::2] = words & 0xF
        nib[..., 1::2] = words >> 4
        vals = E2M1[nib]
    vals = vals * np.repeat(np.exp2(scales.astype(np.float64) - 127.0), 8, axis=1)[..., None]
    return vals.transpose(0, 1, 3, 2).reshape(g * 512, n)


B, H0, W0, H1, W1, C = 2, 24, 32, 24, 32, 512
L, S = H0 * W0, H1 * W1
THR = 0.2
TEMPERATURE = 0.1
BORDER = 2
NM = min(L, S) // 2
ND = NM // 16
DUP = 0.92
RB = 0.5
ZT = 4.5
SD = ZT - np.sqrt(ZT**2 - 2.0 * np.log(min(L, S) * THR / (1.0 - THR)))
SIG = SD / np.sqrt(1.0 + RB**2 / 2.0)
G = np.sqrt(SIG * TEMPERATURE * np.sqrt(C / 2.0))
MATCH = np.log(max(L, S)) + SD**2 / 2.0 + 3.5
ALPHA = MATCH / (SIG * np.sqrt(C / 2.0))


def interior_mask(h, w, b):
    vh = (np.arange(h) >= b) & (np.arange(h) < h - b)
    vw = (np.arange(w) >= b) & (np.arange(w) < w - b)
    return (vh[:, None] & vw[None, :]).reshape(-1)


def softmax(v, axis):
    e = np.exp(v - v.max(axis=axis, keepdims=True))
    return e / e.sum(axis=axis, keepdims=True)


def pick(h, w):
    rep = np.random.permutation(np.flatnonzero(interior_mask(h, w, BORDER)))[:ND]
    rest = np.random.permutation(np.setdiff1d(np.arange(h * w), rep))[:NM]
    return rep, rest


def setup_inputs():
    s = mx_kscale(C)
    x0 = np.random.standard_normal((B, L, C))
    x1 = np.random.standard_normal((B, S, C))
    for n in range(B):
        r0, m0 = pick(H0, W0)
        r1, m1 = pick(H1, W1)
        x1[n, m1] = ALPHA * x0[n, m0] + np.sqrt(1.0 - ALPHA**2) * x1[n, m1]
        x0[n, r0] = DUP * x0[n, m0[:ND]]
        x1[n, r1] = DUP * x1[n, m1[:ND]]
    w = np.random.standard_normal((C, C)) * G / np.sqrt(C) / s[None, :]
    words, scales = pack_weight(np.ascontiguousarray(w.T), "e4m3")
    return {"feat_c0": bf(x0 * s),
            "feat_c1": bf(x1 * s),
            "W_words": words,
            "W_scales": scales,
            "b": bf(np.random.standard_normal(C) * RB * G),
            "h0c": H0, "w0c": W0, "h1c": H1, "w1c": W1}


def reference(feat_c0, feat_c1, W_words, W_scales, b, h0c, w0c, h1c, w1c):
    scale = feat_c0.shape[-1] ** 0.5
    wt = unpack_weight(W_words, W_scales, "e4m3")
    f0 = ((mxq(f64(feat_c0), 2, "e4m3") @ wt) + f64(b)) / scale
    f1 = ((mxq(f64(feat_c1), 2, "e4m3") @ wt) + f64(b)) / scale
    sim = (mxq(f0, 2, "e4m3") @ mxq(f1, 2, "e4m3").transpose(0, 2, 1)) / TEMPERATURE

    conf_0to1 = softmax(sim, 2)
    conf_1to0 = softmax(sim, 1)

    mask = (conf_0to1 > THR) & (conf_0to1 == conf_0to1.max(axis=2, keepdims=True))
    mask = mask | ((conf_1to0 > THR) & (conf_1to0 == conf_1to0.max(axis=1, keepdims=True)))

    mask = mask & interior_mask(h0c, w0c, BORDER)[None, :, None]
    mask = mask & interior_mask(h1c, w1c, BORDER)[None, None, :]

    mconf = np.where(mask, np.maximum(conf_0to1, conf_1to0), 0.0)
    return np.stack([conf_0to1, conf_1to0, mconf])

@@ -1,0 +1,315 @@
+from contextlib import ExitStack
+
+import concourse.mybir as mybir
+from concourse.masks import make_identity
+
+F32 = mybir.dt.float32
+BF16 = mybir.dt.bfloat16
+U8 = mybir.dt.uint8
+U32 = mybir.dt.uint32
+I32 = mybir.dt.int32
+FP8X4 = mybir.dt.float8_e4m3fn_x4
+ALU = mybir.AluOpType
+FUNC = mybir.ActivationFunctionType
+AXIS = mybir.AxisListType
+
+P = 128
+PACK = 4
+C = P * PACK
+BATCH = 2
+CELLS = 768
+TILES = CELLS // P
+GRID_W = 32
+BORDER = 2
+EDGE = BORDER * GRID_W
+INNER_ROWS = CELLS // GRID_W - 2 * BORDER
+INNER_COLS = GRID_W - 2 * BORDER
+BANK = 512
+BANK0_ROWS = (BANK - EDGE) // GRID_W
+INV_SQRT_C = 1.0 / (C ** 0.5)
+INV_TEMPERATURE = 10.0
+THRESHOLD = 0.2
+NEVER = 1.0e38
+
+FLOPS = 2 * (2 * BATCH * CELLS) * C * C + 2 * BATCH * CELLS * CELLS * C
+
+
+def inner_cells(cells):
+    return cells.rearrange("p (g c) -> p g c", c=GRID_W)[:, :, BORDER:GRID_W - BORDER]
+
+
+def tile_coarsematching_kernel(
+    tc, feat_c0, feat_c1, W_words, W_scales, b, h0c, w0c, h1c, w1c, out
+):
+    nc = tc.nc
+    with ExitStack() as ctx:
+        const = ctx.enter_context(tc.tile_pool(name="const", bufs=1))
+        keep = ctx.enter_context(tc.tile_pool(name="keep", bufs=1))
+        stage = ctx.enter_context(tc.tile_pool(name="stage", bufs=3))
+        work = ctx.enter_context(tc.tile_pool(name="work", bufs=3))
+        psum_one = ctx.enter_context(tc.psum_pool(name="psum_one", bufs=2))
+        psum_two = ctx.enter_context(tc.psum_pool(name="psum_two", bufs=3))
+
+        w_plane = const.tile([P, C], U8, align_bytes=64)
+        nc.vector.memset(w_plane[:].bitcast(I32), 0)
+        for quadrant in range(4):
+            nc.sync.dma_start(
+                out=w_plane[32 * quadrant:32 * quadrant + 4, :].bitcast(I32),
+                in_=W_scales[0, 4 * quadrant:4 * quadrant + 4, :].bitcast(I32),
+            )
+        bias_rows = const.tile([P, P], BF16)
+        nc.vector.memset(bias_rows[:], 0.0)
+        nc.sync.dma_start(out=bias_rows[0:PACK, :], in_=b.rearrange("(t p) -> t p", p=P))
+        w_words = const.tile([P, C], U32, align_bytes=64)
+        nc.sync.dma_start(
+            out=w_words[:].bitcast(I32),
+            in_=W_words[0].rearrange("p n t -> p (n t)").bitcast(I32),
+        )
+
+        x_sb = {}
+        for n in range(BATCH):
+            x0 = keep.tile([P, TILES, C], BF16, name="x0_%d" % n)
+            nc.sync.dma_start(
+                out=x0[:, 0:TILES - 1, :],
+                in_=feat_c0[n, EDGE:CELLS - EDGE, :].rearrange("(j p) k -> p j k", p=P),
+            )
+            nc.sync.dma_start(out=x0[0:EDGE, TILES - 1, :], in_=feat_c0[n, CELLS - EDGE:CELLS, :])
+            nc.sync.dma_start(out=x0[EDGE:P, TILES - 1, :], in_=feat_c0[n, 0:EDGE, :])
+            x1 = keep.tile([P, TILES, C], BF16, name="x1_%d" % n)
+            nc.sync.dma_start(out=x1[:], in_=feat_c1[n].rearrange("(j p) k -> p j k", p=P))
+            x_sb[(0, n)] = x0
+            x_sb[(1, n)] = x1
+
+        ident = const.tile([P, P], F32)
+        make_identity(nc, ident[:])
+        ident_bf = const.tile([P, P], BF16)
+        make_identity(nc, ident_bf[:])
+
+        zeros = const.tile([P, CELLS], F32)
+        nc.gpsimd.memset(zeros[:], 0.0)
+        mconf_tiles = []
+        for slot in range(3):
+            mconf_sb = const.tile([P, CELLS], F32, name="mconf_%d" % slot)
+            nc.gpsimd.memset(mconf_sb[:], 0.0)
+            mconf_tiles.append(mconf_sb)
+
+        bias_ps = psum_one.tile([P, P], BF16, tag="one")
+        nc.tensor.transpose(bias_ps[:], bias_rows[:], ident_bf[:])
+        bias4 = const.tile([P, PACK], F32)
+        nc.vector.tensor_scalar(
+            out=bias4[:], in0=bias_ps[:, 0:PACK], scalar1=INV_SQRT_C, scalar2=None, op0=ALU.mult
+        )
+
+        pattern = const.tile([P, P], F32)
+        nc.vector.memset(pattern[:], 0.0)
+        nc.vector.memset(inner_cells(pattern[:]), 1.0)
+        pattern_ps = psum_one.tile([P, P], F32, tag="one")
+        nc.tensor.transpose(pattern_ps[:], pattern[:], ident[:])
+        inner_row = const.tile([P, 1], F32)
+        nc.vector.tensor_copy(out=inner_row[:], in_=pattern_ps[:, 0:1])
+        floor_row = const.tile([P, 1], F32)
+        nc.vector.tensor_scalar(
+            out=floor_row[:], in0=inner_row[:], scalar1=-2.0 * NEVER, scalar2=NEVER,
+            op0=ALU.mult, op1=ALU.add,
+        )
+
+        def project(side, n):
+            x_rows = x_sb[(side, n)]
+            x_codes = keep.tile([P, CELLS], U32, align_bytes=64, name="xc_%d_%d" % (side, n))
+            x_plane = keep.tile([P, CELLS], U8, align_bytes=64, name="xp_%d_%d" % (side, n))
+            f_codes = keep.tile([P, CELLS], U32, align_bytes=64, name="fc_%d_%d" % (side, n))
+            f_plane = keep.tile([P, CELLS], U8, align_bytes=64, name="fp_%d_%d" % (side, n))
+            for pair in range(TILES // 2):
+                cols = slice(2 * P * pair, 2 * P * (pair + 1))
+                x_t = psum_one.tile([P, 2, 2 * P], F32, tag="one")
+                for half in range(2):
+                    words = x_rows[:, 2 * pair + half, :].bitcast(F32)
+                    for u in range(2):
+                        nc.tensor.transpose(
+                            x_t[:, u, half * P:(half + 1) * P], words[:, u:C // 2:2], ident[:]
+                        )
+                x_grouped = stage.tile([P, 2 * P * PACK], BF16, align_bytes=64, tag="xg")
+                nc.scalar.copy(
+                    out=x_grouped[:].bitcast(F32).rearrange("p (r u) -> p r u", u=2),
+                    in_=x_t[:].rearrange("p u r -> p r u"),
+                )
+                nc.vector.quantize_mx(
+                    out=x_codes[:, cols].bitcast(FP8X4), scales=x_plane[:, cols], in_=x_grouped[:]
+                )
+            for pair in range(TILES // 2):
+                cols = slice(2 * P * pair, 2 * P * (pair + 1))
+                f_grouped = stage.tile([P, 2 * P, PACK], BF16, align_bytes=64, tag="fg")
+                for half in range(2):
+                    rows = slice((2 * pair + half) * P, (2 * pair + half + 1) * P)
+                    acc = psum_one.tile([P, PACK, P], F32, tag="one")
+                    for t in range(PACK):
+                        nc.tensor.matmul_mx(
+                            out=acc[:, t, :],
+                            lhsT=w_words[:, t * P:(t + 1) * P].bitcast(FP8X4),
+                            lhsT_scale=w_plane[:, t * P:(t + 1) * P],
+                            rhs=x_codes[:, rows].bitcast(FP8X4),
+                            rhs_scale=x_plane[:, rows],
+                            start=True,
+                            stop=True,
+                        )
+                    nc.vector.scalar_tensor_tensor(
+                        out=f_grouped[:, half * P:(half + 1) * P, :],
+                        in0=acc[:].rearrange("p t r -> p r t"),
+                        scalar=INV_SQRT_C,
+                        in1=bias4[:].unsqueeze(1).to_broadcast([P, P, PACK]),
+                        op0=ALU.mult,
+                        op1=ALU.add,
+                    )
+                nc.vector.quantize_mx(
+                    out=f_codes[:, cols].bitcast(FP8X4),
+                    scales=f_plane[:, cols],
+                    in_=f_grouped[:].rearrange("p r t -> p (r t)"),
+                )
+            return (f_codes, f_plane)
+
+        def dot_tile(stationary, moving, j):
+            dots = psum_two.tile([P, 2, BANK], F32, tag="two")
+            for bank in range(2):
+                lo = bank * BANK
+                hi = min(CELLS, lo + BANK)
+                nc.tensor.matmul_mx(
+                    out=dots[:, bank, 0:hi - lo],
+                    lhsT=stationary[0][:, j * P:(j + 1) * P].bitcast(FP8X4),
+                    lhsT_scale=stationary[1][:, j * P:(j + 1) * P],
+                    rhs=moving[0][:, lo:hi].bitcast(FP8X4),
+                    rhs_scale=moving[1][:, lo:hi],
+                    start=True,
+                    stop=True,
+                )
+            return dots
+
+        def softmax(stationary, moving, label):
+            part_top = keep.tile([P, TILES, 2], F32, name="ptop_" + label)
+            for j in range(TILES):
+                dots = dot_tile(stationary, moving, j)
+                nc.vector.reduce_max(out=part_top[:, j, 0:1], in_=dots[:, 0, :], axis=AXIS.X)
+                nc.vector.reduce_max(
+                    out=part_top[:, j, 1:2], in_=dots[:, 1, 0:CELLS - BANK], axis=AXIS.X
+                )
+            top = keep.tile([P, TILES], F32, name="top_" + label)
+            nc.vector.tensor_reduce(out=top[:], in_=part_top[:], axis=AXIS.X, op=ALU.max)
+            shift = keep.tile([P, TILES], F32, name="shift_" + label)
+            nc.vector.tensor_scalar(
+                out=shift[:], in0=top[:], scalar1=-INV_TEMPERATURE, scalar2=None, op0=ALU.mult
+            )
+            part_sum = keep.tile([P, TILES, 2], F32, name="psum_" + label)
+            conf = []
+            for j in range(TILES):
+                dots = dot_tile(stationary, moving, j)
+                e = keep.tile([P, CELLS], F32, name="e_%s_%d" % (label, j))
+                nc.scalar.activation(
+                    out=e[:, 0:BANK], in_=dots[:, 0, :], func=FUNC.Exp,
+                    bias=shift[:, j:j + 1], scale=INV_TEMPERATURE, accum_out=part_sum[:, j, 0:1],
+                )
+                nc.scalar.activation(
+                    out=e[:, BANK:CELLS], in_=dots[:, 1, 0:CELLS - BANK], func=FUNC.Exp,
+                    bias=shift[:, j:j + 1], scale=INV_TEMPERATURE, accum_out=part_sum[:, j, 1:2],
+                )
+                conf.append(e)
+            total = keep.tile([P, TILES], F32, name="total_" + label)
+            nc.vector.tensor_reduce(out=total[:], in_=part_sum[:], axis=AXIS.X, op=ALU.add)
+            inv = keep.tile([P, TILES], F32, name="inv_" + label)
+            nc.vector.reciprocal(out=inv[:], in_=total[:])
+            for j in range(TILES):
+                nc.gpsimd.tensor_scalar(
+                    out=conf[j][:], in0=conf[j][:], scalar1=inv[:, j:j + 1], scalar2=0.0,
+                    op0=ALU.mult, op1=ALU.add,
+                )
+            return conf, top, inv
+
+        def store(plane, n, i, rows_sb):
+            if i < TILES - 1:
+                nc.sync.dma_start(out=out[plane, n, EDGE + i * P:EDGE + (i + 1) * P, :], in_=rows_sb[:])
+            else:
+                nc.sync.dma_start(out=out[plane, n, CELLS - EDGE:CELLS, :], in_=rows_sb[0:EDGE, :])
+                nc.sync.dma_start(out=out[plane, n, 0:EDGE, :], in_=rows_sb[EDGE:P, :])
+
+        def column_bars(n, top1, inv1):
+            bar1 = keep.tile([P, TILES], F32, name="bar1_%d" % n)
+            nc.vector.tensor_scalar(out=bar1[:], in0=inv1[:], scalar1=THRESHOLD, scalar2=None, op0=ALU.is_gt)
+            nc.vector.tensor_scalar(
+                out=bar1[:], in0=bar1[:], scalar1=-2.0 * NEVER, scalar2=NEVER, op0=ALU.mult, op1=ALU.add
+            )
+            nc.vector.tensor_tensor(out=bar1[:], in0=bar1[:], in1=top1[:], op=ALU.max)
+            bar1_rep = work.tile([P, TILES, P], F32, tag="rep")
+            nc.vector.tensor_copy(out=bar1_rep[:], in_=bar1[:].unsqueeze(2).to_broadcast([P, TILES, P]))
+            bar1_ps = psum_two.tile([P, 2, BANK], F32, tag="two")
+            for j in range(TILES):
+                nc.tensor.transpose(
+                    bar1_ps[:, j // 4, (j % 4) * P:(j % 4 + 1) * P], bar1_rep[:, j, :], ident[:]
+                )
+            bar1_all = keep.tile([P, CELLS], F32, name="bar1all_%d" % n)
+            nc.scalar.copy(out=bar1_all[:, 0:BANK], in_=bar1_ps[:, 0, :])
+            nc.scalar.copy(out=bar1_all[:, BANK:CELLS], in_=bar1_ps[:, 1, 0:CELLS - BANK])
+            return bar1_all
+
+        def row_bars(n, top0, inv0):
+            bar0 = keep.tile([P, TILES], F32, name="bar0_%d" % n)
+            nc.vector.tensor_scalar(
+                out=bar0[:], in0=inv0[:], scalar1=THRESHOLD, scalar2=inner_row[:, 0:1],
+                op0=ALU.is_gt, op1=ALU.mult,
+            )
+            nc.vector.tensor_scalar(
+                out=bar0[:], in0=bar0[:], scalar1=-2.0 * NEVER, scalar2=NEVER, op0=ALU.mult, op1=ALU.add
+            )
+            nc.vector.tensor_tensor(out=bar0[:], in0=bar0[:], in1=top0[:], op=ALU.max)
+            return bar0
+
+        def finish(n, f0, f1, conf0, conf1_t, bar0, bar1_all):
+            for i in range(TILES):
+                conf1_ps = psum_two.tile([P, 2, BANK], F32, tag="two")
+                for j in range(TILES):
+                    nc.tensor.transpose(
+                        conf1_ps[:, j // 4, (j % 4) * P:(j % 4 + 1) * P],
+                        conf1_t[j][:, i * P:(i + 1) * P],
+                        ident[:],
+                    )
+                conf1 = work.tile([P, CELLS], F32, tag="conf1")
+                nc.scalar.copy(out=conf1[:, 0:BANK], in_=conf1_ps[:, 0, :])
+                nc.scalar.copy(out=conf1[:, BANK:CELLS], in_=conf1_ps[:, 1, 0:CELLS - BANK])
+                store(1, n, i, conf1)
+                if i == TILES - 1:
+                    store(2, n, i, zeros)
+                    continue
+                bar = work.tile([P, INNER_ROWS, INNER_COLS], F32, tag="bar")
+                nc.gpsimd.tensor_scalar(
+                    out=bar[:], in0=inner_cells(bar1_all[:, EDGE:CELLS - EDGE]),
+                    scalar1=bar0[:, i:i + 1], scalar2=floor_row[:, 0:1], op0=ALU.min, op1=ALU.max,
+                )
+                dots = dot_tile(f0, f1, i)
+                kept = work.tile([P, INNER_ROWS, INNER_COLS], F32, tag="kept")
+                best = work.tile([P, INNER_ROWS, INNER_COLS], F32, tag="best")
+                conf0_inner = inner_cells(conf0[i][:, EDGE:CELLS - EDGE])
+                for bank in range(2):
+                    g = slice(0, BANK0_ROWS) if bank == 0 else slice(BANK0_ROWS, INNER_ROWS)
+                    c = slice(EDGE, BANK) if bank == 0 else slice(0, CELLS - EDGE - BANK)
+                    nc.vector.tensor_tensor(
+                        out=kept[:, g, :], in0=bar[:, g, :], in1=inner_cells(dots[:, bank, c]), op=ALU.is_le
+                    )
+                    nc.vector.tensor_tensor(
+                        out=best[:, g, :], in0=conf0_inner[:, g, :], in1=inner_cells(conf1_ps[:, bank, c]),
+                        op=ALU.max,
+                    )
+                mconf_sb = mconf_tiles[i % 3]
+                nc.gpsimd.tensor_tensor(
+                    out=inner_cells(mconf_sb[:, EDGE:CELLS - EDGE]), in0=kept[:], in1=best[:], op=ALU.mult
+                )
+                store(2, n, i, mconf_sb)
+
+        batches = range(BATCH)
+        f0 = [project(0, n) for n in batches]
+        f1 = [project(1, n) for n in batches]
+        columns = [softmax(f1[n], f0[n], "c%d" % n) for n in batches]
+        bar1_all = [column_bars(n, columns[n][1], columns[n][2]) for n in batches]
+        rows = [softmax(f0[n], f1[n], "r%d" % n) for n in batches]
+        for n in batches:
+            for i in range(TILES):
+                store(0, n, i, rows[n][0][i])
+        bar0 = [row_bars(n, rows[n][1], rows[n][2]) for n in batches]
+        for n in batches:
+            finish(n, f0[n], f1[n], rows[n][0], columns[n][0], bar0[n], bar1_all[n])

@@ -19,6 +19,8 @@ C = P * PACK
 BATCH = 2
 CELLS = 768
 TILES = CELLS // P
+QUAD = 4 * P
+QUADS = 2 * CELLS // QUAD
 GRID_W = 32
 BORDER = 2
 EDGE = BORDER * GRID_W
@@ -26,6 +28,9 @@ INNER_ROWS = CELLS // GRID_W - 2 * BORDER
 INNER_COLS = GRID_W - 2 * BORDER
 BANK = 512
 BANK0_ROWS = (BANK - EDGE) // GRID_W
+GRID1 = 0
+GRID0 = CELLS
+LAG = 2
 INV_SQRT_C = 1.0 / (C ** 0.5)
 INV_TEMPERATURE = 10.0
 THRESHOLD = 0.2
@@ -45,10 +50,8 @@ def tile_coarsematching_kernel(
     with ExitStack() as ctx:
         const = ctx.enter_context(tc.tile_pool(name="const", bufs=1))
         keep = ctx.enter_context(tc.tile_pool(name="keep", bufs=1))
-        stage = ctx.enter_context(tc.tile_pool(name="stage", bufs=3))
-        work = ctx.enter_context(tc.tile_pool(name="work", bufs=3))
-        psum_one = ctx.enter_context(tc.psum_pool(name="psum_one", bufs=2))
-        psum_two = ctx.enter_context(tc.psum_pool(name="psum_two", bufs=3))
+        stage = ctx.enter_context(tc.tile_pool(name="stage", bufs=2))
+        psum = ctx.enter_context(tc.psum_pool(name="psum", bufs=4))
 
         w_plane = const.tile([P, C], U8, align_bytes=64)
         nc.vector.memset(w_plane[:].bitcast(I32), 0)
@@ -60,31 +63,31 @@ def tile_coarsematching_kernel(
         bias_rows = const.tile([P, P], BF16)
         nc.vector.memset(bias_rows[:], 0.0)
         nc.sync.dma_start(out=bias_rows[0:PACK, :], in_=b.rearrange("(t p) -> t p", p=P))
-        w_words = const.tile([P, C], U32, align_bytes=64)
-        nc.sync.dma_start(
-            out=w_words[:].bitcast(I32),
-            in_=W_words[0].rearrange("p n t -> p (n t)").bitcast(I32),
-        )
 
-        x_sb = {}
+        x_sb = []
         for n in range(BATCH):
-            x0 = keep.tile([P, TILES, C], BF16, name="x0_%d" % n)
+            x_rows = keep.tile([P, 2 * TILES, C], BF16, name="x_%d" % n)
             nc.sync.dma_start(
-                out=x0[:, 0:TILES - 1, :],
+                out=x_rows[:, 0:TILES, :], in_=feat_c1[n].rearrange("(j p) k -> p j k", p=P)
+            )
+            nc.sync.dma_start(
+                out=x_rows[:, TILES:2 * TILES - 1, :],
                 in_=feat_c0[n, EDGE:CELLS - EDGE, :].rearrange("(j p) k -> p j k", p=P),
             )
-            nc.sync.dma_start(out=x0[0:EDGE, TILES - 1, :], in_=feat_c0[n, CELLS - EDGE:CELLS, :])
-            nc.sync.dma_start(out=x0[EDGE:P, TILES - 1, :], in_=feat_c0[n, 0:EDGE, :])
-            x1 = keep.tile([P, TILES, C], BF16, name="x1_%d" % n)
-            nc.sync.dma_start(out=x1[:], in_=feat_c1[n].rearrange("(j p) k -> p j k", p=P))
-            x_sb[(0, n)] = x0
-            x_sb[(1, n)] = x1
+            nc.sync.dma_start(out=x_rows[0:EDGE, 2 * TILES - 1, :], in_=feat_c0[n, CELLS - EDGE:CELLS, :])
+            nc.sync.dma_start(out=x_rows[EDGE:P, 2 * TILES - 1, :], in_=feat_c0[n, 0:EDGE, :])
+            x_sb.append(x_rows)
+            if n == 0:
+                w_words = const.tile([P, C], U32, align_bytes=64)
+                nc.sync.dma_start(
+                    out=w_words[:].bitcast(I32),
+                    in_=W_words[0].rearrange("p n t -> p (n t)").bitcast(I32),
+                )
 
         ident = const.tile([P, P], F32)
         make_identity(nc, ident[:])
         ident_bf = const.tile([P, P], BF16)
         make_identity(nc, ident_bf[:])
-
         zeros = const.tile([P, CELLS], F32)
         nc.gpsimd.memset(zeros[:], 0.0)
         mconf_tiles = []
@@ -92,153 +95,157 @@ def tile_coarsematching_kernel(
             mconf_sb = const.tile([P, CELLS], F32, name="mconf_%d" % slot)
             nc.gpsimd.memset(mconf_sb[:], 0.0)
             mconf_tiles.append(mconf_sb)
+        warm = const.tile([P, 1], F32)
+        nc.vector.memset(warm[:], 0.0)
+        nc.scalar.activation(out=warm[:], in_=warm[:], func=FUNC.Exp)
+        floor_free = const.tile([P, P], F32)
+        nc.vector.memset(floor_free[:], NEVER)
+        nc.vector.memset(inner_cells(floor_free[:]), -NEVER)
 
-        bias_ps = psum_one.tile([P, P], BF16, tag="one")
-        nc.tensor.transpose(bias_ps[:], bias_rows[:], ident_bf[:])
-        bias4 = const.tile([P, PACK], F32)
-        nc.vector.tensor_scalar(
-            out=bias4[:], in0=bias_ps[:, 0:PACK], scalar1=INV_SQRT_C, scalar2=None, op0=ALU.mult
-        )
+        x_codes = [keep.tile([P, 2 * CELLS], U32, align_bytes=64, name="xc_%d" % n) for n in range(BATCH)]
+        x_plane = [keep.tile([P, 2 * CELLS], U8, align_bytes=64, name="xp_%d" % n) for n in range(BATCH)]
+        f_codes = [keep.tile([P, 2 * CELLS], U32, align_bytes=64, name="fc_%d" % n) for n in range(BATCH)]
+        f_plane = [keep.tile([P, 2 * CELLS], U8, align_bytes=64, name="fp_%d" % n) for n in range(BATCH)]
 
-        pattern = const.tile([P, P], F32)
-        nc.vector.memset(pattern[:], 0.0)
-        nc.vector.memset(inner_cells(pattern[:]), 1.0)
-        pattern_ps = psum_one.tile([P, P], F32, tag="one")
-        nc.tensor.transpose(pattern_ps[:], pattern[:], ident[:])
-        inner_row = const.tile([P, 1], F32)
-        nc.vector.tensor_copy(out=inner_row[:], in_=pattern_ps[:, 0:1])
-        floor_row = const.tile([P, 1], F32)
-        nc.vector.tensor_scalar(
-            out=floor_row[:], in0=inner_row[:], scalar1=-2.0 * NEVER, scalar2=NEVER,
-            op0=ALU.mult, op1=ALU.add,
-        )
-
-        def project(side, n):
-            x_rows = x_sb[(side, n)]
-            x_codes = keep.tile([P, CELLS], U32, align_bytes=64, name="xc_%d_%d" % (side, n))
-            x_plane = keep.tile([P, CELLS], U8, align_bytes=64, name="xp_%d_%d" % (side, n))
-            f_codes = keep.tile([P, CELLS], U32, align_bytes=64, name="fc_%d_%d" % (side, n))
-            f_plane = keep.tile([P, CELLS], U8, align_bytes=64, name="fp_%d_%d" % (side, n))
-            for pair in range(TILES // 2):
-                cols = slice(2 * P * pair, 2 * P * (pair + 1))
-                x_t = psum_one.tile([P, 2, 2 * P], F32, tag="one")
+        def transpose_quad(n, q):
+            x_t = psum.tile([P, 2, 2, 2 * P], F32, tag="two")
+            for bank in range(2):
                 for half in range(2):
-                    words = x_rows[:, 2 * pair + half, :].bitcast(F32)
+                    words = x_sb[n][:, 4 * q + 2 * bank + half, :].bitcast(F32)
                     for u in range(2):
                         nc.tensor.transpose(
-                            x_t[:, u, half * P:(half + 1) * P], words[:, u:C // 2:2], ident[:]
+                            x_t[:, bank, u, half * P:(half + 1) * P], words[:, u:C // 2:2], ident[:]
                         )
-                x_grouped = stage.tile([P, 2 * P * PACK], BF16, align_bytes=64, tag="xg")
+            x_grouped = stage.tile([P, QUAD * PACK], BF16, align_bytes=64, tag="xg")
+            for bank in range(2):
                 nc.scalar.copy(
-                    out=x_grouped[:].bitcast(F32).rearrange("p (r u) -> p r u", u=2),
-                    in_=x_t[:].rearrange("p u r -> p r u"),
+                    out=x_grouped[:, bank * QUAD * 2:(bank + 1) * QUAD * 2]
+                    .bitcast(F32).rearrange("p (r u) -> p r u", u=2),
+                    in_=x_t[:, bank].rearrange("p u r -> p r u"),
                 )
-                nc.vector.quantize_mx(
-                    out=x_codes[:, cols].bitcast(FP8X4), scales=x_plane[:, cols], in_=x_grouped[:]
-                )
-            for pair in range(TILES // 2):
-                cols = slice(2 * P * pair, 2 * P * (pair + 1))
-                f_grouped = stage.tile([P, 2 * P, PACK], BF16, align_bytes=64, tag="fg")
-                for half in range(2):
-                    rows = slice((2 * pair + half) * P, (2 * pair + half + 1) * P)
-                    acc = psum_one.tile([P, PACK, P], F32, tag="one")
+            cells = slice(q * QUAD, (q + 1) * QUAD)
+            nc.vector.quantize_mx(
+                out=x_codes[n][:, cells].bitcast(FP8X4), scales=x_plane[n][:, cells], in_=x_grouped[:]
+            )
+
+        def project_quad(n, q):
+            f_grouped = stage.tile([P, QUAD, PACK], BF16, align_bytes=64, tag="fg")
+            for pair in range(2):
+                acc = psum.tile([P, 2, PACK, P], F32, tag="two")
+                for bank in range(2):
+                    first = (2 * pair + bank) * P
+                    cells = slice(q * QUAD + first, q * QUAD + first + P)
                     for t in range(PACK):
                         nc.tensor.matmul_mx(
-                            out=acc[:, t, :],
+                            out=acc[:, bank, t, :],
                             lhsT=w_words[:, t * P:(t + 1) * P].bitcast(FP8X4),
                             lhsT_scale=w_plane[:, t * P:(t + 1) * P],
-                            rhs=x_codes[:, rows].bitcast(FP8X4),
-                            rhs_scale=x_plane[:, rows],
+                            rhs=x_codes[n][:, cells].bitcast(FP8X4),
+                            rhs_scale=x_plane[n][:, cells],
                             start=True,
                             stop=True,
                         )
                     nc.vector.scalar_tensor_tensor(
-                        out=f_grouped[:, half * P:(half + 1) * P, :],
-                        in0=acc[:].rearrange("p t r -> p r t"),
+                        out=f_grouped[:, first:first + P, :],
+                        in0=acc[:, bank].rearrange("p t r -> p r t"),
                         scalar=INV_SQRT_C,
                         in1=bias4[:].unsqueeze(1).to_broadcast([P, P, PACK]),
                         op0=ALU.mult,
                         op1=ALU.add,
                     )
-                nc.vector.quantize_mx(
-                    out=f_codes[:, cols].bitcast(FP8X4),
-                    scales=f_plane[:, cols],
-                    in_=f_grouped[:].rearrange("p r t -> p (r t)"),
-                )
-            return (f_codes, f_plane)
+            cells = slice(q * QUAD, (q + 1) * QUAD)
+            nc.vector.quantize_mx(
+                out=f_codes[n][:, cells].bitcast(FP8X4),
+                scales=f_plane[n][:, cells],
+                in_=f_grouped[:].rearrange("p r t -> p (r t)"),
+            )
 
-        def dot_tile(stationary, moving, j):
-            dots = psum_two.tile([P, 2, BANK], F32, tag="two")
+        def dot_tile(n, own, other, j):
+            dots = psum.tile([P, 2, BANK], F32, tag="two")
             for bank in range(2):
                 lo = bank * BANK
                 hi = min(CELLS, lo + BANK)
                 nc.tensor.matmul_mx(
                     out=dots[:, bank, 0:hi - lo],
-                    lhsT=stationary[0][:, j * P:(j + 1) * P].bitcast(FP8X4),
-                    lhsT_scale=stationary[1][:, j * P:(j + 1) * P],
-                    rhs=moving[0][:, lo:hi].bitcast(FP8X4),
-                    rhs_scale=moving[1][:, lo:hi],
+                    lhsT=f_codes[n][:, own + j * P:own + (j + 1) * P].bitcast(FP8X4),
+                    lhsT_scale=f_plane[n][:, own + j * P:own + (j + 1) * P],
+                    rhs=f_codes[n][:, other + lo:other + hi].bitcast(FP8X4),
+                    rhs_scale=f_plane[n][:, other + lo:other + hi],
                     start=True,
                     stop=True,
                 )
             return dots
 
-        def softmax(stationary, moving, label):
-            part_top = keep.tile([P, TILES, 2], F32, name="ptop_" + label)
-            for j in range(TILES):
-                dots = dot_tile(stationary, moving, j)
-                nc.vector.reduce_max(out=part_top[:, j, 0:1], in_=dots[:, 0, :], axis=AXIS.X)
-                nc.vector.reduce_max(
-                    out=part_top[:, j, 1:2], in_=dots[:, 1, 0:CELLS - BANK], axis=AXIS.X
-                )
-            top = keep.tile([P, TILES], F32, name="top_" + label)
-            nc.vector.tensor_reduce(out=top[:], in_=part_top[:], axis=AXIS.X, op=ALU.max)
-            shift = keep.tile([P, TILES], F32, name="shift_" + label)
+        def open_softmax(n, own, other, label):
+            return {
+                "n": n,
+                "own": own,
+                "other": other,
+                "label": label,
+                "part_top": keep.tile([P, TILES, 2], F32, name="ptop_" + label),
+                "shift": keep.tile([P, TILES], F32, name="shift_" + label),
+                "part_sum": keep.tile([P, TILES, 2], F32, name="psum_" + label),
+                "conf": [keep.tile([P, CELLS], F32, name="e_%s_%d" % (label, j)) for j in range(TILES)],
+            }
+
+        waiting = []
+
+        def softmax_tile(group, j):
+            dots = dot_tile(group["n"], group["own"], group["other"], j)
+            part_top = group["part_top"]
+            nc.vector.reduce_max(out=part_top[:, j, 0:1], in_=dots[:, 0, :], axis=AXIS.X)
+            nc.vector.reduce_max(out=part_top[:, j, 1:2], in_=dots[:, 1, 0:CELLS - BANK], axis=AXIS.X)
+            softmax_exp()
+            waiting.append((group, j, dots))
+
+        def softmax_exp():
+            if not waiting:
+                return
+            group, j, dots = waiting.pop()
+            part_top = group["part_top"]
+            shift = group["shift"]
             nc.vector.tensor_scalar(
-                out=shift[:], in0=top[:], scalar1=-INV_TEMPERATURE, scalar2=None, op0=ALU.mult
+                out=shift[:, j:j + 1], in0=part_top[:, j, 0:1], scalar1=part_top[:, j, 1:2],
+                scalar2=-INV_TEMPERATURE, op0=ALU.max, op1=ALU.mult,
             )
-            part_sum = keep.tile([P, TILES, 2], F32, name="psum_" + label)
-            conf = []
-            for j in range(TILES):
-                dots = dot_tile(stationary, moving, j)
-                e = keep.tile([P, CELLS], F32, name="e_%s_%d" % (label, j))
-                nc.scalar.activation(
-                    out=e[:, 0:BANK], in_=dots[:, 0, :], func=FUNC.Exp,
-                    bias=shift[:, j:j + 1], scale=INV_TEMPERATURE, accum_out=part_sum[:, j, 0:1],
-                )
-                nc.scalar.activation(
-                    out=e[:, BANK:CELLS], in_=dots[:, 1, 0:CELLS - BANK], func=FUNC.Exp,
-                    bias=shift[:, j:j + 1], scale=INV_TEMPERATURE, accum_out=part_sum[:, j, 1:2],
-                )
-                conf.append(e)
+            e = group["conf"][j]
+            nc.scalar.activation(
+                out=e[:, 0:BANK], in_=dots[:, 0, :], func=FUNC.Exp,
+                bias=shift[:, j:j + 1], scale=INV_TEMPERATURE, accum_out=group["part_sum"][:, j, 0:1],
+            )
+            nc.scalar.activation(
+                out=e[:, BANK:CELLS], in_=dots[:, 1, 0:CELLS - BANK], func=FUNC.Exp,
+                bias=shift[:, j:j + 1], scale=INV_TEMPERATURE, accum_out=group["part_sum"][:, j, 1:2],
+            )
+
+        def close_softmax(group):
+            label = group["label"]
             total = keep.tile([P, TILES], F32, name="total_" + label)
-            nc.vector.tensor_reduce(out=total[:], in_=part_sum[:], axis=AXIS.X, op=ALU.add)
+            nc.vector.tensor_reduce(out=total[:], in_=group["part_sum"][:], axis=AXIS.X, op=ALU.add)
             inv = keep.tile([P, TILES], F32, name="inv_" + label)
             nc.vector.reciprocal(out=inv[:], in_=total[:])
             for j in range(TILES):
                 nc.gpsimd.tensor_scalar(
-                    out=conf[j][:], in0=conf[j][:], scalar1=inv[:, j:j + 1], scalar2=0.0,
+                    out=group["conf"][j][:], in0=group["conf"][j][:], scalar1=inv[:, j:j + 1], scalar2=0.0,
                     op0=ALU.mult, op1=ALU.add,
                 )
-            return conf, top, inv
-
-        def store(plane, n, i, rows_sb):
-            if i < TILES - 1:
-                nc.sync.dma_start(out=out[plane, n, EDGE + i * P:EDGE + (i + 1) * P, :], in_=rows_sb[:])
-            else:
-                nc.sync.dma_start(out=out[plane, n, CELLS - EDGE:CELLS, :], in_=rows_sb[0:EDGE, :])
-                nc.sync.dma_start(out=out[plane, n, 0:EDGE, :], in_=rows_sb[EDGE:P, :])
-
-        def column_bars(n, top1, inv1):
-            bar1 = keep.tile([P, TILES], F32, name="bar1_%d" % n)
-            nc.vector.tensor_scalar(out=bar1[:], in0=inv1[:], scalar1=THRESHOLD, scalar2=None, op0=ALU.is_gt)
+            top = keep.tile([P, TILES], F32, name="top_" + label)
+            nc.vector.tensor_reduce(out=top[:], in_=group["part_top"][:], axis=AXIS.X, op=ALU.max)
+            bar = keep.tile([P, TILES], F32, name="bar_" + label)
+            nc.vector.tensor_scalar(out=bar[:], in0=inv[:], scalar1=THRESHOLD, scalar2=None, op0=ALU.is_gt)
             nc.vector.tensor_scalar(
-                out=bar1[:], in0=bar1[:], scalar1=-2.0 * NEVER, scalar2=NEVER, op0=ALU.mult, op1=ALU.add
+                out=bar[:], in0=bar[:], scalar1=-2.0 * NEVER, scalar2=NEVER, op0=ALU.mult, op1=ALU.add
             )
-            nc.vector.tensor_tensor(out=bar1[:], in0=bar1[:], in1=top1[:], op=ALU.max)
-            bar1_rep = work.tile([P, TILES, P], F32, tag="rep")
-            nc.vector.tensor_copy(out=bar1_rep[:], in_=bar1[:].unsqueeze(2).to_broadcast([P, TILES, P]))
-            bar1_ps = psum_two.tile([P, 2, BANK], F32, tag="two")
+            nc.vector.tensor_tensor(out=bar[:], in0=bar[:], in1=top[:], op=ALU.max)
+            return bar
+
+        def spread(n, bar1):
+            bar1_rep = keep.tile([P, TILES, P], F32, name="rep_%d" % n)
+            nc.vector.tensor_tensor(
+                out=bar1_rep[:], in0=bar1[:].unsqueeze(2).to_broadcast([P, TILES, P]),
+                in1=floor_free[:].unsqueeze(1).to_broadcast([P, TILES, P]), op=ALU.max,
+            )
+            bar1_ps = psum.tile([P, 2, BANK], F32, tag="two")
             for j in range(TILES):
                 nc.tensor.transpose(
                     bar1_ps[:, j // 4, (j % 4) * P:(j % 4 + 1) * P], bar1_rep[:, j, :], ident[:]
@@ -248,68 +255,108 @@ def tile_coarsematching_kernel(
             nc.scalar.copy(out=bar1_all[:, BANK:CELLS], in_=bar1_ps[:, 1, 0:CELLS - BANK])
             return bar1_all
 
-        def row_bars(n, top0, inv0):
-            bar0 = keep.tile([P, TILES], F32, name="bar0_%d" % n)
-            nc.vector.tensor_scalar(
-                out=bar0[:], in0=inv0[:], scalar1=THRESHOLD, scalar2=inner_row[:, 0:1],
-                op0=ALU.is_gt, op1=ALU.mult,
-            )
-            nc.vector.tensor_scalar(
-                out=bar0[:], in0=bar0[:], scalar1=-2.0 * NEVER, scalar2=NEVER, op0=ALU.mult, op1=ALU.add
-            )
-            nc.vector.tensor_tensor(out=bar0[:], in0=bar0[:], in1=top0[:], op=ALU.max)
-            return bar0
+        def store(plane, n, i, rows_sb):
+            if i < TILES - 1:
+                nc.sync.dma_start(out=out[plane, n, EDGE + i * P:EDGE + (i + 1) * P, :], in_=rows_sb[:])
+            else:
+                nc.sync.dma_start(out=out[plane, n, CELLS - EDGE:CELLS, :], in_=rows_sb[0:EDGE, :])
+                nc.sync.dma_start(out=out[plane, n, 0:EDGE, :], in_=rows_sb[EDGE:P, :])
 
-        def finish(n, f0, f1, conf0, conf1_t, bar0, bar1_all):
-            for i in range(TILES):
-                conf1_ps = psum_two.tile([P, 2, BANK], F32, tag="two")
-                for j in range(TILES):
-                    nc.tensor.transpose(
-                        conf1_ps[:, j // 4, (j % 4) * P:(j % 4 + 1) * P],
-                        conf1_t[j][:, i * P:(i + 1) * P],
-                        ident[:],
-                    )
-                conf1 = work.tile([P, CELLS], F32, tag="conf1")
-                nc.scalar.copy(out=conf1[:, 0:BANK], in_=conf1_ps[:, 0, :])
-                nc.scalar.copy(out=conf1[:, BANK:CELLS], in_=conf1_ps[:, 1, 0:CELLS - BANK])
-                store(1, n, i, conf1)
-                if i == TILES - 1:
-                    store(2, n, i, zeros)
-                    continue
-                bar = work.tile([P, INNER_ROWS, INNER_COLS], F32, tag="bar")
-                nc.gpsimd.tensor_scalar(
-                    out=bar[:], in0=inner_cells(bar1_all[:, EDGE:CELLS - EDGE]),
-                    scalar1=bar0[:, i:i + 1], scalar2=floor_row[:, 0:1], op0=ALU.min, op1=ALU.max,
-                )
-                dots = dot_tile(f0, f1, i)
-                kept = work.tile([P, INNER_ROWS, INNER_COLS], F32, tag="kept")
-                best = work.tile([P, INNER_ROWS, INNER_COLS], F32, tag="best")
-                conf0_inner = inner_cells(conf0[i][:, EDGE:CELLS - EDGE])
-                for bank in range(2):
-                    g = slice(0, BANK0_ROWS) if bank == 0 else slice(BANK0_ROWS, INNER_ROWS)
-                    c = slice(EDGE, BANK) if bank == 0 else slice(0, CELLS - EDGE - BANK)
-                    nc.vector.tensor_tensor(
-                        out=kept[:, g, :], in0=bar[:, g, :], in1=inner_cells(dots[:, bank, c]), op=ALU.is_le
-                    )
-                    nc.vector.tensor_tensor(
-                        out=best[:, g, :], in0=conf0_inner[:, g, :], in1=inner_cells(conf1_ps[:, bank, c]),
-                        op=ALU.max,
-                    )
-                mconf_sb = mconf_tiles[i % 3]
-                nc.gpsimd.tensor_tensor(
-                    out=inner_cells(mconf_sb[:, EDGE:CELLS - EDGE]), in0=kept[:], in1=best[:], op=ALU.mult
-                )
-                store(2, n, i, mconf_sb)
+        conf1_sb = [
+            [keep.tile([P, CELLS], F32, name="conf1_%d_%d" % (n, i)) for i in range(TILES)]
+            for n in range(BATCH)
+        ]
 
-        batches = range(BATCH)
-        f0 = [project(0, n) for n in batches]
-        f1 = [project(1, n) for n in batches]
-        columns = [softmax(f1[n], f0[n], "c%d" % n) for n in batches]
-        bar1_all = [column_bars(n, columns[n][1], columns[n][2]) for n in batches]
-        rows = [softmax(f0[n], f1[n], "r%d" % n) for n in batches]
-        for n in batches:
+        def bring_home(n, i, conf1_t):
+            conf1_ps = psum.tile([P, 2, BANK], F32, tag="two")
+            for j in range(TILES):
+                nc.tensor.transpose(
+                    conf1_ps[:, j // 4, (j % 4) * P:(j % 4 + 1) * P], conf1_t[j][:, i * P:(i + 1) * P], ident[:]
+                )
+            conf1 = conf1_sb[n][i]
+            nc.scalar.copy(out=conf1[:, 0:BANK], in_=conf1_ps[:, 0, :])
+            nc.scalar.copy(out=conf1[:, BANK:CELLS], in_=conf1_ps[:, 1, 0:CELLS - BANK])
+            store(1, n, i, conf1)
+            if i == TILES - 1:
+                store(2, n, i, zeros)
+
+        def match_tile(n, i, conf0, bar0, bar1_all):
+            dots = dot_tile(n, GRID0, GRID1, i)
+            kept = stage.tile([P, INNER_ROWS, INNER_COLS], F32, tag="kept")
+            bar1_inner = inner_cells(bar1_all[:, EDGE:CELLS - EDGE])
+            for bank in range(2):
+                g = slice(0, BANK0_ROWS) if bank == 0 else slice(BANK0_ROWS, INNER_ROWS)
+                c = slice(EDGE, BANK) if bank == 0 else slice(0, CELLS - EDGE - BANK)
+                nc.vector.scalar_tensor_tensor(
+                    out=kept[:, g, :], in0=bar1_inner[:, g, :], scalar=bar0[:, i:i + 1],
+                    in1=inner_cells(dots[:, bank, c]), op0=ALU.min, op1=ALU.is_le,
+                )
+            best = stage.tile([P, INNER_ROWS, INNER_COLS], F32, tag="best")
+            nc.vector.tensor_tensor(
+                out=best[:], in0=inner_cells(conf0[i][:, EDGE:CELLS - EDGE]),
+                in1=inner_cells(conf1_sb[n][i][:, EDGE:CELLS - EDGE]), op=ALU.max,
+            )
+            mconf_sb = mconf_tiles[i % 3]
+            nc.gpsimd.tensor_tensor(
+                out=inner_cells(mconf_sb[:, EDGE:CELLS - EDGE]), in0=kept[:], in1=best[:], op=ALU.mult
+            )
+            store(2, n, i, mconf_sb)
+
+        def close_rows(n):
+            bar = close_softmax(rows[n])
+            nc.vector.tensor_scalar(out=bar[:], in0=bar[:], scalar1=floor_row[:, 0:1], scalar2=None, op0=ALU.max)
             for i in range(TILES):
-                store(0, n, i, rows[n][0][i])
-        bar0 = [row_bars(n, rows[n][1], rows[n][2]) for n in batches]
-        for n in batches:
-            finish(n, f0[n], f1[n], rows[n][0], columns[n][0], bar0[n], bar1_all[n])
+                store(0, n, i, rows[n]["conf"][i])
+            return bar
+
+        columns = [open_softmax(n, GRID1, GRID0, "c%d" % n) for n in range(BATCH)]
+        rows = [open_softmax(n, GRID0, GRID1, "r%d" % n) for n in range(BATCH)]
+        bar0 = [None, None]
+        bar1_all = [None, None]
+
+        transpose_quad(0, 0)
+        transpose_quad(0, 1)
+        bias_ps = psum.tile([P, P], BF16, tag="two")
+        nc.tensor.transpose(bias_ps[:], bias_rows[:], ident_bf[:])
+        bias4 = const.tile([P, PACK], F32)
+        nc.vector.tensor_scalar(
+            out=bias4[:], in0=bias_ps[:, 0:PACK], scalar1=INV_SQRT_C, scalar2=None, op0=ALU.mult
+        )
+        project_quad(0, 0)
+        transpose_quad(0, 2)
+        project_quad(0, 1)
+        project_quad(0, 2)
+        floor_ps = psum.tile([P, P], F32, tag="two")
+        nc.tensor.transpose(floor_ps[:], floor_free[:], ident[:])
+        floor_row = const.tile([P, 1], F32)
+        nc.vector.tensor_copy(out=floor_row[:], in_=floor_ps[:, 0:1])
+
+        for j in range(TILES):
+            softmax_tile(rows[0], j)
+            if j % 2 == 1:
+                transpose_quad(1, j // 2)
+        for j in range(TILES):
+            softmax_tile(columns[0], j)
+            if j == LAG:
+                bar0[0] = close_rows(0)
+            if j % 2 == 1:
+                project_quad(1, j // 2)
+
+        for k in range(2 * TILES):
+            softmax_tile(columns[1] if k < TILES else rows[1], k % TILES)
+            if k == LAG:
+                bar1_all[0] = spread(0, close_softmax(columns[0]))
+            if k == TILES + LAG:
+                bar1_all[1] = spread(1, close_softmax(columns[1]))
+            home = k - LAG - 1
+            if home >= 0:
+                bring_home(home // TILES, home % TILES, columns[home // TILES]["conf"])
+            if home >= 1 and home % 2 == 1:
+                match_tile(0, home // 2, rows[0]["conf"], bar0[0], bar1_all[0])
+        softmax_exp()
+        for home in range(2 * TILES - LAG - 1, 2 * TILES):
+            bring_home(1, home % TILES, columns[1]["conf"])
+        match_tile(0, TILES - 2, rows[0]["conf"], bar0[0], bar1_all[0])
+        bar0[1] = close_rows(1)
+        for i in range(TILES - 1):
+            match_tile(1, i, rows[1]["conf"], bar0[1], bar1_all[1])

@@ -30,7 +30,6 @@ BANK = 512
 BANK0_ROWS = (BANK - EDGE) // GRID_W
 GRID1 = 0
 GRID0 = CELLS
-LAG = 2
 INV_SQRT_C = 1.0 / (C ** 0.5)
 INV_TEMPERATURE = 10.0
 THRESHOLD = 0.2
@@ -52,6 +51,7 @@ def tile_coarsematching_kernel(
         keep = ctx.enter_context(tc.tile_pool(name="keep", bufs=1))
         stage = ctx.enter_context(tc.tile_pool(name="stage", bufs=2))
         psum = ctx.enter_context(tc.psum_pool(name="psum", bufs=4))
+        ctx.enter_context(tc.manual_schedule())
 
         w_plane = const.tile([P, C], U8, align_bytes=64)
         nc.vector.memset(w_plane[:].bitcast(I32), 0)
@@ -98,67 +98,96 @@ def tile_coarsematching_kernel(
         warm = const.tile([P, 1], F32)
         nc.vector.memset(warm[:], 0.0)
         nc.scalar.activation(out=warm[:], in_=warm[:], func=FUNC.Exp)
-        floor_free = const.tile([P, P], F32)
-        nc.vector.memset(floor_free[:], NEVER)
-        nc.vector.memset(inner_cells(floor_free[:]), -NEVER)
+        handicap_free = const.tile([P, P], F32)
+        nc.vector.memset(handicap_free[:], NEVER)
+        nc.vector.memset(inner_cells(handicap_free[:]), 0.0)
 
         x_codes = [keep.tile([P, 2 * CELLS], U32, align_bytes=64, name="xc_%d" % n) for n in range(BATCH)]
         x_plane = [keep.tile([P, 2 * CELLS], U8, align_bytes=64, name="xp_%d" % n) for n in range(BATCH)]
         f_codes = [keep.tile([P, 2 * CELLS], U32, align_bytes=64, name="fc_%d" % n) for n in range(BATCH)]
         f_plane = [keep.tile([P, 2 * CELLS], U8, align_bytes=64, name="fp_%d" % n) for n in range(BATCH)]
 
-        def transpose_quad(n, q):
-            x_t = psum.tile([P, 2, 2, 2 * P], F32, tag="two")
-            for bank in range(2):
-                for half in range(2):
-                    words = x_sb[n][:, 4 * q + 2 * bank + half, :].bitcast(F32)
-                    for u in range(2):
-                        nc.tensor.transpose(
-                            x_t[:, bank, u, half * P:(half + 1) * P], words[:, u:C // 2:2], ident[:]
-                        )
-            x_grouped = stage.tile([P, QUAD * PACK], BF16, align_bytes=64, tag="xg")
-            for bank in range(2):
-                nc.scalar.copy(
-                    out=x_grouped[:, bank * QUAD * 2:(bank + 1) * QUAD * 2]
-                    .bitcast(F32).rearrange("p (r u) -> p r u", u=2),
-                    in_=x_t[:, bank].rearrange("p u r -> p r u"),
-                )
-            cells = slice(q * QUAD, (q + 1) * QUAD)
-            nc.vector.quantize_mx(
-                out=x_codes[n][:, cells].bitcast(FP8X4), scales=x_plane[n][:, cells], in_=x_grouped[:]
-            )
+        bias4 = const.tile([P, PACK], F32)
+        handicap_row = const.tile([P, 1], F32)
+        live = {}
 
-        def project_quad(n, q):
-            f_grouped = stage.tile([P, QUAD, PACK], BF16, align_bytes=64, tag="fg")
-            for pair in range(2):
-                acc = psum.tile([P, 2, PACK, P], F32, tag="two")
+        def stage1_fill(n, u):
+            if u < QUADS:
+                x_t = psum.tile([P, 2, 2, 2 * P], F32, tag="two")
                 for bank in range(2):
-                    first = (2 * pair + bank) * P
-                    cells = slice(q * QUAD + first, q * QUAD + first + P)
-                    for t in range(PACK):
-                        nc.tensor.matmul_mx(
-                            out=acc[:, bank, t, :],
-                            lhsT=w_words[:, t * P:(t + 1) * P].bitcast(FP8X4),
-                            lhsT_scale=w_plane[:, t * P:(t + 1) * P],
-                            rhs=x_codes[n][:, cells].bitcast(FP8X4),
-                            rhs_scale=x_plane[n][:, cells],
-                            start=True,
-                            stop=True,
-                        )
-                    nc.vector.scalar_tensor_tensor(
-                        out=f_grouped[:, first:first + P, :],
-                        in0=acc[:, bank].rearrange("p t r -> p r t"),
-                        scalar=INV_SQRT_C,
-                        in1=bias4[:].unsqueeze(1).to_broadcast([P, P, PACK]),
-                        op0=ALU.mult,
-                        op1=ALU.add,
+                    for half in range(2):
+                        words = x_sb[n][:, 4 * u + 2 * bank + half, :].bitcast(F32)
+                        for w in range(2):
+                            nc.tensor.transpose(
+                                x_t[:, bank, w, half * P:(half + 1) * P], words[:, w:C // 2:2], ident[:]
+                            )
+                live[("s1", n, u)] = x_t
+            else:
+                q, pair = (u - QUADS) // 2, (u - QUADS) % 2
+                cells = slice(q * QUAD, (q + 1) * QUAD)
+                acc = psum.tile([P, 2, BANK], F32, tag="two")
+                for bank in range(2):
+                    t = 2 * pair + bank
+                    nc.tensor.matmul_mx(
+                        out=acc[:, bank, :],
+                        lhsT=w_words[:, t * P:(t + 1) * P].bitcast(FP8X4),
+                        lhsT_scale=w_plane[:, t * P:(t + 1) * P],
+                        rhs=x_codes[n][:, cells].bitcast(FP8X4),
+                        rhs_scale=x_plane[n][:, cells],
+                        start=True,
+                        stop=True,
                     )
-            cells = slice(q * QUAD, (q + 1) * QUAD)
-            nc.vector.quantize_mx(
-                out=f_codes[n][:, cells].bitcast(FP8X4),
-                scales=f_plane[n][:, cells],
-                in_=f_grouped[:].rearrange("p r t -> p (r t)"),
-            )
+                live[("s1", n, u)] = acc
+
+        def stage1_drain(n, u):
+            filled = live.pop(("s1", n, u))
+            if u < QUADS:
+                x_grouped = stage.tile([P, QUAD * PACK], BF16, align_bytes=64, tag="xg")
+                for bank in range(2):
+                    nc.scalar.copy(
+                        out=x_grouped[:, bank * QUAD * 2:(bank + 1) * QUAD * 2]
+                        .bitcast(F32).rearrange("p (r w) -> p r w", w=2),
+                        in_=filled[:, bank].rearrange("p w r -> p r w"),
+                    )
+                live[("xg", n, u)] = x_grouped
+            else:
+                q, pair = (u - QUADS) // 2, (u - QUADS) % 2
+                if pair == 0:
+                    live[("planes", n, q)] = stage.tile([P, PACK, QUAD], BF16, tag="planes", name="planes")
+                planes = live[("planes", n, q)]
+                for bank in range(2):
+                    t = 2 * pair + bank
+                    nc.scalar.activation(
+                        out=planes[:, t, :], in_=filled[:, bank, :], func=FUNC.Identity,
+                        bias=bias4[:, t:t + 1], scale=INV_SQRT_C,
+                    )
+
+        def stage1_post(n, u):
+            if u < QUADS:
+                cells = slice(u * QUAD, (u + 1) * QUAD)
+                nc.vector.quantize_mx(
+                    out=x_codes[n][:, cells].bitcast(FP8X4), scales=x_plane[n][:, cells],
+                    in_=live.pop(("xg", n, u))[:],
+                )
+            elif (u - QUADS) % 2 == 1:
+                q = (u - QUADS) // 2
+                cells = slice(q * QUAD, (q + 1) * QUAD)
+                f_grouped = stage.tile([P, QUAD, PACK], BF16, align_bytes=64, tag="fg")
+                nc.vector.tensor_copy(out=f_grouped[:], in_=live.pop(("planes", n, q))[:].rearrange("p t r -> p r t"))
+                nc.vector.quantize_mx(
+                    out=f_codes[n][:, cells].bitcast(FP8X4), scales=f_plane[n][:, cells],
+                    in_=f_grouped[:].rearrange("p r t -> p (r t)"),
+                )
+
+        UNITS = 3 * QUADS
+
+        def stage1_step(n, step):
+            if 0 <= step - 1 < UNITS:
+                stage1_drain(n, step - 1)
+            if 0 <= step - 2 < UNITS:
+                stage1_post(n, step - 2)
+            if 0 <= step < UNITS:
+                stage1_fill(n, step)
 
         def dot_tile(n, own, other, j):
             dots = psum.tile([P, 2, BANK], F32, tag="two")
@@ -177,38 +206,31 @@ def tile_coarsematching_kernel(
             return dots
 
         def open_softmax(n, own, other, label):
-            return {
-                "n": n,
-                "own": own,
-                "other": other,
-                "label": label,
-                "part_top": keep.tile([P, TILES, 2], F32, name="ptop_" + label),
-                "shift": keep.tile([P, TILES], F32, name="shift_" + label),
-                "part_sum": keep.tile([P, TILES, 2], F32, name="psum_" + label),
-                "conf": [keep.tile([P, CELLS], F32, name="e_%s_%d" % (label, j)) for j in range(TILES)],
-            }
+            group = {"n": n, "own": own, "other": other, "label": label}
+            group["part_top"] = keep.tile([P, TILES, 2], F32, name="ptop_" + label)
+            group["part_sum"] = keep.tile([P, TILES, 2], F32, name="psum_" + label)
+            for what in ("shift", "total", "inv", "low", "top", "bar"):
+                group[what] = keep.tile([P, TILES], F32, name=what + "_" + label)
+            group["conf"] = [keep.tile([P, CELLS], F32, name="e_%s_%d" % (label, j)) for j in range(TILES)]
+            return group
 
-        waiting = []
+        def softmax_fill(group, j):
+            live[("dots", group["label"], j)] = dot_tile(group["n"], group["own"], group["other"], j)
 
-        def softmax_tile(group, j):
-            dots = dot_tile(group["n"], group["own"], group["other"], j)
+        def softmax_max(group, j):
+            dots = live[("dots", group["label"], j)]
             part_top = group["part_top"]
             nc.vector.reduce_max(out=part_top[:, j, 0:1], in_=dots[:, 0, :], axis=AXIS.X)
             nc.vector.reduce_max(out=part_top[:, j, 1:2], in_=dots[:, 1, 0:CELLS - BANK], axis=AXIS.X)
-            softmax_exp()
-            waiting.append((group, j, dots))
-
-        def softmax_exp():
-            if not waiting:
-                return
-            group, j, dots = waiting.pop()
-            part_top = group["part_top"]
-            shift = group["shift"]
             nc.vector.tensor_scalar(
-                out=shift[:, j:j + 1], in0=part_top[:, j, 0:1], scalar1=part_top[:, j, 1:2],
+                out=group["shift"][:, j:j + 1], in0=part_top[:, j, 0:1], scalar1=part_top[:, j, 1:2],
                 scalar2=-INV_TEMPERATURE, op0=ALU.max, op1=ALU.mult,
             )
+
+        def softmax_exp(group, j):
+            dots = live.pop(("dots", group["label"], j))
             e = group["conf"][j]
+            shift = group["shift"]
             nc.scalar.activation(
                 out=e[:, 0:BANK], in_=dots[:, 0, :], func=FUNC.Exp,
                 bias=shift[:, j:j + 1], scale=INV_TEMPERATURE, accum_out=group["part_sum"][:, j, 0:1],
@@ -218,42 +240,25 @@ def tile_coarsematching_kernel(
                 bias=shift[:, j:j + 1], scale=INV_TEMPERATURE, accum_out=group["part_sum"][:, j, 1:2],
             )
 
-        def close_softmax(group):
-            label = group["label"]
-            total = keep.tile([P, TILES], F32, name="total_" + label)
-            nc.vector.tensor_reduce(out=total[:], in_=group["part_sum"][:], axis=AXIS.X, op=ALU.add)
-            inv = keep.tile([P, TILES], F32, name="inv_" + label)
-            nc.vector.reciprocal(out=inv[:], in_=total[:])
-            for j in range(TILES):
+        def divide(group, first, count):
+            js = slice(first, first + count)
+            nc.vector.tensor_reduce(out=group["total"][:, js], in_=group["part_sum"][:, js, :], axis=AXIS.X, op=ALU.add)
+            nc.vector.reciprocal(out=group["inv"][:, js], in_=group["total"][:, js])
+            for j in range(first, first + count):
+                conf = group["conf"][j]
                 nc.gpsimd.tensor_scalar(
-                    out=group["conf"][j][:], in0=group["conf"][j][:], scalar1=inv[:, j:j + 1], scalar2=0.0,
+                    out=conf[:], in0=conf[:], scalar1=group["inv"][:, j:j + 1], scalar2=0.0,
                     op0=ALU.mult, op1=ALU.add,
                 )
-            top = keep.tile([P, TILES], F32, name="top_" + label)
-            nc.vector.tensor_reduce(out=top[:], in_=group["part_top"][:], axis=AXIS.X, op=ALU.max)
-            bar = keep.tile([P, TILES], F32, name="bar_" + label)
-            nc.vector.tensor_scalar(out=bar[:], in0=inv[:], scalar1=THRESHOLD, scalar2=None, op0=ALU.is_gt)
-            nc.vector.tensor_scalar(
-                out=bar[:], in0=bar[:], scalar1=-2.0 * NEVER, scalar2=NEVER, op0=ALU.mult, op1=ALU.add
-            )
-            nc.vector.tensor_tensor(out=bar[:], in0=bar[:], in1=top[:], op=ALU.max)
-            return bar
 
-        def spread(n, bar1):
-            bar1_rep = keep.tile([P, TILES, P], F32, name="rep_%d" % n)
-            nc.vector.tensor_tensor(
-                out=bar1_rep[:], in0=bar1[:].unsqueeze(2).to_broadcast([P, TILES, P]),
-                in1=floor_free[:].unsqueeze(1).to_broadcast([P, TILES, P]), op=ALU.max,
-            )
-            bar1_ps = psum.tile([P, 2, BANK], F32, tag="two")
-            for j in range(TILES):
-                nc.tensor.transpose(
-                    bar1_ps[:, j // 4, (j % 4) * P:(j % 4 + 1) * P], bar1_rep[:, j, :], ident[:]
-                )
-            bar1_all = keep.tile([P, CELLS], F32, name="bar1all_%d" % n)
-            nc.scalar.copy(out=bar1_all[:, 0:BANK], in_=bar1_ps[:, 0, :])
-            nc.scalar.copy(out=bar1_all[:, BANK:CELLS], in_=bar1_ps[:, 1, 0:CELLS - BANK])
-            return bar1_all
+        def set_bars(group, first, count, handicap):
+            js = slice(first, first + count)
+            low, top, bar = group["low"], group["top"], group["bar"]
+            nc.vector.tensor_reduce(out=top[:, js], in_=group["part_top"][:, js, :], axis=AXIS.X, op=ALU.max)
+            nc.vector.tensor_scalar(out=low[:, js], in0=group["inv"][:, js], scalar1=THRESHOLD, scalar2=NEVER, op0=ALU.is_le, op1=ALU.mult)
+            if handicap is not None:
+                nc.vector.tensor_scalar(out=low[:, js], in0=low[:, js], scalar1=handicap[:, 0:1], scalar2=None, op0=ALU.max)
+            nc.vector.tensor_tensor(out=bar[:, js], in0=low[:, js], in1=top[:, js], op=ALU.add)
 
         def store(plane, n, i, rows_sb):
             if i < TILES - 1:
@@ -266,97 +271,114 @@ def tile_coarsematching_kernel(
             [keep.tile([P, CELLS], F32, name="conf1_%d_%d" % (n, i)) for i in range(TILES)]
             for n in range(BATCH)
         ]
+        bar1_rep = [keep.tile([P, TILES, P], F32, name="rep_%d" % n) for n in range(BATCH)]
+        bar1_all = [keep.tile([P, CELLS], F32, name="bar1all_%d" % n) for n in range(BATCH)]
 
-        def bring_home(n, i, conf1_t):
-            conf1_ps = psum.tile([P, 2, BANK], F32, tag="two")
+        def home_fill(n, u):
+            back = psum.tile([P, 2, BANK], F32, tag="two")
             for j in range(TILES):
-                nc.tensor.transpose(
-                    conf1_ps[:, j // 4, (j % 4) * P:(j % 4 + 1) * P], conf1_t[j][:, i * P:(i + 1) * P], ident[:]
-                )
-            conf1 = conf1_sb[n][i]
-            nc.scalar.copy(out=conf1[:, 0:BANK], in_=conf1_ps[:, 0, :])
-            nc.scalar.copy(out=conf1[:, BANK:CELLS], in_=conf1_ps[:, 1, 0:CELLS - BANK])
-            store(1, n, i, conf1)
-            if i == TILES - 1:
-                store(2, n, i, zeros)
+                source = bar1_rep[n][:, j, :] if u == 0 else columns[n]["conf"][j][:, (u - 1) * P:u * P]
+                nc.tensor.transpose(back[:, j // 4, (j % 4) * P:(j % 4 + 1) * P], source, ident[:])
+            live[("home", n, u)] = back
 
-        def match_tile(n, i, conf0, bar0, bar1_all):
-            dots = dot_tile(n, GRID0, GRID1, i)
+        def home_drain(n, u):
+            back = live.pop(("home", n, u))
+            target = bar1_all[n] if u == 0 else conf1_sb[n][u - 1]
+            nc.scalar.copy(out=target[:, 0:BANK], in_=back[:, 0, :])
+            nc.scalar.copy(out=target[:, BANK:CELLS], in_=back[:, 1, 0:CELLS - BANK])
+            if u > 0:
+                store(1, n, u - 1, target)
+            if u == TILES:
+                store(2, n, TILES - 1, zeros)
+
+        def match_fill(n, i):
+            live[("match", n, i)] = dot_tile(n, GRID0, GRID1, i)
+
+        def match_keep(n, i):
+            dots = live.pop(("match", n, i))
             kept = stage.tile([P, INNER_ROWS, INNER_COLS], F32, tag="kept")
-            bar1_inner = inner_cells(bar1_all[:, EDGE:CELLS - EDGE])
+            bar1_inner = inner_cells(bar1_all[n][:, EDGE:CELLS - EDGE])
             for bank in range(2):
                 g = slice(0, BANK0_ROWS) if bank == 0 else slice(BANK0_ROWS, INNER_ROWS)
                 c = slice(EDGE, BANK) if bank == 0 else slice(0, CELLS - EDGE - BANK)
                 nc.vector.scalar_tensor_tensor(
-                    out=kept[:, g, :], in0=bar1_inner[:, g, :], scalar=bar0[:, i:i + 1],
+                    out=kept[:, g, :], in0=bar1_inner[:, g, :], scalar=rows[n]["bar"][:, i:i + 1],
                     in1=inner_cells(dots[:, bank, c]), op0=ALU.min, op1=ALU.is_le,
                 )
             best = stage.tile([P, INNER_ROWS, INNER_COLS], F32, tag="best")
             nc.vector.tensor_tensor(
-                out=best[:], in0=inner_cells(conf0[i][:, EDGE:CELLS - EDGE]),
+                out=best[:], in0=inner_cells(rows[n]["conf"][i][:, EDGE:CELLS - EDGE]),
                 in1=inner_cells(conf1_sb[n][i][:, EDGE:CELLS - EDGE]), op=ALU.max,
             )
-            mconf_sb = mconf_tiles[i % 3]
+            mconf_sb = mconf_tiles[(n * (TILES - 1) + i) % len(mconf_tiles)]
             nc.gpsimd.tensor_tensor(
                 out=inner_cells(mconf_sb[:, EDGE:CELLS - EDGE]), in0=kept[:], in1=best[:], op=ALU.mult
             )
             store(2, n, i, mconf_sb)
 
-        def close_rows(n):
-            bar = close_softmax(rows[n])
-            nc.vector.tensor_scalar(out=bar[:], in0=bar[:], scalar1=floor_row[:, 0:1], scalar2=None, op0=ALU.max)
-            for i in range(TILES):
-                store(0, n, i, rows[n]["conf"][i])
-            return bar
-
         columns = [open_softmax(n, GRID1, GRID0, "c%d" % n) for n in range(BATCH)]
         rows = [open_softmax(n, GRID0, GRID1, "r%d" % n) for n in range(BATCH)]
-        bar0 = [None, None]
-        bar1_all = [None, None]
+        groups = [rows[0], columns[0], columns[1], rows[1]]
+        ROUNDS_SM = len(groups) * TILES
+        PAIR = 2
+        CL = 1
+        LEAD = 10
+        HOME = [14, 21]
+        MATCH = [16, 24]
+        LAST = max(MATCH[1] + TILES, HOME[1] + TILES + 2)
 
-        transpose_quad(0, 0)
-        transpose_quad(0, 1)
-        bias_ps = psum.tile([P, P], BF16, tag="two")
-        nc.tensor.transpose(bias_ps[:], bias_rows[:], ident_bf[:])
-        bias4 = const.tile([P, PACK], F32)
-        nc.vector.tensor_scalar(
-            out=bias4[:], in0=bias_ps[:, 0:PACK], scalar1=INV_SQRT_C, scalar2=None, op0=ALU.mult
-        )
-        project_quad(0, 0)
-        transpose_quad(0, 2)
-        project_quad(0, 1)
-        project_quad(0, 2)
-        floor_ps = psum.tile([P, P], F32, tag="two")
-        nc.tensor.transpose(floor_ps[:], floor_free[:], ident[:])
-        floor_row = const.tile([P, 1], F32)
-        nc.vector.tensor_copy(out=floor_row[:], in_=floor_ps[:, 0:1])
+        def stage1_of(r):
+            return ((0, r + LEAD), (1, r))
 
-        for j in range(TILES):
-            softmax_tile(rows[0], j)
-            if j % 2 == 1:
-                transpose_quad(1, j // 2)
-        for j in range(TILES):
-            softmax_tile(columns[0], j)
-            if j == LAG:
-                bar0[0] = close_rows(0)
-            if j % 2 == 1:
-                project_quad(1, j // 2)
-
-        for k in range(2 * TILES):
-            softmax_tile(columns[1] if k < TILES else rows[1], k % TILES)
-            if k == LAG:
-                bar1_all[0] = spread(0, close_softmax(columns[0]))
-            if k == TILES + LAG:
-                bar1_all[1] = spread(1, close_softmax(columns[1]))
-            home = k - LAG - 1
-            if home >= 0:
-                bring_home(home // TILES, home % TILES, columns[home // TILES]["conf"])
-            if home >= 1 and home % 2 == 1:
-                match_tile(0, home // 2, rows[0]["conf"], bar0[0], bar1_all[0])
-        softmax_exp()
-        for home in range(2 * TILES - LAG - 1, 2 * TILES):
-            bring_home(1, home % TILES, columns[1]["conf"])
-        match_tile(0, TILES - 2, rows[0]["conf"], bar0[0], bar1_all[0])
-        bar0[1] = close_rows(1)
-        for i in range(TILES - 1):
-            match_tile(1, i, rows[1]["conf"], bar0[1], bar1_all[1])
+        for r in range(-LEAD, LAST + 1):
+            if 0 <= r < ROUNDS_SM:
+                softmax_max(groups[r // TILES], r % TILES)
+            for n, step in stage1_of(r):
+                if 0 <= step - 1 < UNITS:
+                    stage1_drain(n, step - 1)
+            for n in range(BATCH):
+                if 0 <= r - 1 - HOME[n] <= TILES:
+                    home_drain(n, r - 1 - HOME[n])
+            if 0 <= r < ROUNDS_SM:
+                softmax_exp(groups[r // TILES], r % TILES)
+            for n in range(BATCH):
+                if 0 <= r - 1 - MATCH[n] < TILES - 1:
+                    match_keep(n, r - 1 - MATCH[n])
+            for n, step in stage1_of(r):
+                if 0 <= step - 2 < UNITS:
+                    stage1_post(n, step - 2)
+            t_last = r - CL
+            if 0 <= t_last < ROUNDS_SM and t_last % PAIR == PAIR - 1:
+                group = groups[t_last // TILES]
+                first = t_last % TILES - PAIR + 1
+                divide(group, first, PAIR)
+                n = group["n"]
+                if group is rows[n]:
+                    set_bars(group, first, PAIR, handicap_row)
+                    for i in range(first, first + PAIR):
+                        store(0, n, i, group["conf"][i])
+                elif first + PAIR == TILES:
+                    set_bars(group, 0, TILES, None)
+                    nc.vector.tensor_tensor(
+                        out=bar1_rep[n][:], in0=group["bar"][:].unsqueeze(2).to_broadcast([P, TILES, P]),
+                        in1=handicap_free[:].unsqueeze(1).to_broadcast([P, TILES, P]), op=ALU.add,
+                    )
+            if 0 <= r + 1 < ROUNDS_SM:
+                softmax_fill(groups[(r + 1) // TILES], (r + 1) % TILES)
+            for n, step in stage1_of(r):
+                if 0 <= step < UNITS:
+                    stage1_fill(n, step)
+            if r == 1 - LEAD:
+                bias_ps = psum.tile([P, P], BF16, tag="two")
+                nc.tensor.transpose(bias_ps[:], bias_rows[:], ident_bf[:])
+                nc.vector.tensor_scalar(
+                    out=bias4[:], in0=bias_ps[:, 0:PACK], scalar1=INV_SQRT_C, scalar2=None, op0=ALU.mult
+                )
+                handicap_ps = psum.tile([P, P], F32, tag="two")
+                nc.tensor.transpose(handicap_ps[:], handicap_free[:], ident[:])
+                nc.vector.tensor_copy(out=handicap_row[:], in_=handicap_ps[:, 0:1])
+            for n in range(BATCH):
+                if 0 <= r - HOME[n] <= TILES:
+                    home_fill(n, r - HOME[n])
+                if 0 <= r - MATCH[n] < TILES - 1:
+                    match_fill(n, r - MATCH[n])

@@ -191,11 +191,11 @@ def tile_coarsematching_kernel(
 
         def dot_tile(n, own, other, j):
             dots = psum.tile([P, 2, BANK], F32, tag="two")
-            for bank in range(2):
-                lo = bank * BANK
-                hi = min(CELLS, lo + BANK)
+            for bank in (0, 0, 1, 1):
+                lo = bank * (CELLS - BANK)
+                hi = lo + BANK
                 nc.tensor.matmul_mx(
-                    out=dots[:, bank, 0:hi - lo],
+                    out=dots[:, bank, :],
                     lhsT=f_codes[n][:, own + j * P:own + (j + 1) * P].bitcast(FP8X4),
                     lhsT_scale=f_plane[n][:, own + j * P:own + (j + 1) * P],
                     rhs=f_codes[n][:, other + lo:other + hi].bitcast(FP8X4),
@@ -221,7 +221,7 @@ def tile_coarsematching_kernel(
             dots = live[("dots", group["label"], j)]
             part_top = group["part_top"]
             nc.vector.reduce_max(out=part_top[:, j, 0:1], in_=dots[:, 0, :], axis=AXIS.X)
-            nc.vector.reduce_max(out=part_top[:, j, 1:2], in_=dots[:, 1, 0:CELLS - BANK], axis=AXIS.X)
+            nc.vector.reduce_max(out=part_top[:, j, 1:2], in_=dots[:, 1, 2 * BANK - CELLS:BANK], axis=AXIS.X)
             nc.vector.tensor_scalar(
                 out=group["shift"][:, j:j + 1], in0=part_top[:, j, 0:1], scalar1=part_top[:, j, 1:2],
                 scalar2=-INV_TEMPERATURE, op0=ALU.max, op1=ALU.mult,
@@ -236,7 +236,7 @@ def tile_coarsematching_kernel(
                 bias=shift[:, j:j + 1], scale=INV_TEMPERATURE, accum_out=group["part_sum"][:, j, 0:1],
             )
             nc.scalar.activation(
-                out=e[:, BANK:CELLS], in_=dots[:, 1, 0:CELLS - BANK], func=FUNC.Exp,
+                out=e[:, BANK:CELLS], in_=dots[:, 1, 2 * BANK - CELLS:BANK], func=FUNC.Exp,
                 bias=shift[:, j:j + 1], scale=INV_TEMPERATURE, accum_out=group["part_sum"][:, j, 1:2],
             )
 
@@ -300,7 +300,7 @@ def tile_coarsematching_kernel(
             bar1_inner = inner_cells(bar1_all[n][:, EDGE:CELLS - EDGE])
             for bank in range(2):
                 g = slice(0, BANK0_ROWS) if bank == 0 else slice(BANK0_ROWS, INNER_ROWS)
-                c = slice(EDGE, BANK) if bank == 0 else slice(0, CELLS - EDGE - BANK)
+                c = slice(EDGE, BANK) if bank == 0 else slice(2 * BANK - CELLS, BANK - EDGE)
                 nc.vector.scalar_tensor_tensor(
                     out=kept[:, g, :], in0=bar1_inner[:, g, :], scalar=rows[n]["bar"][:, i:i + 1],
                     in1=inner_cells(dots[:, bank, c]), op0=ALU.min, op1=ALU.is_le,

@@ -51,7 +51,6 @@ def tile_coarsematching_kernel(
         keep = ctx.enter_context(tc.tile_pool(name="keep", bufs=1))
         stage = ctx.enter_context(tc.tile_pool(name="stage", bufs=2))
         psum = ctx.enter_context(tc.psum_pool(name="psum", bufs=4))
-        ctx.enter_context(tc.manual_schedule())
 
         w_plane = const.tile([P, C], U8, align_bytes=64)
         nc.vector.memset(w_plane[:].bitcast(I32), 0)
@@ -107,24 +106,32 @@ def tile_coarsematching_kernel(
         f_codes = [keep.tile([P, 2 * CELLS], U32, align_bytes=64, name="fc_%d" % n) for n in range(BATCH)]
         f_plane = [keep.tile([P, 2 * CELLS], U8, align_bytes=64, name="fp_%d" % n) for n in range(BATCH)]
 
-        bias4 = const.tile([P, PACK], F32)
-        handicap_row = const.tile([P, 1], F32)
-        live = {}
+        def transpose_quad(n, q):
+            x_t = psum.tile([P, 2, 2, 2 * P], F32, tag="two")
+            for bank in range(2):
+                for half in range(2):
+                    words = x_sb[n][:, 4 * q + 2 * bank + half, :].bitcast(F32)
+                    for u in range(2):
+                        nc.tensor.transpose(
+                            x_t[:, bank, u, half * P:(half + 1) * P], words[:, u:C // 2:2], ident[:]
+                        )
+            x_grouped = stage.tile([P, QUAD * PACK], BF16, align_bytes=64, tag="xg")
+            for bank in range(2):
+                nc.scalar.copy(
+                    out=x_grouped[:, bank * QUAD * 2:(bank + 1) * QUAD * 2]
+                    .bitcast(F32).rearrange("p (r u) -> p r u", u=2),
+                    in_=x_t[:, bank].rearrange("p u r -> p r u"),
+                )
+            cells = slice(q * QUAD, (q + 1) * QUAD)
+            nc.vector.quantize_mx(
+                out=x_codes[n][:, cells].bitcast(FP8X4), scales=x_plane[n][:, cells], in_=x_grouped[:]
+            )
 
-        def stage1_fill(n, u):
-            if u < QUADS:
-                x_t = psum.tile([P, 2, 2, 2 * P], F32, tag="two")
-                for bank in range(2):
-                    for half in range(2):
-                        words = x_sb[n][:, 4 * u + 2 * bank + half, :].bitcast(F32)
-                        for w in range(2):
-                            nc.tensor.transpose(
-                                x_t[:, bank, w, half * P:(half + 1) * P], words[:, w:C // 2:2], ident[:]
-                            )
-                live[("s1", n, u)] = x_t
-            else:
-                q, pair = (u - QUADS) // 2, (u - QUADS) % 2
-                cells = slice(q * QUAD, (q + 1) * QUAD)
+        def project_quad(n, q):
+            f_grouped = stage.tile([P, QUAD, PACK], BF16, align_bytes=64, tag="fg")
+            cells = slice(q * QUAD, (q + 1) * QUAD)
+            planes = stage.tile([P, PACK, QUAD], BF16, tag="planes")
+            for pair in range(2):
                 acc = psum.tile([P, 2, BANK], F32, tag="two")
                 for bank in range(2):
                     t = 2 * pair + bank
@@ -137,65 +144,24 @@ def tile_coarsematching_kernel(
                         start=True,
                         stop=True,
                     )
-                live[("s1", n, u)] = acc
-
-        def stage1_drain(n, u):
-            filled = live.pop(("s1", n, u))
-            if u < QUADS:
-                x_grouped = stage.tile([P, QUAD * PACK], BF16, align_bytes=64, tag="xg")
-                for bank in range(2):
-                    nc.scalar.copy(
-                        out=x_grouped[:, bank * QUAD * 2:(bank + 1) * QUAD * 2]
-                        .bitcast(F32).rearrange("p (r w) -> p r w", w=2),
-                        in_=filled[:, bank].rearrange("p w r -> p r w"),
-                    )
-                live[("xg", n, u)] = x_grouped
-            else:
-                q, pair = (u - QUADS) // 2, (u - QUADS) % 2
-                if pair == 0:
-                    live[("planes", n, q)] = stage.tile([P, PACK, QUAD], BF16, tag="planes", name="planes")
-                planes = live[("planes", n, q)]
-                for bank in range(2):
-                    t = 2 * pair + bank
                     nc.scalar.activation(
-                        out=planes[:, t, :], in_=filled[:, bank, :], func=FUNC.Identity,
+                        out=planes[:, t, :], in_=acc[:, bank, :], func=FUNC.Identity,
                         bias=bias4[:, t:t + 1], scale=INV_SQRT_C,
                     )
-
-        def stage1_post(n, u):
-            if u < QUADS:
-                cells = slice(u * QUAD, (u + 1) * QUAD)
-                nc.vector.quantize_mx(
-                    out=x_codes[n][:, cells].bitcast(FP8X4), scales=x_plane[n][:, cells],
-                    in_=live.pop(("xg", n, u))[:],
-                )
-            elif (u - QUADS) % 2 == 1:
-                q = (u - QUADS) // 2
-                cells = slice(q * QUAD, (q + 1) * QUAD)
-                f_grouped = stage.tile([P, QUAD, PACK], BF16, align_bytes=64, tag="fg")
-                nc.vector.tensor_copy(out=f_grouped[:], in_=live.pop(("planes", n, q))[:].rearrange("p t r -> p r t"))
-                nc.vector.quantize_mx(
-                    out=f_codes[n][:, cells].bitcast(FP8X4), scales=f_plane[n][:, cells],
-                    in_=f_grouped[:].rearrange("p r t -> p (r t)"),
-                )
-
-        UNITS = 3 * QUADS
-
-        def stage1_step(n, step):
-            if 0 <= step - 1 < UNITS:
-                stage1_drain(n, step - 1)
-            if 0 <= step - 2 < UNITS:
-                stage1_post(n, step - 2)
-            if 0 <= step < UNITS:
-                stage1_fill(n, step)
+            nc.vector.tensor_copy(out=f_grouped[:], in_=planes[:].rearrange("p t r -> p r t"))
+            nc.vector.quantize_mx(
+                out=f_codes[n][:, cells].bitcast(FP8X4),
+                scales=f_plane[n][:, cells],
+                in_=f_grouped[:].rearrange("p r t -> p (r t)"),
+            )
 
         def dot_tile(n, own, other, j):
             dots = psum.tile([P, 2, BANK], F32, tag="two")
-            for bank in (0, 0, 1, 1):
-                lo = bank * (CELLS - BANK)
-                hi = lo + BANK
+            for bank in range(2):
+                lo = bank * BANK
+                hi = min(CELLS, lo + BANK)
                 nc.tensor.matmul_mx(
-                    out=dots[:, bank, :],
+                    out=dots[:, bank, 0:hi - lo],
                     lhsT=f_codes[n][:, own + j * P:own + (j + 1) * P].bitcast(FP8X4),
                     lhsT_scale=f_plane[n][:, own + j * P:own + (j + 1) * P],
                     rhs=f_codes[n][:, other + lo:other + hi].bitcast(FP8X4),
@@ -214,51 +180,58 @@ def tile_coarsematching_kernel(
             group["conf"] = [keep.tile([P, CELLS], F32, name="e_%s_%d" % (label, j)) for j in range(TILES)]
             return group
 
-        def softmax_fill(group, j):
-            live[("dots", group["label"], j)] = dot_tile(group["n"], group["own"], group["other"], j)
-
-        def softmax_max(group, j):
-            dots = live[("dots", group["label"], j)]
+        def softmax_tile(group, j):
+            dots = dot_tile(group["n"], group["own"], group["other"], j)
             part_top = group["part_top"]
+            shift = group["shift"]
             nc.vector.reduce_max(out=part_top[:, j, 0:1], in_=dots[:, 0, :], axis=AXIS.X)
-            nc.vector.reduce_max(out=part_top[:, j, 1:2], in_=dots[:, 1, 2 * BANK - CELLS:BANK], axis=AXIS.X)
+            nc.vector.reduce_max(out=part_top[:, j, 1:2], in_=dots[:, 1, 0:CELLS - BANK], axis=AXIS.X)
             nc.vector.tensor_scalar(
-                out=group["shift"][:, j:j + 1], in0=part_top[:, j, 0:1], scalar1=part_top[:, j, 1:2],
+                out=shift[:, j:j + 1], in0=part_top[:, j, 0:1], scalar1=part_top[:, j, 1:2],
                 scalar2=-INV_TEMPERATURE, op0=ALU.max, op1=ALU.mult,
             )
-
-        def softmax_exp(group, j):
-            dots = live.pop(("dots", group["label"], j))
             e = group["conf"][j]
-            shift = group["shift"]
             nc.scalar.activation(
                 out=e[:, 0:BANK], in_=dots[:, 0, :], func=FUNC.Exp,
                 bias=shift[:, j:j + 1], scale=INV_TEMPERATURE, accum_out=group["part_sum"][:, j, 0:1],
             )
             nc.scalar.activation(
-                out=e[:, BANK:CELLS], in_=dots[:, 1, 2 * BANK - CELLS:BANK], func=FUNC.Exp,
+                out=e[:, BANK:CELLS], in_=dots[:, 1, 0:CELLS - BANK], func=FUNC.Exp,
                 bias=shift[:, j:j + 1], scale=INV_TEMPERATURE, accum_out=group["part_sum"][:, j, 1:2],
             )
 
-        def divide(group, first, count):
+        def close_softmax(group, first, count, handicap):
             js = slice(first, first + count)
-            nc.vector.tensor_reduce(out=group["total"][:, js], in_=group["part_sum"][:, js, :], axis=AXIS.X, op=ALU.add)
-            nc.vector.reciprocal(out=group["inv"][:, js], in_=group["total"][:, js])
+            total, inv, low, top, bar = group["total"], group["inv"], group["low"], group["top"], group["bar"]
+            nc.vector.tensor_reduce(out=total[:, js], in_=group["part_sum"][:, js, :], axis=AXIS.X, op=ALU.add)
+            nc.vector.reciprocal(out=inv[:, js], in_=total[:, js])
             for j in range(first, first + count):
                 conf = group["conf"][j]
-                nc.gpsimd.tensor_scalar(
-                    out=conf[:], in0=conf[:], scalar1=group["inv"][:, j:j + 1], scalar2=0.0,
-                    op0=ALU.mult, op1=ALU.add,
-                )
-
-        def set_bars(group, first, count, handicap):
-            js = slice(first, first + count)
-            low, top, bar = group["low"], group["top"], group["bar"]
+                if handicap is None:
+                    nc.vector.tensor_scalar(out=conf[:], in0=conf[:], scalar1=inv[:, j:j + 1], scalar2=None, op0=ALU.mult)
+                else:
+                    nc.scalar.activation(out=conf[:], in_=conf[:], func=FUNC.Copy, scale=inv[:, j:j + 1])
             nc.vector.tensor_reduce(out=top[:, js], in_=group["part_top"][:, js, :], axis=AXIS.X, op=ALU.max)
-            nc.vector.tensor_scalar(out=low[:, js], in0=group["inv"][:, js], scalar1=THRESHOLD, scalar2=NEVER, op0=ALU.is_le, op1=ALU.mult)
+            nc.vector.tensor_scalar(out=low[:, js], in0=inv[:, js], scalar1=THRESHOLD, scalar2=NEVER, op0=ALU.is_le, op1=ALU.mult)
             if handicap is not None:
                 nc.vector.tensor_scalar(out=low[:, js], in0=low[:, js], scalar1=handicap[:, 0:1], scalar2=None, op0=ALU.max)
             nc.vector.tensor_tensor(out=bar[:, js], in0=low[:, js], in1=top[:, js], op=ALU.add)
+
+        def spread(n, bar1):
+            bar1_rep = keep.tile([P, TILES, P], F32, name="rep_%d" % n)
+            nc.vector.tensor_tensor(
+                out=bar1_rep[:], in0=bar1[:].unsqueeze(2).to_broadcast([P, TILES, P]),
+                in1=handicap_free[:].unsqueeze(1).to_broadcast([P, TILES, P]), op=ALU.add,
+            )
+            bar1_ps = psum.tile([P, 2, BANK], F32, tag="two")
+            for j in range(TILES):
+                nc.tensor.transpose(
+                    bar1_ps[:, j // 4, (j % 4) * P:(j % 4 + 1) * P], bar1_rep[:, j, :], ident[:]
+                )
+            bar1_all = keep.tile([P, CELLS], F32, name="bar1all_%d" % n)
+            nc.scalar.copy(out=bar1_all[:, 0:BANK], in_=bar1_ps[:, 0, :])
+            nc.scalar.copy(out=bar1_all[:, BANK:CELLS], in_=bar1_ps[:, 1, 0:CELLS - BANK])
+            return bar1_all
 
         def store(plane, n, i, rows_sb):
             if i < TILES - 1:
@@ -271,114 +244,92 @@ def tile_coarsematching_kernel(
             [keep.tile([P, CELLS], F32, name="conf1_%d_%d" % (n, i)) for i in range(TILES)]
             for n in range(BATCH)
         ]
-        bar1_rep = [keep.tile([P, TILES, P], F32, name="rep_%d" % n) for n in range(BATCH)]
-        bar1_all = [keep.tile([P, CELLS], F32, name="bar1all_%d" % n) for n in range(BATCH)]
 
-        def home_fill(n, u):
-            back = psum.tile([P, 2, BANK], F32, tag="two")
+        def bring_home(n, i, conf1_t):
+            conf1_ps = psum.tile([P, 2, BANK], F32, tag="two")
             for j in range(TILES):
-                source = bar1_rep[n][:, j, :] if u == 0 else columns[n]["conf"][j][:, (u - 1) * P:u * P]
-                nc.tensor.transpose(back[:, j // 4, (j % 4) * P:(j % 4 + 1) * P], source, ident[:])
-            live[("home", n, u)] = back
+                nc.tensor.transpose(
+                    conf1_ps[:, j // 4, (j % 4) * P:(j % 4 + 1) * P], conf1_t[j][:, i * P:(i + 1) * P], ident[:]
+                )
+            conf1 = conf1_sb[n][i]
+            nc.scalar.copy(out=conf1[:, 0:BANK], in_=conf1_ps[:, 0, :])
+            nc.scalar.copy(out=conf1[:, BANK:CELLS], in_=conf1_ps[:, 1, 0:CELLS - BANK])
+            store(1, n, i, conf1)
+            if i == TILES - 1:
+                store(2, n, i, zeros)
 
-        def home_drain(n, u):
-            back = live.pop(("home", n, u))
-            target = bar1_all[n] if u == 0 else conf1_sb[n][u - 1]
-            nc.scalar.copy(out=target[:, 0:BANK], in_=back[:, 0, :])
-            nc.scalar.copy(out=target[:, BANK:CELLS], in_=back[:, 1, 0:CELLS - BANK])
-            if u > 0:
-                store(1, n, u - 1, target)
-            if u == TILES:
-                store(2, n, TILES - 1, zeros)
-
-        def match_fill(n, i):
-            live[("match", n, i)] = dot_tile(n, GRID0, GRID1, i)
-
-        def match_keep(n, i):
-            dots = live.pop(("match", n, i))
+        def match_tile(n, i, conf0, bar0, bar1_all):
+            dots = dot_tile(n, GRID0, GRID1, i)
             kept = stage.tile([P, INNER_ROWS, INNER_COLS], F32, tag="kept")
-            bar1_inner = inner_cells(bar1_all[n][:, EDGE:CELLS - EDGE])
+            bar1_inner = inner_cells(bar1_all[:, EDGE:CELLS - EDGE])
             for bank in range(2):
                 g = slice(0, BANK0_ROWS) if bank == 0 else slice(BANK0_ROWS, INNER_ROWS)
-                c = slice(EDGE, BANK) if bank == 0 else slice(2 * BANK - CELLS, BANK - EDGE)
+                c = slice(EDGE, BANK) if bank == 0 else slice(0, CELLS - EDGE - BANK)
                 nc.vector.scalar_tensor_tensor(
-                    out=kept[:, g, :], in0=bar1_inner[:, g, :], scalar=rows[n]["bar"][:, i:i + 1],
+                    out=kept[:, g, :], in0=bar1_inner[:, g, :], scalar=bar0[:, i:i + 1],
                     in1=inner_cells(dots[:, bank, c]), op0=ALU.min, op1=ALU.is_le,
                 )
             best = stage.tile([P, INNER_ROWS, INNER_COLS], F32, tag="best")
             nc.vector.tensor_tensor(
-                out=best[:], in0=inner_cells(rows[n]["conf"][i][:, EDGE:CELLS - EDGE]),
+                out=best[:], in0=inner_cells(conf0[i][:, EDGE:CELLS - EDGE]),
                 in1=inner_cells(conf1_sb[n][i][:, EDGE:CELLS - EDGE]), op=ALU.max,
             )
             mconf_sb = mconf_tiles[(n * (TILES - 1) + i) % len(mconf_tiles)]
-            nc.gpsimd.tensor_tensor(
+            nc.vector.tensor_tensor(
                 out=inner_cells(mconf_sb[:, EDGE:CELLS - EDGE]), in0=kept[:], in1=best[:], op=ALU.mult
             )
             store(2, n, i, mconf_sb)
 
         columns = [open_softmax(n, GRID1, GRID0, "c%d" % n) for n in range(BATCH)]
         rows = [open_softmax(n, GRID0, GRID1, "r%d" % n) for n in range(BATCH)]
-        groups = [rows[0], columns[0], columns[1], rows[1]]
-        ROUNDS_SM = len(groups) * TILES
-        PAIR = 2
-        CL = 1
-        LEAD = 10
-        HOME = [14, 21]
-        MATCH = [16, 24]
-        LAST = max(MATCH[1] + TILES, HOME[1] + TILES + 2)
 
-        def stage1_of(r):
-            return ((0, r + LEAD), (1, r))
+        def stage1_consts():
+            bias_ps = psum.tile([P, P], BF16, tag="two")
+            nc.tensor.transpose(bias_ps[:], bias_rows[:], ident_bf[:])
+            nc.vector.tensor_scalar(
+                out=bias4[:], in0=bias_ps[:, 0:PACK], scalar1=INV_SQRT_C, scalar2=None, op0=ALU.mult
+            )
+            handicap_ps = psum.tile([P, P], F32, tag="two")
+            nc.tensor.transpose(handicap_ps[:], handicap_free[:], ident[:])
+            nc.vector.tensor_copy(out=handicap_row[:], in_=handicap_ps[:, 0:1])
 
-        for r in range(-LEAD, LAST + 1):
-            if 0 <= r < ROUNDS_SM:
-                softmax_max(groups[r // TILES], r % TILES)
-            for n, step in stage1_of(r):
-                if 0 <= step - 1 < UNITS:
-                    stage1_drain(n, step - 1)
-            for n in range(BATCH):
-                if 0 <= r - 1 - HOME[n] <= TILES:
-                    home_drain(n, r - 1 - HOME[n])
-            if 0 <= r < ROUNDS_SM:
-                softmax_exp(groups[r // TILES], r % TILES)
-            for n in range(BATCH):
-                if 0 <= r - 1 - MATCH[n] < TILES - 1:
-                    match_keep(n, r - 1 - MATCH[n])
-            for n, step in stage1_of(r):
-                if 0 <= step - 2 < UNITS:
-                    stage1_post(n, step - 2)
-            t_last = r - CL
-            if 0 <= t_last < ROUNDS_SM and t_last % PAIR == PAIR - 1:
-                group = groups[t_last // TILES]
-                first = t_last % TILES - PAIR + 1
-                divide(group, first, PAIR)
-                n = group["n"]
-                if group is rows[n]:
-                    set_bars(group, first, PAIR, handicap_row)
-                    for i in range(first, first + PAIR):
-                        store(0, n, i, group["conf"][i])
-                elif first + PAIR == TILES:
-                    set_bars(group, 0, TILES, None)
-                    nc.vector.tensor_tensor(
-                        out=bar1_rep[n][:], in0=group["bar"][:].unsqueeze(2).to_broadcast([P, TILES, P]),
-                        in1=handicap_free[:].unsqueeze(1).to_broadcast([P, TILES, P]), op=ALU.add,
-                    )
-            if 0 <= r + 1 < ROUNDS_SM:
-                softmax_fill(groups[(r + 1) // TILES], (r + 1) % TILES)
-            for n, step in stage1_of(r):
-                if 0 <= step < UNITS:
-                    stage1_fill(n, step)
-            if r == 1 - LEAD:
-                bias_ps = psum.tile([P, P], BF16, tag="two")
-                nc.tensor.transpose(bias_ps[:], bias_rows[:], ident_bf[:])
-                nc.vector.tensor_scalar(
-                    out=bias4[:], in0=bias_ps[:, 0:PACK], scalar1=INV_SQRT_C, scalar2=None, op0=ALU.mult
-                )
-                handicap_ps = psum.tile([P, P], F32, tag="two")
-                nc.tensor.transpose(handicap_ps[:], handicap_free[:], ident[:])
-                nc.vector.tensor_copy(out=handicap_row[:], in_=handicap_ps[:, 0:1])
-            for n in range(BATCH):
-                if 0 <= r - HOME[n] <= TILES:
-                    home_fill(n, r - HOME[n])
-                if 0 <= r - MATCH[n] < TILES - 1:
-                    match_fill(n, r - MATCH[n])
+        bias4 = const.tile([P, PACK], F32)
+        handicap_row = const.tile([P, 1], F32)
+
+        def stage1(n):
+            for q in range(QUADS):
+                transpose_quad(n, q)
+            if n == 0:
+                stage1_consts()
+            for q in range(QUADS):
+                project_quad(n, q)
+
+        def column_side(n):
+            for j in range(TILES):
+                softmax_tile(columns[n], j)
+            close_softmax(columns[n], 0, TILES, None)
+            return spread(n, columns[n]["bar"])
+
+        def home(n):
+            for i in range(TILES):
+                bring_home(n, i, columns[n]["conf"])
+
+        def row_side(n, bar1_all, with_match):
+            every = 2
+            for j in range(TILES):
+                softmax_tile(rows[n], j)
+                if j % every == every - 1:
+                    close_softmax(rows[n], j - every + 1, every, handicap_row)
+                    for i in range(j - every + 1, j + 1):
+                        store(0, n, i, rows[n]["conf"][i])
+                        if with_match and i < TILES - 1:
+                            match_tile(n, i, rows[n]["conf"], rows[n]["bar"], bar1_all)
+
+        stage1(0)
+        bars0 = column_side(0)
+        stage1(1)
+        home(0)
+        row_side(0, bars0, True)
+        bars1 = column_side(1)
+        home(1)
+        row_side(1, bars1, True)

@@ -30,6 +30,8 @@ BANK = 512
 BANK0_ROWS = (BANK - EDGE) // GRID_W
 GRID1 = 0
 GRID0 = CELLS
+LAG = 2
+MCONF_TILES = 3
 INV_SQRT_C = 1.0 / (C ** 0.5)
 INV_TEMPERATURE = 10.0
 THRESHOLD = 0.2
@@ -90,16 +92,16 @@ def tile_coarsematching_kernel(
         zeros = const.tile([P, CELLS], F32)
         nc.gpsimd.memset(zeros[:], 0.0)
         mconf_tiles = []
-        for slot in range(3):
+        for slot in range(MCONF_TILES):
             mconf_sb = const.tile([P, CELLS], F32, name="mconf_%d" % slot)
             nc.gpsimd.memset(mconf_sb[:], 0.0)
             mconf_tiles.append(mconf_sb)
         warm = const.tile([P, 1], F32)
         nc.vector.memset(warm[:], 0.0)
         nc.scalar.activation(out=warm[:], in_=warm[:], func=FUNC.Exp)
-        handicap_free = const.tile([P, P], F32)
-        nc.vector.memset(handicap_free[:], NEVER)
-        nc.vector.memset(inner_cells(handicap_free[:]), 0.0)
+        floor_free = const.tile([P, P], F32)
+        nc.vector.memset(floor_free[:], NEVER)
+        nc.vector.memset(inner_cells(floor_free[:]), -NEVER)
 
         x_codes = [keep.tile([P, 2 * CELLS], U32, align_bytes=64, name="xc_%d" % n) for n in range(BATCH)]
         x_plane = [keep.tile([P, 2 * CELLS], U8, align_bytes=64, name="xp_%d" % n) for n in range(BATCH)]
@@ -129,26 +131,30 @@ def tile_coarsematching_kernel(
 
         def project_quad(n, q):
             f_grouped = stage.tile([P, QUAD, PACK], BF16, align_bytes=64, tag="fg")
-            cells = slice(q * QUAD, (q + 1) * QUAD)
-            planes = stage.tile([P, PACK, QUAD], BF16, tag="planes")
             for pair in range(2):
-                acc = psum.tile([P, 2, BANK], F32, tag="two")
+                acc = psum.tile([P, 2, PACK, P], F32, tag="two")
                 for bank in range(2):
-                    t = 2 * pair + bank
-                    nc.tensor.matmul_mx(
-                        out=acc[:, bank, :],
-                        lhsT=w_words[:, t * P:(t + 1) * P].bitcast(FP8X4),
-                        lhsT_scale=w_plane[:, t * P:(t + 1) * P],
-                        rhs=x_codes[n][:, cells].bitcast(FP8X4),
-                        rhs_scale=x_plane[n][:, cells],
-                        start=True,
-                        stop=True,
+                    first = (2 * pair + bank) * P
+                    cells = slice(q * QUAD + first, q * QUAD + first + P)
+                    for t in range(PACK):
+                        nc.tensor.matmul_mx(
+                            out=acc[:, bank, t, :],
+                            lhsT=w_words[:, t * P:(t + 1) * P].bitcast(FP8X4),
+                            lhsT_scale=w_plane[:, t * P:(t + 1) * P],
+                            rhs=x_codes[n][:, cells].bitcast(FP8X4),
+                            rhs_scale=x_plane[n][:, cells],
+                            start=True,
+                            stop=True,
+                        )
+                    nc.vector.scalar_tensor_tensor(
+                        out=f_grouped[:, first:first + P, :],
+                        in0=acc[:, bank].rearrange("p t r -> p r t"),
+                        scalar=INV_SQRT_C,
+                        in1=bias4[:].unsqueeze(1).to_broadcast([P, P, PACK]),
+                        op0=ALU.mult,
+                        op1=ALU.add,
                     )
-                    nc.scalar.activation(
-                        out=planes[:, t, :], in_=acc[:, bank, :], func=FUNC.Identity,
-                        bias=bias4[:, t:t + 1], scale=INV_SQRT_C,
-                    )
-            nc.vector.tensor_copy(out=f_grouped[:], in_=planes[:].rearrange("p t r -> p r t"))
+            cells = slice(q * QUAD, (q + 1) * QUAD)
             nc.vector.quantize_mx(
                 out=f_codes[n][:, cells].bitcast(FP8X4),
                 scales=f_plane[n][:, cells],
@@ -172,20 +178,33 @@ def tile_coarsematching_kernel(
             return dots
 
         def open_softmax(n, own, other, label):
-            group = {"n": n, "own": own, "other": other, "label": label}
-            group["part_top"] = keep.tile([P, TILES, 2], F32, name="ptop_" + label)
-            group["part_sum"] = keep.tile([P, TILES, 2], F32, name="psum_" + label)
-            for what in ("shift", "total", "inv", "low", "top", "bar"):
-                group[what] = keep.tile([P, TILES], F32, name=what + "_" + label)
-            group["conf"] = [keep.tile([P, CELLS], F32, name="e_%s_%d" % (label, j)) for j in range(TILES)]
-            return group
+            return {
+                "n": n,
+                "own": own,
+                "other": other,
+                "label": label,
+                "part_top": keep.tile([P, TILES, 2], F32, name="ptop_" + label),
+                "shift": keep.tile([P, TILES], F32, name="shift_" + label),
+                "part_sum": keep.tile([P, TILES, 2], F32, name="psum_" + label),
+                "conf": [keep.tile([P, CELLS], F32, name="e_%s_%d" % (label, j)) for j in range(TILES)],
+            }
+
+        waiting = []
 
         def softmax_tile(group, j):
             dots = dot_tile(group["n"], group["own"], group["other"], j)
             part_top = group["part_top"]
-            shift = group["shift"]
             nc.vector.reduce_max(out=part_top[:, j, 0:1], in_=dots[:, 0, :], axis=AXIS.X)
             nc.vector.reduce_max(out=part_top[:, j, 1:2], in_=dots[:, 1, 0:CELLS - BANK], axis=AXIS.X)
+            softmax_exp()
+            waiting.append((group, j, dots))
+
+        def softmax_exp():
+            if not waiting:
+                return
+            group, j, dots = waiting.pop()
+            part_top = group["part_top"]
+            shift = group["shift"]
             nc.vector.tensor_scalar(
                 out=shift[:, j:j + 1], in0=part_top[:, j, 0:1], scalar1=part_top[:, j, 1:2],
                 scalar2=-INV_TEMPERATURE, op0=ALU.max, op1=ALU.mult,
@@ -200,28 +219,42 @@ def tile_coarsematching_kernel(
                 bias=shift[:, j:j + 1], scale=INV_TEMPERATURE, accum_out=group["part_sum"][:, j, 1:2],
             )
 
-        def close_softmax(group, first, count, handicap):
-            js = slice(first, first + count)
-            total, inv, low, top, bar = group["total"], group["inv"], group["low"], group["top"], group["bar"]
-            nc.vector.tensor_reduce(out=total[:, js], in_=group["part_sum"][:, js, :], axis=AXIS.X, op=ALU.add)
-            nc.vector.reciprocal(out=inv[:, js], in_=total[:, js])
-            for j in range(first, first + count):
+        def close_softmax(group, on_vector):
+            label = group["label"]
+            total = keep.tile([P, TILES], F32, name="total_" + label)
+            nc.vector.tensor_reduce(out=total[:], in_=group["part_sum"][:], axis=AXIS.X, op=ALU.add)
+            inv = keep.tile([P, TILES], F32, name="inv_" + label)
+            nc.vector.reciprocal(out=inv[:], in_=total[:])
+            for j in range(TILES):
                 conf = group["conf"][j]
-                if handicap is None:
-                    nc.vector.tensor_scalar(out=conf[:], in0=conf[:], scalar1=inv[:, j:j + 1], scalar2=None, op0=ALU.mult)
+                if on_vector:
+                    nc.vector.tensor_scalar(
+                        out=conf[:], in0=conf[:], scalar1=inv[:, j:j + 1], scalar2=None, op0=ALU.mult
+                    )
                 else:
                     nc.scalar.activation(out=conf[:], in_=conf[:], func=FUNC.Copy, scale=inv[:, j:j + 1])
-            nc.vector.tensor_reduce(out=top[:, js], in_=group["part_top"][:, js, :], axis=AXIS.X, op=ALU.max)
-            nc.vector.tensor_scalar(out=low[:, js], in0=inv[:, js], scalar1=THRESHOLD, scalar2=NEVER, op0=ALU.is_le, op1=ALU.mult)
-            if handicap is not None:
-                nc.vector.tensor_scalar(out=low[:, js], in0=low[:, js], scalar1=handicap[:, 0:1], scalar2=None, op0=ALU.max)
-            nc.vector.tensor_tensor(out=bar[:, js], in0=low[:, js], in1=top[:, js], op=ALU.add)
+            top = keep.tile([P, TILES], F32, name="top_" + label)
+            nc.vector.tensor_reduce(out=top[:], in_=group["part_top"][:], axis=AXIS.X, op=ALU.max)
+            bar = keep.tile([P, TILES], F32, name="bar_" + label)
+            nc.vector.tensor_scalar(out=bar[:], in0=inv[:], scalar1=THRESHOLD, scalar2=None, op0=ALU.is_gt)
+            nc.vector.tensor_scalar(
+                out=bar[:], in0=bar[:], scalar1=-2.0 * NEVER, scalar2=NEVER, op0=ALU.mult, op1=ALU.add
+            )
+            nc.vector.tensor_tensor(out=bar[:], in0=bar[:], in1=top[:], op=ALU.max)
+            return bar
+
+        def close_rows(n):
+            bar = close_softmax(rows[n], False)
+            nc.vector.tensor_scalar(out=bar[:], in0=bar[:], scalar1=floor_row[:, 0:1], scalar2=None, op0=ALU.max)
+            for i in range(TILES):
+                store(0, n, i, rows[n]["conf"][i])
+            return bar
 
         def spread(n, bar1):
             bar1_rep = keep.tile([P, TILES, P], F32, name="rep_%d" % n)
             nc.vector.tensor_tensor(
                 out=bar1_rep[:], in0=bar1[:].unsqueeze(2).to_broadcast([P, TILES, P]),
-                in1=handicap_free[:].unsqueeze(1).to_broadcast([P, TILES, P]), op=ALU.add,
+                in1=floor_free[:].unsqueeze(1).to_broadcast([P, TILES, P]), op=ALU.max,
             )
             bar1_ps = psum.tile([P, 2, BANK], F32, tag="two")
             for j in range(TILES):
@@ -274,7 +307,7 @@ def tile_coarsematching_kernel(
                 out=best[:], in0=inner_cells(conf0[i][:, EDGE:CELLS - EDGE]),
                 in1=inner_cells(conf1_sb[n][i][:, EDGE:CELLS - EDGE]), op=ALU.max,
             )
-            mconf_sb = mconf_tiles[(n * (TILES - 1) + i) % len(mconf_tiles)]
+            mconf_sb = mconf_tiles[i % MCONF_TILES]
             nc.vector.tensor_tensor(
                 out=inner_cells(mconf_sb[:, EDGE:CELLS - EDGE]), in0=kept[:], in1=best[:], op=ALU.mult
             )
@@ -282,54 +315,53 @@ def tile_coarsematching_kernel(
 
         columns = [open_softmax(n, GRID1, GRID0, "c%d" % n) for n in range(BATCH)]
         rows = [open_softmax(n, GRID0, GRID1, "r%d" % n) for n in range(BATCH)]
+        bar0 = [None, None]
+        bar1_all = [None, None]
 
-        def stage1_consts():
-            bias_ps = psum.tile([P, P], BF16, tag="two")
-            nc.tensor.transpose(bias_ps[:], bias_rows[:], ident_bf[:])
-            nc.vector.tensor_scalar(
-                out=bias4[:], in0=bias_ps[:, 0:PACK], scalar1=INV_SQRT_C, scalar2=None, op0=ALU.mult
-            )
-            handicap_ps = psum.tile([P, P], F32, tag="two")
-            nc.tensor.transpose(handicap_ps[:], handicap_free[:], ident[:])
-            nc.vector.tensor_copy(out=handicap_row[:], in_=handicap_ps[:, 0:1])
-
+        transpose_quad(0, 0)
+        transpose_quad(0, 1)
+        bias_ps = psum.tile([P, P], BF16, tag="two")
+        nc.tensor.transpose(bias_ps[:], bias_rows[:], ident_bf[:])
         bias4 = const.tile([P, PACK], F32)
-        handicap_row = const.tile([P, 1], F32)
+        nc.vector.tensor_scalar(
+            out=bias4[:], in0=bias_ps[:, 0:PACK], scalar1=INV_SQRT_C, scalar2=None, op0=ALU.mult
+        )
+        project_quad(0, 0)
+        transpose_quad(0, 2)
+        project_quad(0, 1)
+        project_quad(0, 2)
+        floor_ps = psum.tile([P, P], F32, tag="two")
+        nc.tensor.transpose(floor_ps[:], floor_free[:], ident[:])
+        floor_row = const.tile([P, 1], F32)
+        nc.vector.tensor_copy(out=floor_row[:], in_=floor_ps[:, 0:1])
 
-        def stage1(n):
-            for q in range(QUADS):
-                transpose_quad(n, q)
-            if n == 0:
-                stage1_consts()
-            for q in range(QUADS):
-                project_quad(n, q)
+        for j in range(TILES):
+            softmax_tile(rows[0], j)
+            if j % 2 == 1:
+                transpose_quad(1, j // 2)
+        for j in range(TILES):
+            softmax_tile(columns[0], j)
+            if j == LAG:
+                bar0[0] = close_rows(0)
+            if j % 2 == 1:
+                project_quad(1, j // 2)
 
-        def column_side(n):
-            for j in range(TILES):
-                softmax_tile(columns[n], j)
-            close_softmax(columns[n], 0, TILES, None)
-            return spread(n, columns[n]["bar"])
+        for k in range(2 * TILES):
+            softmax_tile(columns[1] if k < TILES else rows[1], k % TILES)
+            if k == LAG:
+                bar1_all[0] = spread(0, close_softmax(columns[0], True))
+            if k == TILES + LAG:
+                bar1_all[1] = spread(1, close_softmax(columns[1], True))
+            home = k - LAG - 1
+            if home >= 0:
+                bring_home(home // TILES, home % TILES, columns[home // TILES]["conf"])
+            if home >= 1 and home % 2 == 1:
+                match_tile(0, home // 2, rows[0]["conf"], bar0[0], bar1_all[0])
 
-        def home(n):
-            for i in range(TILES):
-                bring_home(n, i, columns[n]["conf"])
-
-        def row_side(n, bar1_all, with_match):
-            every = 2
-            for j in range(TILES):
-                softmax_tile(rows[n], j)
-                if j % every == every - 1:
-                    close_softmax(rows[n], j - every + 1, every, handicap_row)
-                    for i in range(j - every + 1, j + 1):
-                        store(0, n, i, rows[n]["conf"][i])
-                        if with_match and i < TILES - 1:
-                            match_tile(n, i, rows[n]["conf"], rows[n]["bar"], bar1_all)
-
-        stage1(0)
-        bars0 = column_side(0)
-        stage1(1)
-        home(0)
-        row_side(0, bars0, True)
-        bars1 = column_side(1)
-        home(1)
-        row_side(1, bars1, True)
+        softmax_exp()
+        for home in range(2 * TILES - LAG - 1, 2 * TILES):
+            bring_home(1, home % TILES, columns[1]["conf"])
+        match_tile(0, TILES - 2, rows[0]["conf"], bar0[0], bar1_all[0])
+        bar0[1] = close_rows(1)
+        for i in range(TILES - 1):
+            match_tile(1, i, rows[1]["conf"], bar0[1], bar1_all[1])

@@ -27,10 +27,10 @@ EDGE = BORDER * GRID_W
 INNER_ROWS = CELLS // GRID_W - 2 * BORDER
 INNER_COLS = GRID_W - 2 * BORDER
 BANK = 512
-BANK0_ROWS = (BANK - EDGE) // GRID_W
+SPANS = ((0, BANK), (BANK, CELLS))
+INNER_SPANS = ((EDGE, EDGE + BANK), (EDGE + BANK, CELLS - EDGE))
 GRID1 = 0
 GRID0 = CELLS
-LAG = 2
 MCONF_TILES = 3
 INV_SQRT_C = 1.0 / (C ** 0.5)
 INV_TEMPERATURE = 10.0
@@ -38,6 +38,14 @@ THRESHOLD = 0.2
 NEVER = 1.0e38
 
 FLOPS = 2 * (2 * BATCH * CELLS) * C * C + 2 * BATCH * CELLS * CELLS * C
+
+S_COL = "G"
+S_ROW = "G"
+FIN = "G"
+EV0 = (3,)
+EV1 = (1,3,)
+H0 = 9
+STEP0 = 1
 
 
 def inner_cells(cells):
@@ -52,38 +60,51 @@ def tile_coarsematching_kernel(
         const = ctx.enter_context(tc.tile_pool(name="const", bufs=1))
         keep = ctx.enter_context(tc.tile_pool(name="keep", bufs=1))
         stage = ctx.enter_context(tc.tile_pool(name="stage", bufs=2))
-        psum = ctx.enter_context(tc.psum_pool(name="psum", bufs=4))
+        mask = ctx.enter_context(tc.tile_pool(name="mask", bufs=3))
+        psum = ctx.enter_context(tc.psum_pool(name="psum", bufs=8))
 
         w_plane = const.tile([P, C], U8, align_bytes=64)
         nc.vector.memset(w_plane[:].bitcast(I32), 0)
+        bias_rows = const.tile([P, P], BF16)
+        nc.vector.memset(bias_rows[:], 0.0)
+        w_words = const.tile([P, C], U32, align_bytes=64)
+        x_sb = [keep.tile([P, 2 * TILES, C], BF16, name="x_%d" % n) for n in range(BATCH)]
+
+        def load_cells(n, first, last):
+            mid = min(max(first, TILES), last)
+            if first < mid:
+                nc.sync.dma_start(
+                    out=x_sb[n][:, first:mid, :],
+                    in_=feat_c1[n, first * P:mid * P, :].rearrange("(j p) k -> p j k", p=P),
+                )
+            if mid < last:
+                lo = EDGE + (mid - TILES) * P
+                nc.sync.dma_start(
+                    out=x_sb[n][:, mid:last, :],
+                    in_=feat_c0[n, lo:lo + (last - mid) * P, :].rearrange("(j p) k -> p j k", p=P),
+                )
+
+        def load_border(n):
+            nc.sync.dma_start(out=x_sb[n][0:EDGE, 2 * TILES - 1, :], in_=feat_c0[n, CELLS - EDGE:CELLS, :])
+            nc.sync.dma_start(out=x_sb[n][EDGE:P, 2 * TILES - 1, :], in_=feat_c0[n, 0:EDGE, :])
+
+        load_cells(0, 0, 2)
+        load_cells(0, 2, 4)
+        nc.sync.dma_start(
+            out=w_words[:].bitcast(I32), in_=W_words[0].rearrange("p n t -> p (n t)").bitcast(I32)
+        )
         for quadrant in range(4):
             nc.sync.dma_start(
                 out=w_plane[32 * quadrant:32 * quadrant + 4, :].bitcast(I32),
                 in_=W_scales[0, 4 * quadrant:4 * quadrant + 4, :].bitcast(I32),
             )
-        bias_rows = const.tile([P, P], BF16)
-        nc.vector.memset(bias_rows[:], 0.0)
         nc.sync.dma_start(out=bias_rows[0:PACK, :], in_=b.rearrange("(t p) -> t p", p=P))
-
-        x_sb = []
-        for n in range(BATCH):
-            x_rows = keep.tile([P, 2 * TILES, C], BF16, name="x_%d" % n)
-            nc.sync.dma_start(
-                out=x_rows[:, 0:TILES, :], in_=feat_c1[n].rearrange("(j p) k -> p j k", p=P)
-            )
-            nc.sync.dma_start(
-                out=x_rows[:, TILES:2 * TILES - 1, :],
-                in_=feat_c0[n, EDGE:CELLS - EDGE, :].rearrange("(j p) k -> p j k", p=P),
-            )
-            nc.sync.dma_start(out=x_rows[0:EDGE, 2 * TILES - 1, :], in_=feat_c0[n, CELLS - EDGE:CELLS, :])
-            nc.sync.dma_start(out=x_rows[EDGE:P, 2 * TILES - 1, :], in_=feat_c0[n, 0:EDGE, :])
-            x_sb.append(x_rows)
-            if n == 0:
-                w_words = const.tile([P, C], U32, align_bytes=64)
-                nc.sync.dma_start(
-                    out=w_words[:].bitcast(I32),
-                    in_=W_words[0].rearrange("p n t -> p (n t)").bitcast(I32),
-                )
+        load_cells(0, 4, 8)
+        load_cells(0, 8, 11)
+        load_border(0)
+        for q in range(QUADS):
+            load_cells(1, 4 * q, min(4 * q + 4, 2 * TILES - 1))
+        load_border(1)
 
         ident = const.tile([P, P], F32)
         make_identity(nc, ident[:])
@@ -101,73 +122,94 @@ def tile_coarsematching_kernel(
         nc.scalar.activation(out=warm[:], in_=warm[:], func=FUNC.Exp)
         floor_free = const.tile([P, P], F32)
         nc.vector.memset(floor_free[:], NEVER)
-        nc.vector.memset(inner_cells(floor_free[:]), -NEVER)
+        nc.vector.memset(inner_cells(floor_free[:]), 0.0)
 
         x_codes = [keep.tile([P, 2 * CELLS], U32, align_bytes=64, name="xc_%d" % n) for n in range(BATCH)]
         x_plane = [keep.tile([P, 2 * CELLS], U8, align_bytes=64, name="xp_%d" % n) for n in range(BATCH)]
         f_codes = [keep.tile([P, 2 * CELLS], U32, align_bytes=64, name="fc_%d" % n) for n in range(BATCH)]
         f_plane = [keep.tile([P, 2 * CELLS], U8, align_bytes=64, name="fp_%d" % n) for n in range(BATCH)]
 
-        def transpose_quad(n, q):
-            x_t = psum.tile([P, 2, 2, 2 * P], F32, tag="two")
-            for bank in range(2):
-                for half in range(2):
-                    words = x_sb[n][:, 4 * q + 2 * bank + half, :].bitcast(F32)
+        def bank():
+            one_bank = psum.tile([P, BANK], F32, tag="bank", name="one_bank")
+            return one_bank
+
+        x_grouped = {}
+        f_grouped = {}
+
+        def turn(n, q):
+            grouped = stage.tile([P, QUAD * PACK], BF16, align_bytes=64, tag="xg", name="xg")
+            x_grouped[n, q] = grouped
+            for half in range(2):
+                x_t = bank()
+                for c in range(2):
+                    words = x_sb[n][:, 4 * q + 2 * half + c, :].bitcast(F32)
                     for u in range(2):
                         nc.tensor.transpose(
-                            x_t[:, bank, u, half * P:(half + 1) * P], words[:, u:C // 2:2], ident[:]
+                            x_t[:, u * 2 * P + c * P:u * 2 * P + (c + 1) * P], words[:, u:C // 2:2], ident[:]
                         )
-            x_grouped = stage.tile([P, QUAD * PACK], BF16, align_bytes=64, tag="xg")
-            for bank in range(2):
                 nc.scalar.copy(
-                    out=x_grouped[:, bank * QUAD * 2:(bank + 1) * QUAD * 2]
+                    out=grouped[:, half * QUAD * 2:(half + 1) * QUAD * 2]
                     .bitcast(F32).rearrange("p (r u) -> p r u", u=2),
-                    in_=x_t[:, bank].rearrange("p u r -> p r u"),
+                    in_=x_t[:].rearrange("p (u r) -> p r u", u=2),
                 )
+
+        def quantize_x(n, q):
             cells = slice(q * QUAD, (q + 1) * QUAD)
             nc.vector.quantize_mx(
-                out=x_codes[n][:, cells].bitcast(FP8X4), scales=x_plane[n][:, cells], in_=x_grouped[:]
+                out=x_codes[n][:, cells].bitcast(FP8X4), scales=x_plane[n][:, cells], in_=x_grouped[n, q][:]
             )
 
-        def project_quad(n, q):
-            f_grouped = stage.tile([P, QUAD, PACK], BF16, align_bytes=64, tag="fg")
-            for pair in range(2):
-                acc = psum.tile([P, 2, PACK, P], F32, tag="two")
-                for bank in range(2):
-                    first = (2 * pair + bank) * P
-                    cells = slice(q * QUAD + first, q * QUAD + first + P)
-                    for t in range(PACK):
-                        nc.tensor.matmul_mx(
-                            out=acc[:, bank, t, :],
-                            lhsT=w_words[:, t * P:(t + 1) * P].bitcast(FP8X4),
-                            lhsT_scale=w_plane[:, t * P:(t + 1) * P],
-                            rhs=x_codes[n][:, cells].bitcast(FP8X4),
-                            rhs_scale=x_plane[n][:, cells],
-                            start=True,
-                            stop=True,
-                        )
-                    nc.vector.scalar_tensor_tensor(
-                        out=f_grouped[:, first:first + P, :],
-                        in0=acc[:, bank].rearrange("p t r -> p r t"),
-                        scalar=INV_SQRT_C,
-                        in1=bias4[:].unsqueeze(1).to_broadcast([P, P, PACK]),
-                        op0=ALU.mult,
-                        op1=ALU.add,
-                    )
-            cells = slice(q * QUAD, (q + 1) * QUAD)
-            nc.vector.quantize_mx(
-                out=f_codes[n][:, cells].bitcast(FP8X4),
-                scales=f_plane[n][:, cells],
-                in_=f_grouped[:].rearrange("p r t -> p (r t)"),
-            )
-
-        def dot_tile(n, own, other, j):
-            dots = psum.tile([P, 2, BANK], F32, tag="two")
-            for bank in range(2):
-                lo = bank * BANK
-                hi = min(CELLS, lo + BANK)
+        def project(n, q, c, on_vector):
+            if c == 0:
+                f_grouped[n, q] = stage.tile([P, QUAD, PACK], BF16, align_bytes=64, tag="fg", name="fg")
+            first = c * P
+            cells = slice(q * QUAD + first, q * QUAD + first + P)
+            acc = bank()
+            for t in range(PACK):
                 nc.tensor.matmul_mx(
-                    out=dots[:, bank, 0:hi - lo],
+                    out=acc[:, t * P:(t + 1) * P],
+                    lhsT=w_words[:, t * P:(t + 1) * P].bitcast(FP8X4),
+                    lhsT_scale=w_plane[:, t * P:(t + 1) * P],
+                    rhs=x_codes[n][:, cells].bitcast(FP8X4),
+                    rhs_scale=x_plane[n][:, cells],
+                    start=True,
+                    stop=True,
+                )
+            target = f_grouped[n, q][:, first:first + P, :]
+            if on_vector:
+                nc.vector.scalar_tensor_tensor(
+                    out=target,
+                    in0=acc[:].rearrange("p (t r) -> p r t", t=PACK),
+                    scalar=INV_SQRT_C,
+                    in1=bias4[:].unsqueeze(1).to_broadcast([P, P, PACK]),
+                    op0=ALU.mult,
+                    op1=ALU.add,
+                )
+            else:
+                rows4 = stage.tile([P, PACK, P], BF16, tag="rows4", name="rows4")
+                for t in range(PACK):
+                    nc.scalar.activation(
+                        out=rows4[:, t, :], in_=acc[:, t * P:(t + 1) * P], func=FUNC.Identity,
+                        scale=INV_SQRT_C, bias=bias4[:, t:t + 1],
+                    )
+                nc.gpsimd.tensor_scalar(
+                    out=target, in0=rows4[:].rearrange("p t r -> p r t"),
+                    scalar1=1.0, scalar2=0.0, op0=ALU.mult, op1=ALU.add,
+                )
+
+        def quantize_f(n, q):
+            cells = slice(q * QUAD, (q + 1) * QUAD)
+            nc.vector.quantize_mx(
+                out=f_codes[n][:, cells].bitcast(FP8X4), scales=f_plane[n][:, cells],
+                in_=f_grouped[n, q][:].rearrange("p r t -> p (r t)"),
+            )
+
+        def dot_banks(n, own, other, j, spans):
+            banks = []
+            for lo, hi in spans:
+                dots = bank()
+                nc.tensor.matmul_mx(
+                    out=dots[:, 0:hi - lo],
                     lhsT=f_codes[n][:, own + j * P:own + (j + 1) * P].bitcast(FP8X4),
                     lhsT_scale=f_plane[n][:, own + j * P:own + (j + 1) * P],
                     rhs=f_codes[n][:, other + lo:other + hi].bitcast(FP8X4),
@@ -175,96 +217,99 @@ def tile_coarsematching_kernel(
                     start=True,
                     stop=True,
                 )
-            return dots
+                banks.append(dots[:, 0:hi - lo])
+            return banks
 
         def open_softmax(n, own, other, label):
-            return {
+            group = {
                 "n": n,
                 "own": own,
                 "other": other,
-                "label": label,
-                "part_top": keep.tile([P, TILES, 2], F32, name="ptop_" + label),
+                "tops": keep.tile([P, TILES, 4], F32, name="tops_" + label),
                 "shift": keep.tile([P, TILES], F32, name="shift_" + label),
-                "part_sum": keep.tile([P, TILES, 2], F32, name="psum_" + label),
+                "sums": keep.tile([P, TILES, 2], F32, name="sums_" + label),
+                "total": keep.tile([P, TILES], F32, name="total_" + label),
+                "inv": keep.tile([P, TILES], F32, name="inv_" + label),
+                "bar": keep.tile([P, TILES], F32, name="bar_" + label),
                 "conf": [keep.tile([P, CELLS], F32, name="e_%s_%d" % (label, j)) for j in range(TILES)],
             }
+            return group
 
-        waiting = []
+        def dots_of(tile):
+            group, j = tile
+            group[j] = dot_banks(group["n"], group["own"], group["other"], j, SPANS)
 
-        def softmax_tile(group, j):
-            dots = dot_tile(group["n"], group["own"], group["other"], j)
-            part_top = group["part_top"]
-            nc.vector.reduce_max(out=part_top[:, j, 0:1], in_=dots[:, 0, :], axis=AXIS.X)
-            nc.vector.reduce_max(out=part_top[:, j, 1:2], in_=dots[:, 1, 0:CELLS - BANK], axis=AXIS.X)
-            softmax_exp()
-            waiting.append((group, j, dots))
+        def tops_of(tile):
+            group, j = tile
+            for k in range(2):
+                nc.vector.reduce_max(out=group["tops"][:, j, k:k + 1], in_=group[j][k], axis=AXIS.X)
 
-        def softmax_exp():
-            if not waiting:
-                return
-            group, j, dots = waiting.pop()
-            part_top = group["part_top"]
-            shift = group["shift"]
+        def shift_of(tile):
+            group, j = tile
             nc.vector.tensor_scalar(
-                out=shift[:, j:j + 1], in0=part_top[:, j, 0:1], scalar1=part_top[:, j, 1:2],
-                scalar2=-INV_TEMPERATURE, op0=ALU.max, op1=ALU.mult,
-            )
-            e = group["conf"][j]
-            nc.scalar.activation(
-                out=e[:, 0:BANK], in_=dots[:, 0, :], func=FUNC.Exp,
-                bias=shift[:, j:j + 1], scale=INV_TEMPERATURE, accum_out=group["part_sum"][:, j, 0:1],
-            )
-            nc.scalar.activation(
-                out=e[:, BANK:CELLS], in_=dots[:, 1, 0:CELLS - BANK], func=FUNC.Exp,
-                bias=shift[:, j:j + 1], scale=INV_TEMPERATURE, accum_out=group["part_sum"][:, j, 1:2],
+                out=group["shift"][:, j:j + 1], in0=group["tops"][:, j, 0:1],
+                scalar1=group["tops"][:, j, 1:2], scalar2=-INV_TEMPERATURE, op0=ALU.max, op1=ALU.mult,
             )
 
-        def close_softmax(group, on_vector):
-            label = group["label"]
-            total = keep.tile([P, TILES], F32, name="total_" + label)
-            nc.vector.tensor_reduce(out=total[:], in_=group["part_sum"][:], axis=AXIS.X, op=ALU.add)
-            inv = keep.tile([P, TILES], F32, name="inv_" + label)
-            nc.vector.reciprocal(out=inv[:], in_=total[:])
-            for j in range(TILES):
-                conf = group["conf"][j]
-                if on_vector:
-                    nc.vector.tensor_scalar(
-                        out=conf[:], in0=conf[:], scalar1=inv[:, j:j + 1], scalar2=None, op0=ALU.mult
-                    )
-                else:
-                    nc.scalar.activation(out=conf[:], in_=conf[:], func=FUNC.Copy, scale=inv[:, j:j + 1])
-            top = keep.tile([P, TILES], F32, name="top_" + label)
-            nc.vector.tensor_reduce(out=top[:], in_=group["part_top"][:], axis=AXIS.X, op=ALU.max)
-            bar = keep.tile([P, TILES], F32, name="bar_" + label)
-            nc.vector.tensor_scalar(out=bar[:], in0=inv[:], scalar1=THRESHOLD, scalar2=None, op0=ALU.is_gt)
-            nc.vector.tensor_scalar(
-                out=bar[:], in0=bar[:], scalar1=-2.0 * NEVER, scalar2=NEVER, op0=ALU.mult, op1=ALU.add
-            )
-            nc.vector.tensor_tensor(out=bar[:], in0=bar[:], in1=top[:], op=ALU.max)
-            return bar
-
-        def close_rows(n):
-            bar = close_softmax(rows[n], False)
-            nc.vector.tensor_scalar(out=bar[:], in0=bar[:], scalar1=floor_row[:, 0:1], scalar2=None, op0=ALU.max)
-            for i in range(TILES):
-                store(0, n, i, rows[n]["conf"][i])
-            return bar
-
-        def spread(n, bar1):
-            bar1_rep = keep.tile([P, TILES, P], F32, name="rep_%d" % n)
-            nc.vector.tensor_tensor(
-                out=bar1_rep[:], in0=bar1[:].unsqueeze(2).to_broadcast([P, TILES, P]),
-                in1=floor_free[:].unsqueeze(1).to_broadcast([P, TILES, P]), op=ALU.max,
-            )
-            bar1_ps = psum.tile([P, 2, BANK], F32, tag="two")
-            for j in range(TILES):
-                nc.tensor.transpose(
-                    bar1_ps[:, j // 4, (j % 4) * P:(j % 4 + 1) * P], bar1_rep[:, j, :], ident[:]
+        def exp_of(tile):
+            group, j = tile
+            for k in range(2):
+                lo, hi = SPANS[k]
+                nc.scalar.activation(
+                    out=group["conf"][j][:, lo:hi], in_=group[j][k], func=FUNC.Exp,
+                    bias=group["shift"][:, j:j + 1], scale=INV_TEMPERATURE,
+                    accum_out=group["sums"][:, j, k:k + 1],
                 )
-            bar1_all = keep.tile([P, CELLS], F32, name="bar1all_%d" % n)
-            nc.scalar.copy(out=bar1_all[:, 0:BANK], in_=bar1_ps[:, 0, :])
-            nc.scalar.copy(out=bar1_all[:, BANK:CELLS], in_=bar1_ps[:, 1, 0:CELLS - BANK])
-            return bar1_all
+
+        def total_of(tile):
+            group, j = tile
+            nc.vector.tensor_reduce(
+                out=group["total"][:, j:j + 1], in_=group["sums"][:, j, :], axis=AXIS.X, op=ALU.add
+            )
+
+        def inverse_of(tile):
+            group, j = tile
+            nc.vector.reciprocal(out=group["inv"][:, j:j + 1], in_=group["total"][:, j:j + 1])
+
+        def divide(tile, engine):
+            group, j = tile
+            conf = group["conf"][j]
+            inv = group["inv"][:, j:j + 1]
+            if engine == "G":
+                nc.gpsimd.tensor_scalar(
+                    out=conf[:], in0=conf[:], scalar1=inv, scalar2=0.0, op0=ALU.mult, op1=ALU.add
+                )
+            elif engine == "V":
+                nc.vector.tensor_scalar(out=conf[:], in0=conf[:], scalar1=inv, scalar2=None, op0=ALU.mult)
+            else:
+                nc.scalar.activation(out=conf[:], in_=conf[:], func=FUNC.Copy, scale=inv)
+            if group["own"] == GRID0:
+                store(0, group["n"], j, conf)
+
+        def bars_of(group, first, last):
+            nc.vector.tensor_scalar(
+                out=group["tops"][:, first:last, 2], in0=group["inv"][:, first:last],
+                scalar1=THRESHOLD, scalar2=-NEVER, op0=ALU.subtract, op1=ALU.mult,
+            )
+            cols = 4 if group["own"] == GRID0 else 3
+            nc.vector.tensor_reduce(
+                out=group["bar"][:, first:last], in_=group["tops"][:, first:last, 0:cols], axis=AXIS.X, op=ALU.max
+            )
+
+        def spread(group):
+            bar_all = keep.tile([P, CELLS], F32, name="barall_%d" % group["n"])
+            for lo, hi in SPANS:
+                ps = bank()
+                for j in range(lo // P, hi // P):
+                    nc.tensor.transpose(
+                        ps[:, j * P - lo:(j + 1) * P - lo],
+                        group["bar"][:, j:j + 1].to_broadcast([P, P]), ident[:]
+                    )
+                nc.scalar.activation(
+                    out=bar_all[:, lo:hi], in_=ps[:, 0:hi - lo], func=FUNC.Identity, bias=floor_row[:, 0:1],
+                    scale=1.0,
+                )
+            return bar_all
 
         def store(plane, n, i, rows_sb):
             if i < TILES - 1:
@@ -277,91 +322,172 @@ def tile_coarsematching_kernel(
             [keep.tile([P, CELLS], F32, name="conf1_%d_%d" % (n, i)) for i in range(TILES)]
             for n in range(BATCH)
         ]
+        home_banks = {}
+        dots_again = {}
+        kept_sb = {}
+        best_sb = {}
 
-        def bring_home(n, i, conf1_t):
-            conf1_ps = psum.tile([P, 2, BANK], F32, tag="two")
-            for j in range(TILES):
-                nc.tensor.transpose(
-                    conf1_ps[:, j // 4, (j % 4) * P:(j % 4 + 1) * P], conf1_t[j][:, i * P:(i + 1) * P], ident[:]
-                )
-            conf1 = conf1_sb[n][i]
-            nc.scalar.copy(out=conf1[:, 0:BANK], in_=conf1_ps[:, 0, :])
-            nc.scalar.copy(out=conf1[:, BANK:CELLS], in_=conf1_ps[:, 1, 0:CELLS - BANK])
-            store(1, n, i, conf1)
-            if i == TILES - 1:
-                store(2, n, i, zeros)
+        def home_turn(n, i):
+            banks = []
+            for lo, hi in SPANS:
+                ps = bank()
+                for j in range(lo // P, hi // P):
+                    nc.tensor.transpose(
+                        ps[:, j * P - lo:(j + 1) * P - lo], columns[n]["conf"][j][:, i * P:(i + 1) * P], ident[:]
+                    )
+                banks.append(ps[:, 0:hi - lo])
+            home_banks[n, i] = banks
 
-        def match_tile(n, i, conf0, bar0, bar1_all):
-            dots = dot_tile(n, GRID0, GRID1, i)
-            kept = stage.tile([P, INNER_ROWS, INNER_COLS], F32, tag="kept")
-            bar1_inner = inner_cells(bar1_all[:, EDGE:CELLS - EDGE])
-            for bank in range(2):
-                g = slice(0, BANK0_ROWS) if bank == 0 else slice(BANK0_ROWS, INNER_ROWS)
-                c = slice(EDGE, BANK) if bank == 0 else slice(0, CELLS - EDGE - BANK)
+        def home_copy(n, i):
+            for k in range(2):
+                lo, hi = SPANS[k]
+                nc.scalar.copy(out=conf1_sb[n][i][:, lo:hi], in_=home_banks[n, i][k])
+            store(1, n, i, conf1_sb[n][i])
+
+        def match_dots(n, i):
+            dots_again[n, i] = dot_banks(n, GRID0, GRID1, i, INNER_SPANS)
+
+        def match_kept(n, i):
+            kept = mask.tile([P, INNER_ROWS, INNER_COLS], F32, tag="kept", name="kept")
+            kept_sb[n, i] = kept
+            for k in range(2):
+                lo, hi = INNER_SPANS[k]
+                g = slice((lo - EDGE) // GRID_W, (hi - EDGE) // GRID_W)
                 nc.vector.scalar_tensor_tensor(
-                    out=kept[:, g, :], in0=bar1_inner[:, g, :], scalar=bar0[:, i:i + 1],
-                    in1=inner_cells(dots[:, bank, c]), op0=ALU.min, op1=ALU.is_le,
+                    out=kept[:, g, :], in0=inner_cells(bar1_all[n][:, lo:hi]), scalar=rows[n]["bar"][:, i:i + 1],
+                    in1=inner_cells(dots_again[n, i][k]), op0=ALU.min, op1=ALU.is_le,
                 )
-            best = stage.tile([P, INNER_ROWS, INNER_COLS], F32, tag="best")
-            nc.vector.tensor_tensor(
-                out=best[:], in0=inner_cells(conf0[i][:, EDGE:CELLS - EDGE]),
-                in1=inner_cells(conf1_sb[n][i][:, EDGE:CELLS - EDGE]), op=ALU.max,
-            )
+
+        def match_best(n, i):
+            best = mask.tile([P, INNER_ROWS, INNER_COLS], F32, tag="best", name="best")
+            best_sb[n, i] = best
+            conf0 = rows[n]["conf"][i]
+            for k in range(2):
+                lo, hi = SPANS[k]
+                lo, hi = max(lo, EDGE), min(hi, CELLS - EDGE)
+                g = slice((lo - EDGE) // GRID_W, (hi - EDGE) // GRID_W)
+                nc.vector.tensor_tensor(
+                    out=best[:, g, :], in0=inner_cells(conf0[:, lo:hi]),
+                    in1=inner_cells(home_banks[n, i][k][:, lo - SPANS[k][0]:hi - SPANS[k][0]]), op=ALU.max,
+                )
+
+        def match_final(n, i, engine):
             mconf_sb = mconf_tiles[i % MCONF_TILES]
-            nc.vector.tensor_tensor(
-                out=inner_cells(mconf_sb[:, EDGE:CELLS - EDGE]), in0=kept[:], in1=best[:], op=ALU.mult
+            eng = nc.gpsimd if engine == "G" else nc.vector
+            eng.tensor_tensor(
+                out=inner_cells(mconf_sb[:, EDGE:CELLS - EDGE]), in0=kept_sb[n, i][:], in1=best_sb[n, i][:],
+                op=ALU.mult,
             )
             store(2, n, i, mconf_sb)
 
         columns = [open_softmax(n, GRID1, GRID0, "c%d" % n) for n in range(BATCH)]
         rows = [open_softmax(n, GRID0, GRID1, "r%d" % n) for n in range(BATCH)]
-        bar0 = [None, None]
         bar1_all = [None, None]
 
-        transpose_quad(0, 0)
-        transpose_quad(0, 1)
-        bias_ps = psum.tile([P, P], BF16, tag="two")
+        turn(0, 0)
+        bias_ps = psum.tile([P, P], BF16, tag="bank", name="bias_ps")
         nc.tensor.transpose(bias_ps[:], bias_rows[:], ident_bf[:])
+        floor_ps = bank()
+        nc.tensor.transpose(floor_ps[:, 0:P], floor_free[:], ident[:])
         bias4 = const.tile([P, PACK], F32)
+        floor_row = const.tile([P, 1], F32)
+        quantize_x(0, 0)
         nc.vector.tensor_scalar(
             out=bias4[:], in0=bias_ps[:, 0:PACK], scalar1=INV_SQRT_C, scalar2=None, op0=ALU.mult
         )
-        project_quad(0, 0)
-        transpose_quad(0, 2)
-        project_quad(0, 1)
-        project_quad(0, 2)
-        floor_ps = psum.tile([P, P], F32, tag="two")
-        nc.tensor.transpose(floor_ps[:], floor_free[:], ident[:])
-        floor_row = const.tile([P, 1], F32)
         nc.vector.tensor_copy(out=floor_row[:], in_=floor_ps[:, 0:1])
+        for group in rows:
+            for j in range(TILES):
+                nc.vector.tensor_scalar(
+                    out=group["tops"][:, j, 3:4], in0=floor_row[:], scalar1=2.0, scalar2=-NEVER,
+                    op0=ALU.mult, op1=ALU.add,
+                )
+        turn(0, 1)
+        project(0, 0, 0, 0 not in EV0)
+        project(0, 0, 1, 1 not in EV0)
+        quantize_x(0, 1)
+        project(0, 0, 2, 2 not in EV0)
+        project(0, 0, 3, 3 not in EV0)
+        turn(0, 2)
+        project(0, 1, 0, 0 not in EV0)
+        quantize_f(0, 0)
+        project(0, 1, 1, 1 not in EV0)
+        project(0, 1, 2, 2 not in EV0)
+        quantize_x(0, 2)
+        project(0, 1, 3, 3 not in EV0)
+        project(0, 2, 0, 0 not in EV0)
+        quantize_f(0, 1)
+        for c in range(1, 4):
+            project(0, 2, c, c not in EV0)
+        quantize_f(0, 2)
 
-        for j in range(TILES):
-            softmax_tile(rows[0], j)
-            if j % 2 == 1:
-                transpose_quad(1, j // 2)
-        for j in range(TILES):
-            softmax_tile(columns[0], j)
-            if j == LAG:
-                bar0[0] = close_rows(0)
-            if j % 2 == 1:
-                project_quad(1, j // 2)
+        tiles = [(columns[0], j) for j in range(TILES)] + [(rows[0], j) for j in range(TILES)]
+        tiles += [(columns[1], j) for j in range(TILES)] + [(rows[1], j) for j in range(TILES)]
+        at = {}
 
-        for k in range(2 * TILES):
-            softmax_tile(columns[1] if k < TILES else rows[1], k % TILES)
-            if k == LAG:
-                bar1_all[0] = spread(0, close_softmax(columns[0], True))
-            if k == TILES + LAG:
-                bar1_all[1] = spread(1, close_softmax(columns[1], True))
-            home = k - LAG - 1
-            if home >= 0:
-                bring_home(home // TILES, home % TILES, columns[home // TILES]["conf"])
-            if home >= 1 and home % 2 == 1:
-                match_tile(0, home // 2, rows[0]["conf"], bar0[0], bar1_all[0])
+        def plan(r, step):
+            at.setdefault(r, []).append(step)
 
-        softmax_exp()
-        for home in range(2 * TILES - LAG - 1, 2 * TILES):
-            bring_home(1, home % TILES, columns[1]["conf"])
-        match_tile(0, TILES - 2, rows[0]["conf"], bar0[0], bar1_all[0])
-        bar0[1] = close_rows(1)
-        for i in range(TILES - 1):
-            match_tile(1, i, rows[1]["conf"], bar0[1], bar1_all[1])
+        for q in range(QUADS):
+            plan(3 * q, ("turn", 1, q))
+            plan(3 * q + 1, ("qx", 1, q))
+            for c in range(4):
+                plan(3 * q + 2 + c // 2, ("proj", 1, q, c))
+            plan(3 * q + 4, ("qf", 1, q))
+        plan(7, ("bars", columns[0], 0, TILES))
+        plan(10, ("bars", rows[0], 0, 3))
+        plan(13, ("bars", rows[0], 3, TILES))
+        plan(19, ("bars", columns[1], 0, TILES))
+        plan(22, ("bars", rows[1], 0, 3))
+        plan(24, ("bars", rows[1], 3, 5))
+        for i in range(TILES):
+            plan(H0 + STEP0 * i, ("home", 0, i))
+            plan(20 + i, ("home", 1, i))
+            if i < TILES - 1:
+                plan(H0 + 2 + STEP0 * i, ("match", 0, i))
+                plan(max(23, 22 + i) if i < 3 else 22 + i, ("match", 1, i))
+
+        dots_of(tiles[0])
+        for k in range(len(tiles) + 4):
+            steps = at.get(k, [])
+            kinds = lambda kind: [s[1:] for s in steps if s[0] == kind]
+            if k + 1 < len(tiles):
+                dots_of(tiles[k + 1])
+            if k < len(tiles):
+                tops_of(tiles[k])
+            for s in kinds("home"):
+                home_turn(*s)
+            for s in kinds("match"):
+                match_dots(*s)
+            for s in kinds("qx"):
+                quantize_x(*s)
+            for s in kinds("qf"):
+                quantize_f(*s)
+            for s in kinds("match"):
+                match_kept(*s)
+            if k < len(tiles):
+                shift_of(tiles[k])
+            for s in kinds("home"):
+                home_copy(*s)
+                if s[1] == TILES - 1:
+                    store(2, s[0], TILES - 1, zeros)
+            if k < len(tiles):
+                exp_of(tiles[k])
+            if 0 <= k - 1 < len(tiles):
+                total_of(tiles[k - 1])
+            for s in kinds("turn"):
+                turn(*s)
+            for s in kinds("proj"):
+                project(*s, s[2] not in EV1)
+            for s in kinds("home"):
+                if s[1] < TILES - 1:
+                    match_best(*s)
+            if 0 <= k - 1 < len(tiles):
+                inverse_of(tiles[k - 1])
+                divide(tiles[k - 1], S_ROW if tiles[k - 1][0]["own"] == GRID0 else S_COL)
+            for s in kinds("bars"):
+                bars_of(*s)
+                if s[0]["own"] == GRID1:
+                    bar1_all[s[0]["n"]] = spread(s[0])
+            for s in kinds("match"):
+                match_final(*s, FIN)

@@ -38,14 +38,7 @@ THRESHOLD = 0.2
 NEVER = 1.0e38
 
 FLOPS = 2 * (2 * BATCH * CELLS) * C * C + 2 * BATCH * CELLS * CELLS * C
-
-S_COL = "G"
-S_ROW = "G"
-FIN = "G"
-EV0 = (3,)
-EV1 = (1,3,)
-H0 = 9
-STEP0 = 1
+PAIR = 2 * P
 
 
 def inner_cells(cells):
@@ -61,8 +54,13 @@ def tile_coarsematching_kernel(
         keep = ctx.enter_context(tc.tile_pool(name="keep", bufs=1))
         stage = ctx.enter_context(tc.tile_pool(name="stage", bufs=2))
         mask = ctx.enter_context(tc.tile_pool(name="mask", bufs=3))
+        exps = ctx.enter_context(tc.tile_pool(name="exps", bufs=8))
+        quot = ctx.enter_context(tc.tile_pool(name="quot", bufs=4))
         psum = ctx.enter_context(tc.psum_pool(name="psum", bufs=8))
+        ctx.enter_context(tc.manual_schedule())
 
+        idle = const.tile([P, BANK], BF16)
+        nc.vector.memset(idle[:], 0.0)
         w_plane = const.tile([P, C], U8, align_bytes=64)
         nc.vector.memset(w_plane[:].bitcast(I32), 0)
         bias_rows = const.tile([P, P], BF16)
@@ -134,36 +132,37 @@ def tile_coarsematching_kernel(
             return one_bank
 
         x_grouped = {}
+        f_banks = {}
         f_grouped = {}
 
-        def turn(n, q):
-            grouped = stage.tile([P, QUAD * PACK], BF16, align_bytes=64, tag="xg", name="xg")
-            x_grouped[n, q] = grouped
-            for half in range(2):
+        def turn(chunk):
+            n, first, count = chunk
+            grouped = stage.tile([P, count * P * PACK], BF16, align_bytes=64, tag="xg%d" % count, name="xg")
+            x_grouped[chunk] = grouped
+            for pair in range(count // 2):
                 x_t = bank()
                 for c in range(2):
-                    words = x_sb[n][:, 4 * q + 2 * half + c, :].bitcast(F32)
+                    words = x_sb[n][:, first + 2 * pair + c, :].bitcast(F32)
                     for u in range(2):
                         nc.tensor.transpose(
-                            x_t[:, u * 2 * P + c * P:u * 2 * P + (c + 1) * P], words[:, u:C // 2:2], ident[:]
+                            x_t[:, u * PAIR + c * P:u * PAIR + (c + 1) * P], words[:, u:C // 2:2], ident[:]
                         )
                 nc.scalar.copy(
-                    out=grouped[:, half * QUAD * 2:(half + 1) * QUAD * 2]
+                    out=grouped[:, pair * PAIR * PACK:(pair + 1) * PAIR * PACK]
                     .bitcast(F32).rearrange("p (r u) -> p r u", u=2),
                     in_=x_t[:].rearrange("p (u r) -> p r u", u=2),
                 )
 
-        def quantize_x(n, q):
-            cells = slice(q * QUAD, (q + 1) * QUAD)
+        def quantize_x(chunk):
+            n, first, count = chunk
+            cells = slice(first * P, (first + count) * P)
             nc.vector.quantize_mx(
-                out=x_codes[n][:, cells].bitcast(FP8X4), scales=x_plane[n][:, cells], in_=x_grouped[n, q][:]
+                out=x_codes[n][:, cells].bitcast(FP8X4), scales=x_plane[n][:, cells], in_=x_grouped[chunk][:]
             )
 
-        def project(n, q, c, on_vector):
-            if c == 0:
-                f_grouped[n, q] = stage.tile([P, QUAD, PACK], BF16, align_bytes=64, tag="fg", name="fg")
-            first = c * P
-            cells = slice(q * QUAD + first, q * QUAD + first + P)
+        def project(chunk, c):
+            n, first, count = chunk
+            cells = slice((first + c) * P, (first + c + 1) * P)
             acc = bank()
             for t in range(PACK):
                 nc.tensor.matmul_mx(
@@ -175,33 +174,43 @@ def tile_coarsematching_kernel(
                     start=True,
                     stop=True,
                 )
-            target = f_grouped[n, q][:, first:first + P, :]
-            if on_vector:
-                nc.vector.scalar_tensor_tensor(
-                    out=target,
-                    in0=acc[:].rearrange("p (t r) -> p r t", t=PACK),
-                    scalar=INV_SQRT_C,
-                    in1=bias4[:].unsqueeze(1).to_broadcast([P, P, PACK]),
-                    op0=ALU.mult,
-                    op1=ALU.add,
-                )
-            else:
-                rows4 = stage.tile([P, PACK, P], BF16, tag="rows4", name="rows4")
-                for t in range(PACK):
-                    nc.scalar.activation(
-                        out=rows4[:, t, :], in_=acc[:, t * P:(t + 1) * P], func=FUNC.Identity,
-                        scale=INV_SQRT_C, bias=bias4[:, t:t + 1],
-                    )
-                nc.gpsimd.tensor_scalar(
-                    out=target, in0=rows4[:].rearrange("p t r -> p r t"),
-                    scalar1=1.0, scalar2=0.0, op0=ALU.mult, op1=ALU.add,
-                )
+            f_banks[chunk, c] = acc
 
-        def quantize_f(n, q):
-            cells = slice(q * QUAD, (q + 1) * QUAD)
+        def f_target(chunk, c):
+            if chunk not in f_grouped:
+                f_grouped[chunk] = stage.tile(
+                    [P, chunk[2] * P, PACK], BF16, align_bytes=64, tag="fg%d" % chunk[2], name="fg"
+                )
+            return f_grouped[chunk][:, c * P:(c + 1) * P, :]
+
+        def emit_on_vector(chunk, c):
+            nc.vector.scalar_tensor_tensor(
+                out=f_target(chunk, c),
+                in0=f_banks[chunk, c][:].rearrange("p (t r) -> p r t", t=PACK),
+                scalar=INV_SQRT_C,
+                in1=bias4[:].unsqueeze(1).to_broadcast([P, P, PACK]),
+                op0=ALU.mult,
+                op1=ALU.add,
+            )
+
+        def emit_on_scalar(chunk, c):
+            rows4 = stage.tile([P, PACK, P], BF16, tag="rows4", name="rows4")
+            for t in range(PACK):
+                nc.scalar.activation(
+                    out=rows4[:, t, :], in_=f_banks[chunk, c][:, t * P:(t + 1) * P], func=FUNC.Identity,
+                    scale=INV_SQRT_C, bias=bias4[:, t:t + 1],
+                )
+            nc.gpsimd.tensor_scalar(
+                out=f_target(chunk, c), in0=rows4[:].rearrange("p t r -> p r t"),
+                scalar1=1.0, scalar2=0.0, op0=ALU.mult, op1=ALU.add,
+            )
+
+        def quantize_f(chunk):
+            n, first, count = chunk
+            cells = slice(first * P, (first + count) * P)
             nc.vector.quantize_mx(
                 out=f_codes[n][:, cells].bitcast(FP8X4), scales=f_plane[n][:, cells],
-                in_=f_grouped[n, q][:].rearrange("p r t -> p (r t)"),
+                in_=f_grouped[chunk][:].rearrange("p r t -> p (r t)"),
             )
 
         def dot_banks(n, own, other, j, spans):
@@ -231,7 +240,7 @@ def tile_coarsematching_kernel(
                 "total": keep.tile([P, TILES], F32, name="total_" + label),
                 "inv": keep.tile([P, TILES], F32, name="inv_" + label),
                 "bar": keep.tile([P, TILES], F32, name="bar_" + label),
-                "conf": [keep.tile([P, CELLS], F32, name="e_%s_%d" % (label, j)) for j in range(TILES)],
+                "e": {},
             }
             return group
 
@@ -239,10 +248,9 @@ def tile_coarsematching_kernel(
             group, j = tile
             group[j] = dot_banks(group["n"], group["own"], group["other"], j, SPANS)
 
-        def tops_of(tile):
+        def top_of(tile, k):
             group, j = tile
-            for k in range(2):
-                nc.vector.reduce_max(out=group["tops"][:, j, k:k + 1], in_=group[j][k], axis=AXIS.X)
+            nc.vector.reduce_max(out=group["tops"][:, j, k:k + 1], in_=group[j][k], axis=AXIS.X)
 
         def shift_of(tile):
             group, j = tile
@@ -253,10 +261,15 @@ def tile_coarsematching_kernel(
 
         def exp_of(tile):
             group, j = tile
+            if group["own"] == GRID0:
+                e = exps.tile([P, CELLS], F32, tag="e", name="e")
+            else:
+                e = keep.tile([P, CELLS], F32, name="col_%d_%d" % (group["n"], j))
+            group["e"][j] = e
             for k in range(2):
                 lo, hi = SPANS[k]
                 nc.scalar.activation(
-                    out=group["conf"][j][:, lo:hi], in_=group[j][k], func=FUNC.Exp,
+                    out=e[:, lo:hi], in_=group[j][k], func=FUNC.Exp,
                     bias=group["shift"][:, j:j + 1], scale=INV_TEMPERATURE,
                     accum_out=group["sums"][:, j, k:k + 1],
                 )
@@ -273,24 +286,29 @@ def tile_coarsematching_kernel(
 
         def divide(tile, engine):
             group, j = tile
-            conf = group["conf"][j]
+            e = group["e"][j]
+            conf = e
+            if group["own"] == GRID0:
+                conf = quot.tile([P, CELLS], F32, tag="conf0", name="conf0")
             inv = group["inv"][:, j:j + 1]
             if engine == "G":
                 nc.gpsimd.tensor_scalar(
-                    out=conf[:], in0=conf[:], scalar1=inv, scalar2=0.0, op0=ALU.mult, op1=ALU.add
+                    out=conf[:], in0=e[:], scalar1=inv, scalar2=0.0, op0=ALU.mult, op1=ALU.add
                 )
             elif engine == "V":
-                nc.vector.tensor_scalar(out=conf[:], in0=conf[:], scalar1=inv, scalar2=None, op0=ALU.mult)
+                nc.vector.tensor_scalar(out=conf[:], in0=e[:], scalar1=inv, scalar2=None, op0=ALU.mult)
             else:
-                nc.scalar.activation(out=conf[:], in_=conf[:], func=FUNC.Copy, scale=inv)
+                nc.scalar.activation(out=conf[:], in_=e[:], func=FUNC.Copy, scale=inv)
             if group["own"] == GRID0:
                 store(0, group["n"], j, conf)
 
-        def bars_of(group, first, last):
+        def pen_of(group, first, last):
             nc.vector.tensor_scalar(
                 out=group["tops"][:, first:last, 2], in0=group["inv"][:, first:last],
                 scalar1=THRESHOLD, scalar2=-NEVER, op0=ALU.subtract, op1=ALU.mult,
             )
+
+        def bar_of(group, first, last):
             cols = 4 if group["own"] == GRID0 else 3
             nc.vector.tensor_reduce(
                 out=group["bar"][:, first:last], in_=group["tops"][:, first:last, 0:cols], axis=AXIS.X, op=ALU.max
@@ -333,7 +351,7 @@ def tile_coarsematching_kernel(
                 ps = bank()
                 for j in range(lo // P, hi // P):
                     nc.tensor.transpose(
-                        ps[:, j * P - lo:(j + 1) * P - lo], columns[n]["conf"][j][:, i * P:(i + 1) * P], ident[:]
+                        ps[:, j * P - lo:(j + 1) * P - lo], columns[n]["e"][j][:, i * P:(i + 1) * P], ident[:]
                     )
                 banks.append(ps[:, 0:hi - lo])
             home_banks[n, i] = banks
@@ -347,29 +365,29 @@ def tile_coarsematching_kernel(
         def match_dots(n, i):
             dots_again[n, i] = dot_banks(n, GRID0, GRID1, i, INNER_SPANS)
 
-        def match_kept(n, i):
-            kept = mask.tile([P, INNER_ROWS, INNER_COLS], F32, tag="kept", name="kept")
-            kept_sb[n, i] = kept
-            for k in range(2):
-                lo, hi = INNER_SPANS[k]
-                g = slice((lo - EDGE) // GRID_W, (hi - EDGE) // GRID_W)
-                nc.vector.scalar_tensor_tensor(
-                    out=kept[:, g, :], in0=inner_cells(bar1_all[n][:, lo:hi]), scalar=rows[n]["bar"][:, i:i + 1],
-                    in1=inner_cells(dots_again[n, i][k]), op0=ALU.min, op1=ALU.is_le,
-                )
+        def match_kept(n, i, k):
+            if k == 0:
+                kept_sb[n, i] = mask.tile([P, INNER_ROWS, INNER_COLS], F32, tag="kept", name="kept")
+            lo, hi = INNER_SPANS[k]
+            g = slice((lo - EDGE) // GRID_W, (hi - EDGE) // GRID_W)
+            nc.vector.scalar_tensor_tensor(
+                out=kept_sb[n, i][:, g, :], in0=inner_cells(bar1_all[n][:, lo:hi]),
+                scalar=rows[n]["bar"][:, i:i + 1],
+                in1=inner_cells(dots_again[n, i][k]), op0=ALU.min, op1=ALU.is_le,
+            )
 
-        def match_best(n, i):
-            best = mask.tile([P, INNER_ROWS, INNER_COLS], F32, tag="best", name="best")
-            best_sb[n, i] = best
-            conf0 = rows[n]["conf"][i]
-            for k in range(2):
-                lo, hi = SPANS[k]
-                lo, hi = max(lo, EDGE), min(hi, CELLS - EDGE)
-                g = slice((lo - EDGE) // GRID_W, (hi - EDGE) // GRID_W)
-                nc.vector.tensor_tensor(
-                    out=best[:, g, :], in0=inner_cells(conf0[:, lo:hi]),
-                    in1=inner_cells(home_banks[n, i][k][:, lo - SPANS[k][0]:hi - SPANS[k][0]]), op=ALU.max,
-                )
+        def match_best(n, i, k):
+            if k == 0:
+                best_sb[n, i] = mask.tile([P, INNER_ROWS, INNER_COLS], F32, tag="best", name="best")
+            lo, hi = SPANS[k]
+            lo, hi = max(lo, EDGE), min(hi, CELLS - EDGE)
+            g = slice((lo - EDGE) // GRID_W, (hi - EDGE) // GRID_W)
+            nc.vector.scalar_tensor_tensor(
+                out=best_sb[n, i][:, g, :], in0=inner_cells(rows[n]["e"][i][:, lo:hi]),
+                scalar=rows[n]["inv"][:, i:i + 1],
+                in1=inner_cells(home_banks[n, i][k][:, lo - SPANS[k][0]:hi - SPANS[k][0]]),
+                op0=ALU.mult, op1=ALU.max,
+            )
 
         def match_final(n, i, engine):
             mconf_sb = mconf_tiles[i % MCONF_TILES]
@@ -383,111 +401,163 @@ def tile_coarsematching_kernel(
         columns = [open_softmax(n, GRID1, GRID0, "c%d" % n) for n in range(BATCH)]
         rows = [open_softmax(n, GRID0, GRID1, "r%d" % n) for n in range(BATCH)]
         bar1_all = [None, None]
+        pending = []
 
-        turn(0, 0)
-        bias_ps = psum.tile([P, P], BF16, tag="bank", name="bias_ps")
-        nc.tensor.transpose(bias_ps[:], bias_rows[:], ident_bf[:])
-        floor_ps = bank()
-        nc.tensor.transpose(floor_ps[:, 0:P], floor_free[:], ident[:])
-        bias4 = const.tile([P, PACK], F32)
-        floor_row = const.tile([P, 1], F32)
-        quantize_x(0, 0)
-        nc.vector.tensor_scalar(
-            out=bias4[:], in0=bias_ps[:, 0:PACK], scalar1=INV_SQRT_C, scalar2=None, op0=ALU.mult
-        )
-        nc.vector.tensor_copy(out=floor_row[:], in_=floor_ps[:, 0:1])
-        for group in rows:
-            for j in range(TILES):
-                nc.vector.tensor_scalar(
-                    out=group["tops"][:, j, 3:4], in0=floor_row[:], scalar1=2.0, scalar2=-NEVER,
-                    op0=ALU.mult, op1=ALU.add,
-                )
-        turn(0, 1)
-        project(0, 0, 0, 0 not in EV0)
-        project(0, 0, 1, 1 not in EV0)
-        quantize_x(0, 1)
-        project(0, 0, 2, 2 not in EV0)
-        project(0, 0, 3, 3 not in EV0)
-        turn(0, 2)
-        project(0, 1, 0, 0 not in EV0)
-        quantize_f(0, 0)
-        project(0, 1, 1, 1 not in EV0)
-        project(0, 1, 2, 2 not in EV0)
-        quantize_x(0, 2)
-        project(0, 1, 3, 3 not in EV0)
-        project(0, 2, 0, 0 not in EV0)
-        quantize_f(0, 1)
-        for c in range(1, 4):
-            project(0, 2, c, c not in EV0)
-        quantize_f(0, 2)
+        def large(step, *args):
+            ready = list(pending)
+            pending.clear()
+            step(*args)
+            for small, small_args in ready:
+                small(*small_args)
 
-        tiles = [(columns[0], j) for j in range(TILES)] + [(rows[0], j) for j in range(TILES)]
-        tiles += [(columns[1], j) for j in range(TILES)] + [(rows[1], j) for j in range(TILES)]
-        at = {}
+        def later(step, *args):
+            pending.append((step, args))
 
-        def plan(r, step):
-            at.setdefault(r, []).append(step)
+        warm_ps = bank()
 
-        for q in range(QUADS):
-            plan(3 * q, ("turn", 1, q))
-            plan(3 * q + 1, ("qx", 1, q))
+        def warm_up(times):
+            for repeat in range(times):
+                nc.tensor.matmul(out=warm_ps[:], lhsT=idle[:, 0:P], rhs=idle[:], start=True, stop=True)
+
+        warm_up(4)
+
+        tiles = [(rows[0], j) for j in range(TILES)] + [(columns[0], j) for j in range(TILES)]
+        tiles += [(columns[1], 0), (columns[1], 1), (columns[1], 2), (columns[1], 3), (columns[1], 4), (columns[1], 5), (rows[1], 0), (rows[1], 1), (rows[1], 2), (rows[1], 3), (rows[1], 4), (rows[1], 5)]
+        chunks = [(0, 0, 2), (0, 2, 2), (0, 4, 4), (0, 8, 4)]
+        on_scalar = [[],[1],[1,3],[1,3]]
+        ahead = 2
+        plan = {}
+
+        def emit(chunk, c, scalar):
+            project(chunk, c)
+            emit_out(chunk, c, scalar)
+
+        def emit_out(chunk, c, scalar):
+            if scalar:
+                emit_on_scalar(chunk, c)
+            else:
+                large(emit_on_vector, chunk, c)
+
+        for q in range(3):
+            chunk = (1, 4 * q, 4)
+            r = -4 + 4 * q
+            plan.setdefault(r, []).append((turn, chunk))
+            plan.setdefault(r + 2, []).append((large, quantize_x, chunk))
             for c in range(4):
-                plan(3 * q + 2 + c // 2, ("proj", 1, q, c))
-            plan(3 * q + 4, ("qf", 1, q))
-        plan(7, ("bars", columns[0], 0, TILES))
-        plan(10, ("bars", rows[0], 0, 3))
-        plan(13, ("bars", rows[0], 3, TILES))
-        plan(19, ("bars", columns[1], 0, TILES))
-        plan(22, ("bars", rows[1], 0, 3))
-        plan(24, ("bars", rows[1], 3, 5))
+                plan.setdefault(r + 2 + c // 2, []).append((project, chunk, c))
+            for c in range(4):
+                plan.setdefault(r + 3 + c // 2, []).insert(0, (emit_out, chunk, c, c in [1,3]))
+            plan.setdefault(r + 6, []).insert(0, (large, quantize_f, chunk))
+
+        for step in range(len(chunks) + ahead + 1):
+            if step < len(chunks):
+                turn(chunks[step])
+            if step == 0:
+                bias_ps = psum.tile([P, P], BF16, tag="bank", name="bias_ps")
+                nc.tensor.transpose(bias_ps[:], bias_rows[:], ident_bf[:])
+                floor_ps = bank()
+                nc.tensor.transpose(floor_ps[:, 0:P], floor_free[:], ident[:])
+                bias4 = const.tile([P, PACK], F32)
+                floor_row = const.tile([P, 1], F32)
+                nc.vector.tensor_scalar(
+                    out=bias4[:], in0=bias_ps[:, 0:PACK], scalar1=INV_SQRT_C, scalar2=None, op0=ALU.mult
+                )
+                nc.vector.tensor_copy(out=floor_row[:], in_=floor_ps[:, 0:1])
+                for group in rows:
+                    nc.vector.tensor_scalar(
+                        out=group["tops"][:, :, 3], in0=floor_ps[:, 0:1].to_broadcast([P, TILES]),
+                        scalar1=2.0, scalar2=-NEVER, op0=ALU.mult, op1=ALU.add,
+                    )
+            if step == 1:
+                warm_up(2)
+            old = step - ahead
+            for side in plan.get(step - len(chunks) - 3, []):
+                side[0](*side[1:])
+            if 0 <= old < len(chunks):
+                chunk = chunks[old]
+                for c in range(chunk[2]):
+                    emit(chunk, c, c in on_scalar[old])
+                    if c == 0:
+                        if old >= 1:
+                            quantize_f(chunks[old - 1])
+                        if step < len(chunks):
+                            quantize_x(chunks[step])
+            elif step < len(chunks):
+                quantize_x(chunks[step])
+        quantize_f(chunks[-1])
+
+        home = {}
         for i in range(TILES):
-            plan(H0 + STEP0 * i, ("home", 0, i))
-            plan(20 + i, ("home", 1, i))
-            if i < TILES - 1:
-                plan(H0 + 2 + STEP0 * i, ("match", 0, i))
-                plan(max(23, 22 + i) if i < 3 else 22 + i, ("match", 1, i))
+            home.setdefault(15 + i, []).append((0, i))
+            home.setdefault(20 + i, []).append((1, i))
+
+        def close(tile):
+            group, j = tile
+            divide(tile, "G" if group["own"] == GRID1 else "G")
+            if group["own"] == GRID1 or j < TILES - 1:
+                later(pen_bar, tile)
+
+        def pen_bar(tile):
+            group, j = tile
+            pen_of(group, j, j + 1)
+            if group["own"] == GRID0:
+                later(bar_of, group, j, j + 1)
+            elif j == TILES - 1:
+                later(column_bars, group)
+
+        def column_bars(group):
+            bar_of(group, 0, TILES)
+            bar1_all[group["n"]] = spread(group)
+
+        def invert(tile):
+            inverse_of(tile)
+            close(tile)
+
+        def sum_up(tile):
+            total_of(tile)
+            later(invert, tile)
+
+        def exponentials(k):
+            shift_of(tiles[k])
+            exp_of(tiles[k])
+            if k >= 1:
+                later(sum_up, tiles[k - 1])
+            if k == len(tiles) - 1:
+                later(sum_up_last, k)
+
+        def sum_up_last(k):
+            later(sum_up, tiles[k])
 
         dots_of(tiles[0])
-        for k in range(len(tiles) + 4):
-            steps = at.get(k, [])
-            kinds = lambda kind: [s[1:] for s in steps if s[0] == kind]
+        for k in range(max(home) + 2):
             if k + 1 < len(tiles):
                 dots_of(tiles[k + 1])
+            if k == 1:
+                for n in range(BATCH):
+                    store(2, n, TILES - 1, zeros)
+            coming = home.get(k, [])
+            inner = [s for s in coming if s[1] < TILES - 1]
+            before = [s for s in home.get(k - 1, []) if s[1] < TILES - 1]
             if k < len(tiles):
-                tops_of(tiles[k])
-            for s in kinds("home"):
+                large(top_of, tiles[k], 0)
+                large(top_of, tiles[k], 1)
+                later(exponentials, k)
+            for s in coming:
                 home_turn(*s)
-            for s in kinds("match"):
+            pass
+            for s in before:
+                large(match_kept, *s, 0)
+                large(match_kept, *s, 1)
+                match_final(*s, "G")
+            for s in inner:
                 match_dots(*s)
-            for s in kinds("qx"):
-                quantize_x(*s)
-            for s in kinds("qf"):
-                quantize_f(*s)
-            for s in kinds("match"):
-                match_kept(*s)
-            if k < len(tiles):
-                shift_of(tiles[k])
-            for s in kinds("home"):
+                large(match_best, *s, 0)
+                large(match_best, *s, 1)
+            for s in coming:
                 home_copy(*s)
-                if s[1] == TILES - 1:
-                    store(2, s[0], TILES - 1, zeros)
-            if k < len(tiles):
-                exp_of(tiles[k])
-            if 0 <= k - 1 < len(tiles):
-                total_of(tiles[k - 1])
-            for s in kinds("turn"):
-                turn(*s)
-            for s in kinds("proj"):
-                project(*s, s[2] not in EV1)
-            for s in kinds("home"):
-                if s[1] < TILES - 1:
-                    match_best(*s)
-            if 0 <= k - 1 < len(tiles):
-                inverse_of(tiles[k - 1])
-                divide(tiles[k - 1], S_ROW if tiles[k - 1][0]["own"] == GRID0 else S_COL)
-            for s in kinds("bars"):
-                bars_of(*s)
-                if s[0]["own"] == GRID1:
-                    bar1_all[s[0]["n"]] = spread(s[0])
-            for s in kinds("match"):
-                match_final(*s, FIN)
+            for side in plan.get(k, []):
+                side[0](*side[1:])
+            if k >= len(tiles):
+                large(lambda: None)
+        while pending:
+            large(lambda: None)

@@ -31,13 +31,14 @@ SPANS = ((0, BANK), (BANK, CELLS))
 INNER_SPANS = ((EDGE, EDGE + BANK), (EDGE + BANK, CELLS - EDGE))
 GRID1 = 0
 GRID0 = CELLS
-MCONF_TILES = 3
+MCONF_TILES = 5
 INV_SQRT_C = 1.0 / (C ** 0.5)
 INV_TEMPERATURE = 10.0
 THRESHOLD = 0.2
 NEVER = 1.0e38
 
 FLOPS = 2 * (2 * BATCH * CELLS) * C * C + 2 * BATCH * CELLS * CELLS * C
+HALVES = ((0, CELLS // 2), (CELLS // 2, CELLS))
 PAIR = 2 * P
 
 
@@ -52,9 +53,9 @@ def tile_coarsematching_kernel(
     with ExitStack() as ctx:
         const = ctx.enter_context(tc.tile_pool(name="const", bufs=1))
         keep = ctx.enter_context(tc.tile_pool(name="keep", bufs=1))
-        stage = ctx.enter_context(tc.tile_pool(name="stage", bufs=2))
+        stage = ctx.enter_context(tc.tile_pool(name="stage", bufs=3))
         mask = ctx.enter_context(tc.tile_pool(name="mask", bufs=3))
-        exps = ctx.enter_context(tc.tile_pool(name="exps", bufs=8))
+        exps = ctx.enter_context(tc.tile_pool(name="exps", bufs=12))
         quot = ctx.enter_context(tc.tile_pool(name="quot", bufs=4))
         psum = ctx.enter_context(tc.psum_pool(name="psum", bufs=8))
         ctx.enter_context(tc.manual_schedule())
@@ -135,23 +136,24 @@ def tile_coarsematching_kernel(
         f_banks = {}
         f_grouped = {}
 
-        def turn(chunk):
+        def turn(chunk, pair):
             n, first, count = chunk
-            grouped = stage.tile([P, count * P * PACK], BF16, align_bytes=64, tag="xg%d" % count, name="xg")
-            x_grouped[chunk] = grouped
-            for pair in range(count // 2):
-                x_t = bank()
-                for c in range(2):
-                    words = x_sb[n][:, first + 2 * pair + c, :].bitcast(F32)
-                    for u in range(2):
-                        nc.tensor.transpose(
-                            x_t[:, u * PAIR + c * P:u * PAIR + (c + 1) * P], words[:, u:C // 2:2], ident[:]
-                        )
-                nc.scalar.copy(
-                    out=grouped[:, pair * PAIR * PACK:(pair + 1) * PAIR * PACK]
-                    .bitcast(F32).rearrange("p (r u) -> p r u", u=2),
-                    in_=x_t[:].rearrange("p (u r) -> p r u", u=2),
+            if pair == 0:
+                x_grouped[chunk] = stage.tile(
+                    [P, count * P * PACK], BF16, align_bytes=64, tag="xg%d" % count, name="xg"
                 )
+            x_t = bank()
+            for c in range(2):
+                words = x_sb[n][:, first + 2 * pair + c, :].bitcast(F32)
+                for u in range(2):
+                    nc.tensor.transpose(
+                        x_t[:, u * PAIR + c * P:u * PAIR + (c + 1) * P], words[:, u:C // 2:2], ident[:]
+                    )
+            nc.scalar.copy(
+                out=x_grouped[chunk][:, pair * PAIR * PACK:(pair + 1) * PAIR * PACK]
+                .bitcast(F32).rearrange("p (r u) -> p r u", u=2),
+                in_=x_t[:].rearrange("p (u r) -> p r u", u=2),
+            )
 
         def quantize_x(chunk):
             n, first, count = chunk
@@ -234,9 +236,9 @@ def tile_coarsematching_kernel(
                 "n": n,
                 "own": own,
                 "other": other,
-                "tops": keep.tile([P, TILES, 4], F32, name="tops_" + label),
+                "tops": keep.tile([P, TILES, 3], F32, name="tops_" + label),
+                "part": keep.tile([P, TILES], F32, name="part_" + label),
                 "shift": keep.tile([P, TILES], F32, name="shift_" + label),
-                "sums": keep.tile([P, TILES, 2], F32, name="sums_" + label),
                 "total": keep.tile([P, TILES], F32, name="total_" + label),
                 "inv": keep.tile([P, TILES], F32, name="inv_" + label),
                 "bar": keep.tile([P, TILES], F32, name="bar_" + label),
@@ -244,40 +246,37 @@ def tile_coarsematching_kernel(
             }
             return group
 
-        def dots_of(tile):
+        def dots_of(tile, k):
             group, j = tile
-            group[j] = dot_banks(group["n"], group["own"], group["other"], j, SPANS)
+            group[j, k] = dot_banks(group["n"], group["own"], group["other"], j, SPANS[k:k + 1])[0]
 
-        def top_of(tile, k):
+        def take(tile, k):
             group, j = tile
-            nc.vector.reduce_max(out=group["tops"][:, j, k:k + 1], in_=group[j][k], axis=AXIS.X)
+            if k == 0:
+                if group["own"] == GRID0:
+                    e = exps.tile([P, CELLS], F32, tag="e", name="e")
+                else:
+                    e = keep.tile([P, CELLS], F32, name="col_%d_%d" % (group["n"], j))
+                group["e"][j] = e
+            lo, hi = SPANS[k]
+            nc.vector.tensor_scalar(
+                out=group["e"][j][:, lo:hi], in0=group[j, k], scalar1=1.0,
+                scalar2=None if k == 0 else group["part"][:, j:j + 1], op0=ALU.mult, op1=ALU.max,
+                accum_out=group["part"][:, j:j + 1] if k == 0 else group["tops"][:, j, 0:1],
+            )
 
         def shift_of(tile):
             group, j = tile
-            nc.vector.tensor_scalar(
-                out=group["shift"][:, j:j + 1], in0=group["tops"][:, j, 0:1],
-                scalar1=group["tops"][:, j, 1:2], scalar2=-INV_TEMPERATURE, op0=ALU.max, op1=ALU.mult,
+            nc.scalar.activation(
+                out=group["shift"][:, j:j + 1], in_=group["tops"][:, j, 0:1], func=FUNC.Copy, scale=-INV_TEMPERATURE
             )
 
         def exp_of(tile):
             group, j = tile
-            if group["own"] == GRID0:
-                e = exps.tile([P, CELLS], F32, tag="e", name="e")
-            else:
-                e = keep.tile([P, CELLS], F32, name="col_%d_%d" % (group["n"], j))
-            group["e"][j] = e
-            for k in range(2):
-                lo, hi = SPANS[k]
-                nc.scalar.activation(
-                    out=e[:, lo:hi], in_=group[j][k], func=FUNC.Exp,
-                    bias=group["shift"][:, j:j + 1], scale=INV_TEMPERATURE,
-                    accum_out=group["sums"][:, j, k:k + 1],
-                )
-
-        def total_of(tile):
-            group, j = tile
-            nc.vector.tensor_reduce(
-                out=group["total"][:, j:j + 1], in_=group["sums"][:, j, :], axis=AXIS.X, op=ALU.add
+            e = group["e"][j]
+            nc.scalar.activation(
+                out=e[:], in_=e[:], func=FUNC.Exp, bias=group["shift"][:, j:j + 1], scale=INV_TEMPERATURE,
+                accum_out=group["total"][:, j:j + 1],
             )
 
         def inverse_of(tile):
@@ -302,32 +301,37 @@ def tile_coarsematching_kernel(
             if group["own"] == GRID0:
                 store(0, group["n"], j, conf)
 
-        def pen_of(group, first, last):
-            nc.vector.tensor_scalar(
-                out=group["tops"][:, first:last, 2], in0=group["inv"][:, first:last],
-                scalar1=THRESHOLD, scalar2=-NEVER, op0=ALU.subtract, op1=ALU.mult,
+        def pen_of(tile):
+            group, j = tile
+            nc.scalar.activation(
+                out=group["tops"][:, j, 1:2], in_=group["inv"][:, j:j + 1], func=FUNC.Copy,
+                scale=-NEVER, bias=THRESHOLD * NEVER,
             )
 
         def bar_of(group, first, last):
-            cols = 4 if group["own"] == GRID0 else 3
+            cols = 3 if group["own"] == GRID0 else 2
             nc.vector.tensor_reduce(
                 out=group["bar"][:, first:last], in_=group["tops"][:, first:last, 0:cols], axis=AXIS.X, op=ALU.max
             )
 
-        def spread(group):
-            bar_all = keep.tile([P, CELLS], F32, name="barall_%d" % group["n"])
-            for lo, hi in SPANS:
-                ps = bank()
-                for j in range(lo // P, hi // P):
-                    nc.tensor.transpose(
-                        ps[:, j * P - lo:(j + 1) * P - lo],
-                        group["bar"][:, j:j + 1].to_broadcast([P, P]), ident[:]
-                    )
-                nc.scalar.activation(
-                    out=bar_all[:, lo:hi], in_=ps[:, 0:hi - lo], func=FUNC.Identity, bias=floor_row[:, 0:1],
-                    scale=1.0,
+        def spread(group, k):
+            lo, hi = SPANS[k]
+            ps = bank()
+            for j in range(lo // P, hi // P):
+                nc.tensor.transpose(
+                    ps[:, j * P - lo:(j + 1) * P - lo], group["bar"][:, j:j + 1].to_broadcast([P, P]), ident[:]
                 )
-            return bar_all
+            group["spread", k] = ps
+
+        def spread_copy(group, k):
+            n = group["n"]
+            if k == 0:
+                bar1_all[n] = keep.tile([P, CELLS], F32, name="barall_%d" % n)
+            lo, hi = SPANS[k]
+            nc.scalar.activation(
+                out=bar1_all[n][:, lo:hi], in_=group["spread", k][:, 0:hi - lo], func=FUNC.Identity,
+                bias=floor_row[:, 0:1], scale=1.0,
+            )
 
         def store(plane, n, i, rows_sb):
             if i < TILES - 1:
@@ -336,10 +340,7 @@ def tile_coarsematching_kernel(
                 nc.sync.dma_start(out=out[plane, n, CELLS - EDGE:CELLS, :], in_=rows_sb[0:EDGE, :])
                 nc.sync.dma_start(out=out[plane, n, 0:EDGE, :], in_=rows_sb[EDGE:P, :])
 
-        conf1_sb = [
-            [keep.tile([P, CELLS], F32, name="conf1_%d_%d" % (n, i)) for i in range(TILES)]
-            for n in range(BATCH)
-        ]
+        conf1_sb = {}
         home_banks = {}
         dots_again = {}
         kept_sb = {}
@@ -347,7 +348,7 @@ def tile_coarsematching_kernel(
 
         def home_turn(n, i):
             banks = []
-            for lo, hi in SPANS:
+            for lo, hi in HALVES:
                 ps = bank()
                 for j in range(lo // P, hi // P):
                     nc.tensor.transpose(
@@ -356,11 +357,11 @@ def tile_coarsematching_kernel(
                 banks.append(ps[:, 0:hi - lo])
             home_banks[n, i] = banks
 
-        def home_copy(n, i):
-            for k in range(2):
-                lo, hi = SPANS[k]
-                nc.scalar.copy(out=conf1_sb[n][i][:, lo:hi], in_=home_banks[n, i][k])
-            store(1, n, i, conf1_sb[n][i])
+        def home_copy(n, i, k):
+            lo, hi = HALVES[k]
+            if (n, i) not in conf1_sb:
+                conf1_sb[n, i] = quot.tile([P, CELLS], F32, tag="conf1", name="conf1")
+            nc.scalar.copy(out=conf1_sb[n, i][:, lo:hi], in_=home_banks[n, i][k])
 
         def match_dots(n, i):
             dots_again[n, i] = dot_banks(n, GRID0, GRID1, i, INNER_SPANS)
@@ -379,13 +380,13 @@ def tile_coarsematching_kernel(
         def match_best(n, i, k):
             if k == 0:
                 best_sb[n, i] = mask.tile([P, INNER_ROWS, INNER_COLS], F32, tag="best", name="best")
-            lo, hi = SPANS[k]
+            lo, hi = HALVES[k]
             lo, hi = max(lo, EDGE), min(hi, CELLS - EDGE)
             g = slice((lo - EDGE) // GRID_W, (hi - EDGE) // GRID_W)
             nc.vector.scalar_tensor_tensor(
                 out=best_sb[n, i][:, g, :], in0=inner_cells(rows[n]["e"][i][:, lo:hi]),
                 scalar=rows[n]["inv"][:, i:i + 1],
-                in1=inner_cells(home_banks[n, i][k][:, lo - SPANS[k][0]:hi - SPANS[k][0]]),
+                in1=inner_cells(home_banks[n, i][k][:, lo - HALVES[k][0]:hi - HALVES[k][0]]),
                 op0=ALU.mult, op1=ALU.max,
             )
 
@@ -423,14 +424,7 @@ def tile_coarsematching_kernel(
 
         tiles = [(rows[0], j) for j in range(TILES)] + [(columns[0], j) for j in range(TILES)]
         tiles += [(columns[1], 0), (columns[1], 1), (columns[1], 2), (columns[1], 3), (columns[1], 4), (columns[1], 5), (rows[1], 0), (rows[1], 1), (rows[1], 2), (rows[1], 3), (rows[1], 4), (rows[1], 5)]
-        chunks = [(0, 0, 2), (0, 2, 2), (0, 4, 4), (0, 8, 4)]
-        on_scalar = [[],[1],[1,3],[1,3]]
-        ahead = 2
         plan = {}
-
-        def emit(chunk, c, scalar):
-            project(chunk, c)
-            emit_out(chunk, c, scalar)
 
         def emit_out(chunk, c, scalar):
             if scalar:
@@ -438,21 +432,46 @@ def tile_coarsematching_kernel(
             else:
                 large(emit_on_vector, chunk, c)
 
+        def emit(chunk, c, scalar):
+            project(chunk, c)
+            emit_out(chunk, c, scalar)
+
+        def side(r, late, step, *args):
+            plan.setdefault((r, late), []).append((step, args))
+
+        def do_side(r, late):
+            for step, args in plan.get((r, late), []):
+                step(*args)
+
+        for p in range(6):
+            chunk = (0, 2 * p, 2)
+            r = p - 7
+            share = [0, 1, 1, 0, 0, 1][p]
+            side(r, 1, turn, chunk, 0)
+            if p < 2:
+                side(r, 1, warm_up, 2)
+            elif p < 5:
+                side(r, 1, warm_up, 1)
+            side(r + 1, 0, large, quantize_x, chunk)
+            for c in range(2):
+                side(r + 2, 1, project, chunk, c)
+                side(r + 2 if r < -2 else r + 3, 2 if r < -2 else 0, emit_out, chunk, c, share and c == 1)
+            side(r + (4 if share else 3), 0, large, quantize_f, chunk)
         for q in range(3):
             chunk = (1, 4 * q, 4)
-            r = -4 + 4 * q
-            plan.setdefault(r, []).append((turn, chunk))
-            plan.setdefault(r + 2, []).append((large, quantize_x, chunk))
+            r = [-2,1,4][q]
+            for pair in range(2):
+                side(r + pair, 1, turn, chunk, pair)
+            side(r + 2, 3 if r + 2 >= 0 else 0, large, quantize_x, chunk)
             for c in range(4):
-                plan.setdefault(r + 2 + c // 2, []).append((project, chunk, c))
-            for c in range(4):
-                plan.setdefault(r + 3 + c // 2, []).insert(0, (emit_out, chunk, c, c in [1,3]))
-            plan.setdefault(r + 6, []).insert(0, (large, quantize_f, chunk))
-
-        for step in range(len(chunks) + ahead + 1):
-            if step < len(chunks):
-                turn(chunks[step])
-            if step == 0:
+                side(r + 2 + c // 2, 1, project, chunk, c)
+                side(r + 3 + c // 2, 0, emit_out, chunk, c, c % 2 == 1)
+            side(r + 6, 3, large, quantize_f, chunk)
+        for r in range(-7, 0):
+            do_side(r, 0)
+            do_side(r, 1)
+            do_side(r, 2)
+            if r == -7:
                 bias_ps = psum.tile([P, P], BF16, tag="bank", name="bias_ps")
                 nc.tensor.transpose(bias_ps[:], bias_rows[:], ident_bf[:])
                 floor_ps = bank()
@@ -465,99 +484,94 @@ def tile_coarsematching_kernel(
                 nc.vector.tensor_copy(out=floor_row[:], in_=floor_ps[:, 0:1])
                 for group in rows:
                     nc.vector.tensor_scalar(
-                        out=group["tops"][:, :, 3], in0=floor_ps[:, 0:1].to_broadcast([P, TILES]),
+                        out=group["tops"][:, :, 2], in0=floor_ps[:, 0:1].to_broadcast([P, TILES]),
                         scalar1=2.0, scalar2=-NEVER, op0=ALU.mult, op1=ALU.add,
                     )
-            if step == 1:
-                warm_up(2)
-            old = step - ahead
-            for side in plan.get(step - len(chunks) - 3, []):
-                side[0](*side[1:])
-            if 0 <= old < len(chunks):
-                chunk = chunks[old]
-                for c in range(chunk[2]):
-                    emit(chunk, c, c in on_scalar[old])
-                    if c == 0:
-                        if old >= 1:
-                            quantize_f(chunks[old - 1])
-                        if step < len(chunks):
-                            quantize_x(chunks[step])
-            elif step < len(chunks):
-                quantize_x(chunks[step])
-        quantize_f(chunks[-1])
+
+            pass
 
         home = {}
         for i in range(TILES):
-            home.setdefault(15 + i, []).append((0, i))
-            home.setdefault(20 + i, []).append((1, i))
-
-        def close(tile):
-            group, j = tile
-            divide(tile, "G" if group["own"] == GRID1 else "G")
-            if group["own"] == GRID1 or j < TILES - 1:
-                later(pen_bar, tile)
-
-        def pen_bar(tile):
-            group, j = tile
-            pen_of(group, j, j + 1)
-            if group["own"] == GRID0:
-                later(bar_of, group, j, j + 1)
-            elif j == TILES - 1:
-                later(column_bars, group)
-
-        def column_bars(group):
-            bar_of(group, 0, TILES)
-            bar1_all[group["n"]] = spread(group)
+            home.setdefault([15,16,17,18,19,20][i], []).append((0, i))
+            home.setdefault([21,22,23,24,25,26][i], []).append((1, i))
+        last = max(home) + 1
 
         def invert(tile):
+            group, j = tile
             inverse_of(tile)
-            close(tile)
+            divide(tile, "G")
 
-        def sum_up(tile):
-            total_of(tile)
-            later(invert, tile)
+        def penalise(tile):
+            group, j = tile
+            if group["own"] == GRID1 or j < TILES - 1:
+                pen_of(tile)
 
-        def exponentials(k):
-            shift_of(tiles[k])
-            exp_of(tiles[k])
-            if k >= 1:
-                later(sum_up, tiles[k - 1])
-            if k == len(tiles) - 1:
-                later(sum_up_last, k)
+        def finish(tile):
+            group, j = tile
+            if group["own"] == GRID0:
+                if j < TILES - 1:
+                    bar_of(group, j, j + 1)
+            elif j == TILES - 1:
+                bar_of(group, 0, TILES)
 
-        def sum_up_last(k):
-            later(sum_up, tiles[k])
+        def inner(tiles_home):
+            return [s for s in tiles_home if s[1] < TILES - 1]
 
-        dots_of(tiles[0])
-        for k in range(max(home) + 2):
+        dots_of(tiles[0], 0)
+        dots_of(tiles[1], 0)
+        take(tiles[0], 0)
+        for k in range(last + 1):
+            coming = home.get(k, [])
+            before = home.get(k - 1, [])
+            if k < len(tiles):
+                dots_of(tiles[k], 1)
+            if 0 <= k - 2 < len(tiles):
+                exp_of(tiles[k - 2])
+            if 0 <= k - 1 < len(tiles):
+                shift_of(tiles[k - 1])
+            if k >= 4 and k - 4 < len(tiles) and tiles[k - 4][1] == TILES - 1 and tiles[k - 4][0]["own"] == GRID1:
+                spread_copy(tiles[k - 4][0], 0)
+                spread_copy(tiles[k - 4][0], 1)
+            if 0 <= k - 3 < len(tiles):
+                penalise(tiles[k - 3])
             if k + 1 < len(tiles):
-                dots_of(tiles[k + 1])
+                large(take, tiles[k + 1], 0)
+            for s in coming:
+                if s in inner(coming):
+                    large(match_best, *s, 0)
+                    large(match_best, *s, 1)
+                home_copy(*s, 0)
+                home_copy(*s, 1)
+                store(1, *s, conf1_sb[s])
+            for s in inner(before):
+                large(match_kept, *s, 0)
+                large(match_kept, *s, 1)
+                match_final(*s, "V" if k == last - 1 else "G")
+            do_side(k, 0)
+            if k < len(tiles):
+                large(take, tiles[k], 1)
+            do_side(k, 3)
+            if 0 <= k - 2 < len(tiles):
+                invert(tiles[k - 2])
+            if 0 <= k - 3 < len(tiles):
+                finish(tiles[k - 3])
+            if k + 2 < len(tiles):
+                dots_of(tiles[k + 2], 0)
+            spreading = k >= 3 and k - 3 < len(tiles) and tiles[k - 3][1] == TILES - 1 and tiles[k - 3][0]["own"] == GRID1
+            if spreading:
+                spread(tiles[k - 3][0], 0)
+            for s in inner(coming):
+                match_dots(*s)
+            if spreading:
+                spread(tiles[k - 3][0], 1)
+            for s in home.get(k + 1, []):
+                home_turn(*s)
+            do_side(k, 1)
+            do_side(k, 2)
+            if pending and k >= len(tiles):
+                large(lambda: None)
             if k == 1:
                 for n in range(BATCH):
                     store(2, n, TILES - 1, zeros)
-            coming = home.get(k, [])
-            inner = [s for s in coming if s[1] < TILES - 1]
-            before = [s for s in home.get(k - 1, []) if s[1] < TILES - 1]
-            if k < len(tiles):
-                large(top_of, tiles[k], 0)
-                large(top_of, tiles[k], 1)
-                later(exponentials, k)
-            for s in coming:
-                home_turn(*s)
-            pass
-            for s in before:
-                large(match_kept, *s, 0)
-                large(match_kept, *s, 1)
-                match_final(*s, "G")
-            for s in inner:
-                match_dots(*s)
-                large(match_best, *s, 0)
-                large(match_best, *s, 1)
-            for s in coming:
-                home_copy(*s)
-            for side in plan.get(k, []):
-                side[0](*side[1:])
-            if k >= len(tiles):
-                large(lambda: None)
         while pending:
             large(lambda: None)

@@ -31,7 +31,7 @@ SPANS = ((0, BANK), (BANK, CELLS))
 INNER_SPANS = ((EDGE, EDGE + BANK), (EDGE + BANK, CELLS - EDGE))
 GRID1 = 0
 GRID0 = CELLS
-MCONF_TILES = 5
+MCONF_TILES = 4
 INV_SQRT_C = 1.0 / (C ** 0.5)
 INV_TEMPERATURE = 10.0
 THRESHOLD = 0.2
@@ -53,7 +53,7 @@ def tile_coarsematching_kernel(
     with ExitStack() as ctx:
         const = ctx.enter_context(tc.tile_pool(name="const", bufs=1))
         keep = ctx.enter_context(tc.tile_pool(name="keep", bufs=1))
-        stage = ctx.enter_context(tc.tile_pool(name="stage", bufs=3))
+        stage = ctx.enter_context(tc.tile_pool(name="stage", bufs=2))
         mask = ctx.enter_context(tc.tile_pool(name="mask", bufs=3))
         exps = ctx.enter_context(tc.tile_pool(name="exps", bufs=12))
         quot = ctx.enter_context(tc.tile_pool(name="quot", bufs=4))
@@ -133,15 +133,12 @@ def tile_coarsematching_kernel(
             return one_bank
 
         x_grouped = {}
+        x_banks = {}
         f_banks = {}
         f_grouped = {}
 
         def turn(chunk, pair):
             n, first, count = chunk
-            if pair == 0:
-                x_grouped[chunk] = stage.tile(
-                    [P, count * P * PACK], BF16, align_bytes=64, tag="xg%d" % count, name="xg"
-                )
             x_t = bank()
             for c in range(2):
                 words = x_sb[n][:, first + 2 * pair + c, :].bitcast(F32)
@@ -149,10 +146,18 @@ def tile_coarsematching_kernel(
                     nc.tensor.transpose(
                         x_t[:, u * PAIR + c * P:u * PAIR + (c + 1) * P], words[:, u:C // 2:2], ident[:]
                     )
+            x_banks[chunk, pair] = x_t
+
+        def turn_copy(chunk, pair):
+            n, first, count = chunk
+            if pair == 0:
+                x_grouped[chunk] = stage.tile(
+                    [P, count * P * PACK], BF16, align_bytes=64, tag="xg%d" % count, name="xg"
+                )
             nc.scalar.copy(
                 out=x_grouped[chunk][:, pair * PAIR * PACK:(pair + 1) * PAIR * PACK]
                 .bitcast(F32).rearrange("p (r u) -> p r u", u=2),
-                in_=x_t[:].rearrange("p (u r) -> p r u", u=2),
+                in_=x_banks[chunk, pair][:].rearrange("p (u r) -> p r u", u=2),
             )
 
         def quantize_x(chunk):
@@ -207,6 +212,42 @@ def tile_coarsematching_kernel(
                 scalar1=1.0, scalar2=0.0, op0=ALU.mult, op1=ALU.add,
             )
 
+        planes = {}
+
+        def project_plane(chunk, t):
+            n, first, count = chunk
+            cells = slice(first * P, (first + count) * P)
+            acc = bank()
+            nc.tensor.matmul_mx(
+                out=acc[:],
+                lhsT=w_words[:, t * P:(t + 1) * P].bitcast(FP8X4),
+                lhsT_scale=w_plane[:, t * P:(t + 1) * P],
+                rhs=x_codes[n][:, cells].bitcast(FP8X4),
+                rhs_scale=x_plane[n][:, cells],
+                start=True,
+                stop=True,
+            )
+            f_banks[chunk, t] = acc
+
+        def plane_out(chunk, t):
+            if t == 0:
+                planes[chunk] = stage.tile([P, PACK, BANK], BF16, align_bytes=64, tag="planes", name="planes", bufs=1)
+            nc.scalar.activation(
+                out=planes[chunk][:, t, :], in_=f_banks[chunk, t][:], func=FUNC.Identity,
+                scale=INV_SQRT_C, bias=bias4[:, t:t + 1],
+            )
+
+        def group_planes(chunk, part):
+            if part == 0:
+                f_grouped[chunk] = stage.tile(
+                    [P, chunk[2] * P, PACK], BF16, align_bytes=64, tag="fg%d" % chunk[2], name="fg"
+                )
+            lo, hi = part * (BANK // 2), (part + 1) * (BANK // 2)
+            nc.gpsimd.tensor_scalar(
+                out=f_grouped[chunk][:, lo:hi, :], in0=planes[chunk][:, :, lo:hi].rearrange("p t r -> p r t"),
+                scalar1=1.0, scalar2=0.0, op0=ALU.mult, op1=ALU.add,
+            )
+
         def quantize_f(chunk):
             n, first, count = chunk
             cells = slice(first * P, (first + count) * P)
@@ -236,8 +277,8 @@ def tile_coarsematching_kernel(
                 "n": n,
                 "own": own,
                 "other": other,
-                "tops": keep.tile([P, TILES, 3], F32, name="tops_" + label),
-                "part": keep.tile([P, TILES], F32, name="part_" + label),
+                "tops": keep.tile([P, TILES, 4], F32, name="tops_" + label),
+                "sums": keep.tile([P, TILES, 2], F32, name="sums_" + label),
                 "shift": keep.tile([P, TILES], F32, name="shift_" + label),
                 "total": keep.tile([P, TILES], F32, name="total_" + label),
                 "inv": keep.tile([P, TILES], F32, name="inv_" + label),
@@ -246,42 +287,43 @@ def tile_coarsematching_kernel(
             }
             return group
 
-        def dots_of(tile, k):
+        def dots_of(tile):
             group, j = tile
-            group[j, k] = dot_banks(group["n"], group["own"], group["other"], j, SPANS[k:k + 1])[0]
+            group["dots", j] = dot_banks(group["n"], group["own"], group["other"], j, SPANS)
 
-        def take(tile, k):
+        def top_of(tile, k):
             group, j = tile
-            if k == 0:
-                if group["own"] == GRID0:
-                    e = exps.tile([P, CELLS], F32, tag="e", name="e")
-                else:
-                    e = keep.tile([P, CELLS], F32, name="col_%d_%d" % (group["n"], j))
-                group["e"][j] = e
-            lo, hi = SPANS[k]
-            nc.vector.tensor_scalar(
-                out=group["e"][j][:, lo:hi], in0=group[j, k], scalar1=1.0,
-                scalar2=None if k == 0 else group["part"][:, j:j + 1], op0=ALU.mult, op1=ALU.max,
-                accum_out=group["part"][:, j:j + 1] if k == 0 else group["tops"][:, j, 0:1],
-            )
+            nc.vector.reduce_max(out=group["tops"][:, j, k:k + 1], in_=group["dots", j][k], axis=AXIS.X)
 
         def shift_of(tile):
             group, j = tile
-            nc.scalar.activation(
-                out=group["shift"][:, j:j + 1], in_=group["tops"][:, j, 0:1], func=FUNC.Copy, scale=-INV_TEMPERATURE
+            nc.vector.tensor_scalar(
+                out=group["shift"][:, j:j + 1], in0=group["tops"][:, j, 0:1],
+                scalar1=group["tops"][:, j, 1:2], scalar2=-INV_TEMPERATURE, op0=ALU.max, op1=ALU.mult,
             )
 
         def exp_of(tile):
             group, j = tile
-            e = group["e"][j]
-            nc.scalar.activation(
-                out=e[:], in_=e[:], func=FUNC.Exp, bias=group["shift"][:, j:j + 1], scale=INV_TEMPERATURE,
-                accum_out=group["total"][:, j:j + 1],
+            if group["own"] == GRID0:
+                e = exps.tile([P, CELLS], F32, tag="e", name="e")
+            else:
+                e = keep.tile([P, CELLS], F32, name="col_%d_%d" % (group["n"], j))
+            group["e"][j] = e
+            for k in range(2):
+                lo, hi = SPANS[k]
+                nc.scalar.activation(
+                    out=e[:, lo:hi], in_=group["dots", j][k], func=FUNC.Exp,
+                    bias=group["shift"][:, j:j + 1], scale=INV_TEMPERATURE,
+                    accum_out=group["sums"][:, j, k:k + 1],
+                )
+
+        def total_of(group, first, last):
+            nc.vector.tensor_reduce(
+                out=group["total"][:, first:last], in_=group["sums"][:, first:last, :], axis=AXIS.X, op=ALU.add
             )
 
-        def inverse_of(tile):
-            group, j = tile
-            nc.vector.reciprocal(out=group["inv"][:, j:j + 1], in_=group["total"][:, j:j + 1])
+        def inverse_of(group, first, last):
+            nc.vector.reciprocal(out=group["inv"][:, first:last], in_=group["total"][:, first:last])
 
         def divide(tile, engine):
             group, j = tile
@@ -301,15 +343,14 @@ def tile_coarsematching_kernel(
             if group["own"] == GRID0:
                 store(0, group["n"], j, conf)
 
-        def pen_of(tile):
-            group, j = tile
+        def pen_of(group, first, last):
             nc.scalar.activation(
-                out=group["tops"][:, j, 1:2], in_=group["inv"][:, j:j + 1], func=FUNC.Copy,
+                out=group["tops"][:, first:last, 2], in_=group["inv"][:, first:last], func=FUNC.Copy,
                 scale=-NEVER, bias=THRESHOLD * NEVER,
             )
 
         def bar_of(group, first, last):
-            cols = 3 if group["own"] == GRID0 else 2
+            cols = 4 if group["own"] == GRID0 else 3
             nc.vector.tensor_reduce(
                 out=group["bar"][:, first:last], in_=group["tops"][:, first:last, 0:cols], axis=AXIS.X, op=ALU.max
             )
@@ -360,7 +401,7 @@ def tile_coarsematching_kernel(
         def home_copy(n, i, k):
             lo, hi = HALVES[k]
             if (n, i) not in conf1_sb:
-                conf1_sb[n, i] = quot.tile([P, CELLS], F32, tag="conf1", name="conf1")
+                conf1_sb[n, i] = quot.tile([P, CELLS], F32, tag="conf1", name="conf1", bufs=4)
             nc.scalar.copy(out=conf1_sb[n, i][:, lo:hi], in_=home_banks[n, i][k])
 
         def match_dots(n, i):
@@ -446,8 +487,9 @@ def tile_coarsematching_kernel(
         for p in range(6):
             chunk = (0, 2 * p, 2)
             r = p - 7
-            share = [0, 1, 1, 0, 0, 1][p]
+            share = [0, 0, 1, 0, 0, 0][p]
             side(r, 1, turn, chunk, 0)
+            side(r, 1, turn_copy, chunk, 0)
             if p < 2:
                 side(r, 1, warm_up, 2)
             elif p < 5:
@@ -462,13 +504,30 @@ def tile_coarsematching_kernel(
             r = [-2,1,4][q]
             for pair in range(2):
                 side(r + pair, 1, turn, chunk, pair)
+                if r + pair + 1 >= 0:
+                    side(r + pair + 1, 6, turn_copy, chunk, pair)
+                else:
+                    side(r + pair, 1, turn_copy, chunk, pair)
             side(r + 2, 3 if r + 2 >= 0 else 0, large, quantize_x, chunk)
+            if q in [0]:
+                for c in range(4):
+                    side(r + 2 + c // 2, 1, project_plane, chunk, c)
+                    side(r + 3 + c // 2, 6, plane_out, chunk, c)
+                for c in range(2):
+                    side(r + 4 + (c * 2) // 2, 5, group_planes, chunk, c)
+                side(r + 6, 3, large, quantize_f, chunk)
+                continue
             for c in range(4):
                 side(r + 2 + c // 2, 1, project, chunk, c)
-                side(r + 3 + c // 2, 0, emit_out, chunk, c, c % 2 == 1)
+                if c == 1:
+                    side(r + 3 + c // 2, 6 if r + 3 + c // 2 >= 0 else 0, emit_out, chunk, c, True)
+                else:
+                    side(r + 3 + c // 2, 0, emit_out, chunk, c, False)
             side(r + 6, 3, large, quantize_f, chunk)
         for r in range(-7, 0):
             do_side(r, 0)
+            do_side(r, 4)
+            do_side(r, 5)
             do_side(r, 1)
             do_side(r, 2)
             if r == -7:
@@ -484,7 +543,7 @@ def tile_coarsematching_kernel(
                 nc.vector.tensor_copy(out=floor_row[:], in_=floor_ps[:, 0:1])
                 for group in rows:
                     nc.vector.tensor_scalar(
-                        out=group["tops"][:, :, 2], in0=floor_ps[:, 0:1].to_broadcast([P, TILES]),
+                        out=group["tops"][:, :, 3], in0=floor_ps[:, 0:1].to_broadcast([P, TILES]),
                         scalar1=2.0, scalar2=-NEVER, op0=ALU.mult, op1=ALU.add,
                     )
 
@@ -496,80 +555,83 @@ def tile_coarsematching_kernel(
             home.setdefault([21,22,23,24,25,26][i], []).append((1, i))
         last = max(home) + 1
 
-        def invert(tile):
+        def divider(tile):
             group, j = tile
-            inverse_of(tile)
-            divide(tile, "G")
+            return "G"
 
-        def penalise(tile):
-            group, j = tile
-            if group["own"] == GRID1 or j < TILES - 1:
-                pen_of(tile)
+        batches = {}
+        for k, (group, j) in enumerate(tiles):
+            ends = (1, 3, 5) if group["own"] == GRID1 else ((2, 5) if group["n"] == 0 else (1, 3, 5))
+            if j in ends:
+                place = ends.index(j)
+                batches.setdefault(k + (1 if k >= 18 else 2), []).append((group, ends[place - 1] + 1 if place else 0, j + 1))
+        division = {}
+        for r, group, first, end in [(r,) + batch for r, some in batches.items() for batch in some]:
+            for j in range(first, end):
+                division.setdefault(r if first == 4 or group['own'] == GRID1 else r + j - first, []).append((group, j))
+        divided = []
 
-        def finish(tile):
-            group, j = tile
-            if group["own"] == GRID0:
-                if j < TILES - 1:
-                    bar_of(group, j, j + 1)
-            elif j == TILES - 1:
-                bar_of(group, 0, TILES)
+        def exponentials(k):
+            shift_of(tiles[k])
+            exp_of(tiles[k])
 
         def inner(tiles_home):
             return [s for s in tiles_home if s[1] < TILES - 1]
 
-        dots_of(tiles[0], 0)
-        dots_of(tiles[1], 0)
-        take(tiles[0], 0)
+        dots_of(tiles[0])
         for k in range(last + 1):
+            do_side(k, 6)
             coming = home.get(k, [])
             before = home.get(k - 1, [])
-            if k < len(tiles):
-                dots_of(tiles[k], 1)
-            if 0 <= k - 2 < len(tiles):
-                exp_of(tiles[k - 2])
-            if 0 <= k - 1 < len(tiles):
-                shift_of(tiles[k - 1])
-            if k >= 4 and k - 4 < len(tiles) and tiles[k - 4][1] == TILES - 1 and tiles[k - 4][0]["own"] == GRID1:
-                spread_copy(tiles[k - 4][0], 0)
-                spread_copy(tiles[k - 4][0], 1)
-            if 0 <= k - 3 < len(tiles):
-                penalise(tiles[k - 3])
             if k + 1 < len(tiles):
-                large(take, tiles[k + 1], 0)
-            for s in coming:
-                if s in inner(coming):
-                    large(match_best, *s, 0)
-                    large(match_best, *s, 1)
-                home_copy(*s, 0)
-                home_copy(*s, 1)
-                store(1, *s, conf1_sb[s])
+                dots_of(tiles[k + 1])
+            for group, first, end in batches.get(k - 2, []):
+                if group["own"] == GRID1 and end == TILES:
+                    spread_copy(group, 0)
+                    spread_copy(group, 1)
+            for group, first, end in batches.get(k - 1, []):
+                pen_of(group, first, end)
+            if k < len(tiles):
+                large(top_of, tiles[k], 1)
+                large(top_of, tiles[k], 0)
+                later(exponentials, k)
+            for batch in batches.get(k, []):
+                total_of(*batch)
+            pass
             for s in inner(before):
                 large(match_kept, *s, 0)
                 large(match_kept, *s, 1)
                 match_final(*s, "V" if k == last - 1 else "G")
+            for s in inner(coming):
+                large(match_best, *s, 0)
+                large(match_best, *s, 1)
+            for s in coming:
+                home_copy(*s, 0)
+                home_copy(*s, 1)
+                store(1, *s, conf1_sb[s])
             do_side(k, 0)
-            if k < len(tiles):
-                large(take, tiles[k], 1)
+            do_side(k, 4)
+            do_side(k, 5)
             do_side(k, 3)
-            if 0 <= k - 2 < len(tiles):
-                invert(tiles[k - 2])
-            if 0 <= k - 3 < len(tiles):
-                finish(tiles[k - 3])
-            if k + 2 < len(tiles):
-                dots_of(tiles[k + 2], 0)
-            spreading = k >= 3 and k - 3 < len(tiles) and tiles[k - 3][1] == TILES - 1 and tiles[k - 3][0]["own"] == GRID1
-            if spreading:
-                spread(tiles[k - 3][0], 0)
+            for batch in batches.get(k, []):
+                inverse_of(*batch)
+            for tile in division.get(k, []):
+                divide(tile, divider(tile))
+                divided.append(tile)
+            for group, first, end in batches.get(k - 1, []):
+                bar_of(group, first, end)
+            spreading = [batch[0] for batch in batches.get(k - 1, []) if batch[0]["own"] == GRID1 and batch[2] == TILES]
+            for group in spreading:
+                spread(group, 0)
             for s in inner(coming):
                 match_dots(*s)
-            if spreading:
-                spread(tiles[k - 3][0], 1)
+            for group in spreading:
+                spread(group, 1)
             for s in home.get(k + 1, []):
+                assert all((columns[s[0]], j) in divided for j in range(TILES))
                 home_turn(*s)
             do_side(k, 1)
             do_side(k, 2)
-            if pending and k >= len(tiles):
-                large(lambda: None)
             if k == 1:
                 for n in range(BATCH):
                     store(2, n, TILES - 1, zeros)

@@ -498,7 +498,7 @@ def tile_coarsematching_kernel(
             for c in range(2):
                 side(r + 2, 1, project, chunk, c)
                 side(r + 2 if r < -2 else r + 3, 2 if r < -2 else 0, emit_out, chunk, c, share and c == 1)
-            side(r + (4 if share else 3), 0, large, quantize_f, chunk)
+            side(r + (4 if share else 3), 7, large, quantize_f, chunk)
         for q in range(3):
             chunk = (1, 4 * q, 4)
             r = [-2,1,4][q]
@@ -526,6 +526,7 @@ def tile_coarsematching_kernel(
             side(r + 6, 3, large, quantize_f, chunk)
         for r in range(-7, 0):
             do_side(r, 0)
+            do_side(r, 7)
             do_side(r, 4)
             do_side(r, 5)
             do_side(r, 1)
@@ -557,7 +558,7 @@ def tile_coarsematching_kernel(
 
         def divider(tile):
             group, j = tile
-            return "G"
+            return "S" if group["own"] == GRID0 and group["n"] == 1 and j >= 4 else "G"
 
         batches = {}
         for k, (group, j) in enumerate(tiles):
@@ -610,6 +611,7 @@ def tile_coarsematching_kernel(
                 home_copy(*s, 1)
                 store(1, *s, conf1_sb[s])
             do_side(k, 0)
+            do_side(k, 7)
             do_side(k, 4)
             do_side(k, 5)
             do_side(k, 3)

@@ -35,6 +35,7 @@ MCONF_TILES = 4
 INV_SQRT_C = 1.0 / (C ** 0.5)
 INV_TEMPERATURE = 10.0
 THRESHOLD = 0.2
+HUGE = 1.0e35
 NEVER = 1.0e38
 
 FLOPS = 2 * (2 * BATCH * CELLS) * C * C + 2 * BATCH * CELLS * CELLS * C
@@ -345,8 +346,8 @@ def tile_coarsematching_kernel(
 
         def pen_of(group, first, last):
             nc.scalar.activation(
-                out=group["tops"][:, first:last, 2], in_=group["inv"][:, first:last], func=FUNC.Copy,
-                scale=-NEVER, bias=THRESHOLD * NEVER,
+                out=group["tops"][:, first:last, 2], in_=group["total"][:, first:last], func=FUNC.Copy,
+                scale=HUGE, bias=-HUGE / THRESHOLD,
             )
 
         def bar_of(group, first, last):
@@ -558,7 +559,7 @@ def tile_coarsematching_kernel(
 
         def divider(tile):
             group, j = tile
-            return "S" if group["own"] == GRID0 and group["n"] == 1 and j >= 4 else "G"
+            return "S" if (group["own"] == GRID0 and group["n"] == 1 and j >= 4) or (group["own"] == GRID1 and j == TILES - 1) else "G"
 
         batches = {}
         for k, (group, j) in enumerate(tiles):
@@ -590,14 +591,13 @@ def tile_coarsematching_kernel(
                 if group["own"] == GRID1 and end == TILES:
                     spread_copy(group, 0)
                     spread_copy(group, 1)
-            for group, first, end in batches.get(k - 1, []):
-                pen_of(group, first, end)
             if k < len(tiles):
                 large(top_of, tiles[k], 1)
                 large(top_of, tiles[k], 0)
                 later(exponentials, k)
             for batch in batches.get(k, []):
                 total_of(*batch)
+                pen_of(*batch)
             pass
             for s in inner(before):
                 large(match_kept, *s, 0)

from contextlib import ExitStack

import concourse.mybir as mybir
from concourse.masks import make_identity

F32 = mybir.dt.float32
BF16 = mybir.dt.bfloat16
U8 = mybir.dt.uint8
U32 = mybir.dt.uint32
I32 = mybir.dt.int32
FP8X4 = mybir.dt.float8_e4m3fn_x4
ALU = mybir.AluOpType
FUNC = mybir.ActivationFunctionType
AXIS = mybir.AxisListType

P = 128
PACK = 4
C = P * PACK
BATCH = 2
CELLS = 768
TILES = CELLS // P
QUAD = 4 * P
QUADS = 2 * CELLS // QUAD
GRID_W = 32
BORDER = 2
EDGE = BORDER * GRID_W
INNER_ROWS = CELLS // GRID_W - 2 * BORDER
INNER_COLS = GRID_W - 2 * BORDER
BANK = 512
SPANS = ((0, BANK), (BANK, CELLS))
INNER_SPANS = ((EDGE, EDGE + BANK), (EDGE + BANK, CELLS - EDGE))
GRID1 = 0
GRID0 = CELLS
MCONF_TILES = 4
INV_SQRT_C = 1.0 / (C ** 0.5)
INV_TEMPERATURE = 10.0
THRESHOLD = 0.2
HUGE = 1.0e35
NEVER = 1.0e38

FLOPS = 2 * (2 * BATCH * CELLS) * C * C + 2 * BATCH * CELLS * CELLS * C
HALVES = ((0, CELLS // 2), (CELLS // 2, CELLS))
PAIR = 2 * P


def inner_cells(cells):
    return cells.rearrange("p (g c) -> p g c", c=GRID_W)[:, :, BORDER:GRID_W - BORDER]


def tile_coarsematching_kernel(
    tc, feat_c0, feat_c1, W_words, W_scales, b, h0c, w0c, h1c, w1c, out
):
    nc = tc.nc
    with ExitStack() as ctx:
        const = ctx.enter_context(tc.tile_pool(name="const", bufs=1))
        keep = ctx.enter_context(tc.tile_pool(name="keep", bufs=1))
        stage = ctx.enter_context(tc.tile_pool(name="stage", bufs=2))
        mask = ctx.enter_context(tc.tile_pool(name="mask", bufs=3))
        exps = ctx.enter_context(tc.tile_pool(name="exps", bufs=12))
        quot = ctx.enter_context(tc.tile_pool(name="quot", bufs=4))
        psum = ctx.enter_context(tc.psum_pool(name="psum", bufs=8))
        ctx.enter_context(tc.manual_schedule())

        idle = const.tile([P, BANK], BF16)
        nc.vector.memset(idle[:], 0.0)
        w_plane = const.tile([P, C], U8, align_bytes=64)
        nc.vector.memset(w_plane[:].bitcast(I32), 0)
        bias_rows = const.tile([P, P], BF16)
        nc.vector.memset(bias_rows[:], 0.0)
        w_words = const.tile([P, C], U32, align_bytes=64)
        x_sb = [keep.tile([P, 2 * TILES, C], BF16, name="x_%d" % n) for n in range(BATCH)]

        def load_cells(n, first, last):
            mid = min(max(first, TILES), last)
            if first < mid:
                nc.sync.dma_start(
                    out=x_sb[n][:, first:mid, :],
                    in_=feat_c1[n, first * P:mid * P, :].rearrange("(j p) k -> p j k", p=P),
                )
            if mid < last:
                lo = EDGE + (mid - TILES) * P
                nc.sync.dma_start(
                    out=x_sb[n][:, mid:last, :],
                    in_=feat_c0[n, lo:lo + (last - mid) * P, :].rearrange("(j p) k -> p j k", p=P),
                )

        def load_border(n):
            nc.sync.dma_start(out=x_sb[n][0:EDGE, 2 * TILES - 1, :], in_=feat_c0[n, CELLS - EDGE:CELLS, :])
            nc.sync.dma_start(out=x_sb[n][EDGE:P, 2 * TILES - 1, :], in_=feat_c0[n, 0:EDGE, :])

        load_cells(0, 0, 2)
        load_cells(0, 2, 4)
        nc.sync.dma_start(
            out=w_words[:].bitcast(I32), in_=W_words[0].rearrange("p n t -> p (n t)").bitcast(I32)
        )
        for quadrant in range(4):
            nc.sync.dma_start(
                out=w_plane[32 * quadrant:32 * quadrant + 4, :].bitcast(I32),
                in_=W_scales[0, 4 * quadrant:4 * quadrant + 4, :].bitcast(I32),
            )
        nc.sync.dma_start(out=bias_rows[0:PACK, :], in_=b.rearrange("(t p) -> t p", p=P))
        load_cells(0, 4, 8)
        load_cells(0, 8, 11)
        load_border(0)
        for q in range(QUADS):
            load_cells(1, 4 * q, min(4 * q + 4, 2 * TILES - 1))
        load_border(1)

        ident = const.tile([P, P], F32)
        make_identity(nc, ident[:])
        ident_bf = const.tile([P, P], BF16)
        make_identity(nc, ident_bf[:])
        zeros = const.tile([P, CELLS], F32)
        nc.gpsimd.memset(zeros[:], 0.0)
        mconf_tiles = []
        for slot in range(MCONF_TILES):
            mconf_sb = const.tile([P, CELLS], F32, name="mconf_%d" % slot)
            nc.gpsimd.memset(mconf_sb[:], 0.0)
            mconf_tiles.append(mconf_sb)
        warm = const.tile([P, 1], F32)
        nc.vector.memset(warm[:], 0.0)
        nc.scalar.activation(out=warm[:], in_=warm[:], func=FUNC.Exp)
        floor_free = const.tile([P, P], F32)
        nc.vector.memset(floor_free[:], NEVER)
        nc.vector.memset(inner_cells(floor_free[:]), 0.0)

        x_codes = [keep.tile([P, 2 * CELLS], U32, align_bytes=64, name="xc_%d" % n) for n in range(BATCH)]
        x_plane = [keep.tile([P, 2 * CELLS], U8, align_bytes=64, name="xp_%d" % n) for n in range(BATCH)]
        f_codes = [keep.tile([P, 2 * CELLS], U32, align_bytes=64, name="fc_%d" % n) for n in range(BATCH)]
        f_plane = [keep.tile([P, 2 * CELLS], U8, align_bytes=64, name="fp_%d" % n) for n in range(BATCH)]

        def bank():
            one_bank = psum.tile([P, BANK], F32, tag="bank", name="one_bank")
            return one_bank

        x_grouped = {}
        x_banks = {}
        f_banks = {}
        f_grouped = {}

        def turn(chunk, pair):
            n, first, count = chunk
            x_t = bank()
            for c in range(2):
                words = x_sb[n][:, first + 2 * pair + c, :].bitcast(F32)
                for u in range(2):
                    nc.tensor.transpose(
                        x_t[:, u * PAIR + c * P:u * PAIR + (c + 1) * P], words[:, u:C // 2:2], ident[:]
                    )
            x_banks[chunk, pair] = x_t

        def turn_copy(chunk, pair):
            n, first, count = chunk
            if pair == 0:
                x_grouped[chunk] = stage.tile(
                    [P, count * P * PACK], BF16, align_bytes=64, tag="xg%d" % count, name="xg"
                )
            nc.scalar.copy(
                out=x_grouped[chunk][:, pair * PAIR * PACK:(pair + 1) * PAIR * PACK]
                .bitcast(F32).rearrange("p (r u) -> p r u", u=2),
                in_=x_banks[chunk, pair][:].rearrange("p (u r) -> p r u", u=2),
            )

        def quantize_x(chunk):
            n, first, count = chunk
            cells = slice(first * P, (first + count) * P)
            nc.vector.quantize_mx(
                out=x_codes[n][:, cells].bitcast(FP8X4), scales=x_plane[n][:, cells], in_=x_grouped[chunk][:]
            )

        def project(chunk, c):
            n, first, count = chunk
            cells = slice((first + c) * P, (first + c + 1) * P)
            acc = bank()
            for t in range(PACK):
                nc.tensor.matmul_mx(
                    out=acc[:, t * P:(t + 1) * P],
                    lhsT=w_words[:, t * P:(t + 1) * P].bitcast(FP8X4),
                    lhsT_scale=w_plane[:, t * P:(t + 1) * P],
                    rhs=x_codes[n][:, cells].bitcast(FP8X4),
                    rhs_scale=x_plane[n][:, cells],
                    start=True,
                    stop=True,
                )
            f_banks[chunk, c] = acc

        def f_target(chunk, c):
            if chunk not in f_grouped:
                f_grouped[chunk] = stage.tile(
                    [P, chunk[2] * P, PACK], BF16, align_bytes=64, tag="fg%d" % chunk[2], name="fg"
                )
            return f_grouped[chunk][:, c * P:(c + 1) * P, :]

        def emit_on_vector(chunk, c):
            nc.vector.scalar_tensor_tensor(
                out=f_target(chunk, c),
                in0=f_banks[chunk, c][:].rearrange("p (t r) -> p r t", t=PACK),
                scalar=INV_SQRT_C,
                in1=bias4[:].unsqueeze(1).to_broadcast([P, P, PACK]),
                op0=ALU.mult,
                op1=ALU.add,
            )

        def emit_on_scalar(chunk, c):
            rows4 = stage.tile([P, PACK, P], BF16, tag="rows4", name="rows4")
            for t in range(PACK):
                nc.scalar.activation(
                    out=rows4[:, t, :], in_=f_banks[chunk, c][:, t * P:(t + 1) * P], func=FUNC.Identity,
                    scale=INV_SQRT_C, bias=bias4[:, t:t + 1],
                )
            nc.gpsimd.tensor_scalar(
                out=f_target(chunk, c), in0=rows4[:].rearrange("p t r -> p r t"),
                scalar1=1.0, scalar2=0.0, op0=ALU.mult, op1=ALU.add,
            )

        planes = {}

        def project_plane(chunk, t):
            n, first, count = chunk
            cells = slice(first * P, (first + count) * P)
            acc = bank()
            nc.tensor.matmul_mx(
                out=acc[:],
                lhsT=w_words[:, t * P:(t + 1) * P].bitcast(FP8X4),
                lhsT_scale=w_plane[:, t * P:(t + 1) * P],
                rhs=x_codes[n][:, cells].bitcast(FP8X4),
                rhs_scale=x_plane[n][:, cells],
                start=True,
                stop=True,
            )
            f_banks[chunk, t] = acc

        def plane_out(chunk, t):
            if t == 0:
                planes[chunk] = stage.tile([P, PACK, BANK], BF16, align_bytes=64, tag="planes", name="planes", bufs=1)
            nc.scalar.activation(
                out=planes[chunk][:, t, :], in_=f_banks[chunk, t][:], func=FUNC.Identity,
                scale=INV_SQRT_C, bias=bias4[:, t:t + 1],
            )

        def group_planes(chunk, part):
            if part == 0:
                f_grouped[chunk] = stage.tile(
                    [P, chunk[2] * P, PACK], BF16, align_bytes=64, tag="fg%d" % chunk[2], name="fg"
                )
            lo, hi = part * (BANK // 2), (part + 1) * (BANK // 2)
            nc.gpsimd.tensor_scalar(
                out=f_grouped[chunk][:, lo:hi, :], in0=planes[chunk][:, :, lo:hi].rearrange("p t r -> p r t"),
                scalar1=1.0, scalar2=0.0, op0=ALU.mult, op1=ALU.add,
            )

        def quantize_f(chunk):
            n, first, count = chunk
            cells = slice(first * P, (first + count) * P)
            nc.vector.quantize_mx(
                out=f_codes[n][:, cells].bitcast(FP8X4), scales=f_plane[n][:, cells],
                in_=f_grouped[chunk][:].rearrange("p r t -> p (r t)"),
            )

        def dot_banks(n, own, other, j, spans):
            banks = []
            for lo, hi in spans:
                dots = bank()
                nc.tensor.matmul_mx(
                    out=dots[:, 0:hi - lo],
                    lhsT=f_codes[n][:, own + j * P:own + (j + 1) * P].bitcast(FP8X4),
                    lhsT_scale=f_plane[n][:, own + j * P:own + (j + 1) * P],
                    rhs=f_codes[n][:, other + lo:other + hi].bitcast(FP8X4),
                    rhs_scale=f_plane[n][:, other + lo:other + hi],
                    start=True,
                    stop=True,
                )
                banks.append(dots[:, 0:hi - lo])
            return banks

        def open_softmax(n, own, other, label):
            group = {
                "n": n,
                "own": own,
                "other": other,
                "tops": keep.tile([P, TILES, 4], F32, name="tops_" + label),
                "sums": keep.tile([P, TILES, 2], F32, name="sums_" + label),
                "shift": keep.tile([P, TILES], F32, name="shift_" + label),
                "total": keep.tile([P, TILES], F32, name="total_" + label),
                "inv": keep.tile([P, TILES], F32, name="inv_" + label),
                "bar": keep.tile([P, TILES], F32, name="bar_" + label),
                "e": {},
            }
            return group

        def dots_of(tile):
            group, j = tile
            group["dots", j] = dot_banks(group["n"], group["own"], group["other"], j, SPANS)

        def top_of(tile, k):
            group, j = tile
            nc.vector.reduce_max(out=group["tops"][:, j, k:k + 1], in_=group["dots", j][k], axis=AXIS.X)

        def shift_of(tile):
            group, j = tile
            nc.vector.tensor_scalar(
                out=group["shift"][:, j:j + 1], in0=group["tops"][:, j, 0:1],
                scalar1=group["tops"][:, j, 1:2], scalar2=-INV_TEMPERATURE, op0=ALU.max, op1=ALU.mult,
            )

        def exp_of(tile):
            group, j = tile
            if group["own"] == GRID0:
                e = exps.tile([P, CELLS], F32, tag="e", name="e")
            else:
                e = keep.tile([P, CELLS], F32, name="col_%d_%d" % (group["n"], j))
            group["e"][j] = e
            for k in range(2):
                lo, hi = SPANS[k]
                nc.scalar.activation(
                    out=e[:, lo:hi], in_=group["dots", j][k], func=FUNC.Exp,
                    bias=group["shift"][:, j:j + 1], scale=INV_TEMPERATURE,
                    accum_out=group["sums"][:, j, k:k + 1],
                )

        def total_of(group, first, last):
            nc.vector.tensor_reduce(
                out=group["total"][:, first:last], in_=group["sums"][:, first:last, :], axis=AXIS.X, op=ALU.add
            )

        def inverse_of(group, first, last):
            nc.vector.reciprocal(out=group["inv"][:, first:last], in_=group["total"][:, first:last])

        def divide(tile, engine):
            group, j = tile
            e = group["e"][j]
            conf = e
            if group["own"] == GRID0:
                conf = quot.tile([P, CELLS], F32, tag="conf0", name="conf0")
            inv = group["inv"][:, j:j + 1]
            if engine == "G":
                nc.gpsimd.tensor_scalar(
                    out=conf[:], in0=e[:], scalar1=inv, scalar2=0.0, op0=ALU.mult, op1=ALU.add
                )
            elif engine == "V":
                nc.vector.tensor_scalar(out=conf[:], in0=e[:], scalar1=inv, scalar2=None, op0=ALU.mult)
            else:
                nc.scalar.activation(out=conf[:], in_=e[:], func=FUNC.Copy, scale=inv)
            if group["own"] == GRID0:
                store(0, group["n"], j, conf)

        def pen_of(group, first, last):
            nc.scalar.activation(
                out=group["tops"][:, first:last, 2], in_=group["total"][:, first:last], func=FUNC.Copy,
                scale=HUGE, bias=-HUGE / THRESHOLD,
            )

        def bar_of(group, first, last):
            cols = 4 if group["own"] == GRID0 else 3
            nc.vector.tensor_reduce(
                out=group["bar"][:, first:last], in_=group["tops"][:, first:last, 0:cols], axis=AXIS.X, op=ALU.max
            )

        def spread(group, k):
            lo, hi = SPANS[k]
            ps = bank()
            for j in range(lo // P, hi // P):
                nc.tensor.transpose(
                    ps[:, j * P - lo:(j + 1) * P - lo], group["bar"][:, j:j + 1].to_broadcast([P, P]), ident[:]
                )
            group["spread", k] = ps

        def spread_copy(group, k):
            n = group["n"]
            if k == 0:
                bar1_all[n] = keep.tile([P, CELLS], F32, name="barall_%d" % n)
            lo, hi = SPANS[k]
            nc.scalar.activation(
                out=bar1_all[n][:, lo:hi], in_=group["spread", k][:, 0:hi - lo], func=FUNC.Identity,
                bias=floor_row[:, 0:1], scale=1.0,
            )

        def store(plane, n, i, rows_sb):
            if i < TILES - 1:
                nc.sync.dma_start(out=out[plane, n, EDGE + i * P:EDGE + (i + 1) * P, :], in_=rows_sb[:])
            else:
                nc.sync.dma_start(out=out[plane, n, CELLS - EDGE:CELLS, :], in_=rows_sb[0:EDGE, :])
                nc.sync.dma_start(out=out[plane, n, 0:EDGE, :], in_=rows_sb[EDGE:P, :])

        conf1_sb = {}
        home_banks = {}
        dots_again = {}
        kept_sb = {}
        best_sb = {}

        def home_turn(n, i):
            banks = []
            for lo, hi in HALVES:
                ps = bank()
                for j in range(lo // P, hi // P):
                    nc.tensor.transpose(
                        ps[:, j * P - lo:(j + 1) * P - lo], columns[n]["e"][j][:, i * P:(i + 1) * P], ident[:]
                    )
                banks.append(ps[:, 0:hi - lo])
            home_banks[n, i] = banks

        def home_copy(n, i, k):
            lo, hi = HALVES[k]
            if (n, i) not in conf1_sb:
                conf1_sb[n, i] = quot.tile([P, CELLS], F32, tag="conf1", name="conf1", bufs=4)
            nc.scalar.copy(out=conf1_sb[n, i][:, lo:hi], in_=home_banks[n, i][k])

        def match_dots(n, i):
            dots_again[n, i] = dot_banks(n, GRID0, GRID1, i, INNER_SPANS)

        def match_kept(n, i, k):
            if k == 0:
                kept_sb[n, i] = mask.tile([P, INNER_ROWS, INNER_COLS], F32, tag="kept", name="kept")
            lo, hi = INNER_SPANS[k]
            g = slice((lo - EDGE) // GRID_W, (hi - EDGE) // GRID_W)
            nc.vector.scalar_tensor_tensor(
                out=kept_sb[n, i][:, g, :], in0=inner_cells(bar1_all[n][:, lo:hi]),
                scalar=rows[n]["bar"][:, i:i + 1],
                in1=inner_cells(dots_again[n, i][k]), op0=ALU.min, op1=ALU.is_le,
            )

        def match_best(n, i, k):
            if k == 0:
                best_sb[n, i] = mask.tile([P, INNER_ROWS, INNER_COLS], F32, tag="best", name="best")
            lo, hi = HALVES[k]
            lo, hi = max(lo, EDGE), min(hi, CELLS - EDGE)
            g = slice((lo - EDGE) // GRID_W, (hi - EDGE) // GRID_W)
            nc.vector.scalar_tensor_tensor(
                out=best_sb[n, i][:, g, :], in0=inner_cells(rows[n]["e"][i][:, lo:hi]),
                scalar=rows[n]["inv"][:, i:i + 1],
                in1=inner_cells(home_banks[n, i][k][:, lo - HALVES[k][0]:hi - HALVES[k][0]]),
                op0=ALU.mult, op1=ALU.max,
            )

        def match_final(n, i, engine):
            mconf_sb = mconf_tiles[i % MCONF_TILES]
            eng = nc.gpsimd if engine == "G" else nc.vector
            eng.tensor_tensor(
                out=inner_cells(mconf_sb[:, EDGE:CELLS - EDGE]), in0=kept_sb[n, i][:], in1=best_sb[n, i][:],
                op=ALU.mult,
            )
            store(2, n, i, mconf_sb)

        columns = [open_softmax(n, GRID1, GRID0, "c%d" % n) for n in range(BATCH)]
        rows = [open_softmax(n, GRID0, GRID1, "r%d" % n) for n in range(BATCH)]
        bar1_all = [None, None]
        pending = []

        def large(step, *args):
            ready = list(pending)
            pending.clear()
            step(*args)
            for small, small_args in ready:
                small(*small_args)

        def later(step, *args):
            pending.append((step, args))

        warm_ps = bank()

        def warm_up(times):
            for repeat in range(times):
                nc.tensor.matmul(out=warm_ps[:], lhsT=idle[:, 0:P], rhs=idle[:], start=True, stop=True)

        warm_up(4)

        tiles = [(rows[0], j) for j in range(TILES)] + [(columns[0], j) for j in range(TILES)]
        tiles += [(columns[1], 0), (columns[1], 1), (columns[1], 2), (columns[1], 3), (columns[1], 4), (columns[1], 5), (rows[1], 0), (rows[1], 1), (rows[1], 2), (rows[1], 3), (rows[1], 4), (rows[1], 5)]
        plan = {}

        def emit_out(chunk, c, scalar):
            if scalar:
                emit_on_scalar(chunk, c)
            else:
                large(emit_on_vector, chunk, c)

        def emit(chunk, c, scalar):
            project(chunk, c)
            emit_out(chunk, c, scalar)

        def side(r, late, step, *args):
            plan.setdefault((r, late), []).append((step, args))

        def do_side(r, late):
            for step, args in plan.get((r, late), []):
                step(*args)

        for p in range(6):
            chunk = (0, 2 * p, 2)
            r = p - 7
            share = [0, 0, 1, 0, 0, 0][p]
            side(r, 1, turn, chunk, 0)
            side(r, 1, turn_copy, chunk, 0)
            if p < 2:
                side(r, 1, warm_up, 2)
            elif p < 5:
                side(r, 1, warm_up, 1)
            side(r + 1, 0, large, quantize_x, chunk)
            for c in range(2):
                side(r + 2, 1, project, chunk, c)
                side(r + 2 if r < -2 else r + 3, 2 if r < -2 else 0, emit_out, chunk, c, share and c == 1)
            side(r + (4 if share else 3), 7, large, quantize_f, chunk)
        for q in range(3):
            chunk = (1, 4 * q, 4)
            r = [-2,1,4][q]
            for pair in range(2):
                side(r + pair, 1, turn, chunk, pair)
                if r + pair + 1 >= 0:
                    side(r + pair + 1, 6, turn_copy, chunk, pair)
                else:
                    side(r + pair, 1, turn_copy, chunk, pair)
            side(r + 2, 3 if r + 2 >= 0 else 0, large, quantize_x, chunk)
            if q in [0]:
                for c in range(4):
                    side(r + 2 + c // 2, 1, project_plane, chunk, c)
                    side(r + 3 + c // 2, 6, plane_out, chunk, c)
                for c in range(2):
                    side(r + 4 + (c * 2) // 2, 5, group_planes, chunk, c)
                side(r + 6, 3, large, quantize_f, chunk)
                continue
            for c in range(4):
                side(r + 2 + c // 2, 1, project, chunk, c)
                if c == 1:
                    side(r + 3 + c // 2, 6 if r + 3 + c // 2 >= 0 else 0, emit_out, chunk, c, True)
                else:
                    side(r + 3 + c // 2, 0, emit_out, chunk, c, False)
            side(r + 6, 3, large, quantize_f, chunk)
        for r in range(-7, 0):
            do_side(r, 0)
            do_side(r, 7)
            do_side(r, 4)
            do_side(r, 5)
            do_side(r, 1)
            do_side(r, 2)
            if r == -7:
                bias_ps = psum.tile([P, P], BF16, tag="bank", name="bias_ps")
                nc.tensor.transpose(bias_ps[:], bias_rows[:], ident_bf[:])
                floor_ps = bank()
                nc.tensor.transpose(floor_ps[:, 0:P], floor_free[:], ident[:])
                bias4 = const.tile([P, PACK], F32)
                floor_row = const.tile([P, 1], F32)
                nc.vector.tensor_scalar(
                    out=bias4[:], in0=bias_ps[:, 0:PACK], scalar1=INV_SQRT_C, scalar2=None, op0=ALU.mult
                )
                nc.vector.tensor_copy(out=floor_row[:], in_=floor_ps[:, 0:1])
                for group in rows:
                    nc.vector.tensor_scalar(
                        out=group["tops"][:, :, 3], in0=floor_ps[:, 0:1].to_broadcast([P, TILES]),
                        scalar1=2.0, scalar2=-NEVER, op0=ALU.mult, op1=ALU.add,
                    )

            pass

        home = {}
        for i in range(TILES):
            home.setdefault([15,16,17,18,19,20][i], []).append((0, i))
            home.setdefault([21,22,23,24,25,26][i], []).append((1, i))
        last = max(home) + 1

        def divider(tile):
            group, j = tile
            return "S" if (group["own"] == GRID0 and group["n"] == 1 and j >= 4) or (group["own"] == GRID1 and j == TILES - 1) else "G"

        batches = {}
        for k, (group, j) in enumerate(tiles):
            ends = (1, 3, 5) if group["own"] == GRID1 else ((2, 5) if group["n"] == 0 else (1, 3, 5))
            if j in ends:
                place = ends.index(j)
                batches.setdefault(k + (1 if k >= 18 else 2), []).append((group, ends[place - 1] + 1 if place else 0, j + 1))
        division = {}
        for r, group, first, end in [(r,) + batch for r, some in batches.items() for batch in some]:
            for j in range(first, end):
                division.setdefault(r if first == 4 or group['own'] == GRID1 else r + j - first, []).append((group, j))
        divided = []

        def exponentials(k):
            shift_of(tiles[k])
            exp_of(tiles[k])

        def inner(tiles_home):
            return [s for s in tiles_home if s[1] < TILES - 1]

        dots_of(tiles[0])
        for k in range(last + 1):
            do_side(k, 6)
            coming = home.get(k, [])
            before = home.get(k - 1, [])
            if k + 1 < len(tiles):
                dots_of(tiles[k + 1])
            for group, first, end in batches.get(k - 2, []):
                if group["own"] == GRID1 and end == TILES:
                    spread_copy(group, 0)
                    spread_copy(group, 1)
            if k < len(tiles):
                large(top_of, tiles[k], 1)
                large(top_of, tiles[k], 0)
                later(exponentials, k)
            for batch in batches.get(k, []):
                total_of(*batch)
                pen_of(*batch)
            pass
            for s in inner(before):
                large(match_kept, *s, 0)
                large(match_kept, *s, 1)
                match_final(*s, "V" if k == last - 1 else "G")
            for s in inner(coming):
                large(match_best, *s, 0)
                large(match_best, *s, 1)
            for s in coming:
                home_copy(*s, 0)
                home_copy(*s, 1)
                store(1, *s, conf1_sb[s])
            do_side(k, 0)
            do_side(k, 7)
            do_side(k, 4)
            do_side(k, 5)
            do_side(k, 3)
            for batch in batches.get(k, []):
                inverse_of(*batch)
            for tile in division.get(k, []):
                divide(tile, divider(tile))
                divided.append(tile)
            for group, first, end in batches.get(k - 1, []):
                bar_of(group, first, end)
            spreading = [batch[0] for batch in batches.get(k - 1, []) if batch[0]["own"] == GRID1 and batch[2] == TILES]
            for group in spreading:
                spread(group, 0)
            for s in inner(coming):
                match_dots(*s)
            for group in spreading:
                spread(group, 1)
            for s in home.get(k + 1, []):
                assert all((columns[s[0]], j) in divided for j in range(TILES))
                home_turn(*s)
            do_side(k, 1)
            do_side(k, 2)
            if k == 1:
                for n in range(BATCH):
                    store(2, n, TILES - 1, zeros)
        while pending:
            large(lambda: None)
